import numpy as np
import ml_dtypes


def mxq(x, axis, fmt="e4m3"):
    dtype, down = {"e4m3": (ml_dtypes.float8_e4m3fn, 7), "e5m2": (ml_dtypes.float8_e5m2, 14)}[fmt]
    v = np.moveaxis(np.asarray(x, np.float32).astype(ml_dtypes.bfloat16).astype(np.float64), axis, -1)
    blocks = v.reshape(v.shape[:-1] + (-1, 32))
    amax = np.abs(blocks).max(-1, keepdims=True)
    byte = np.maximum(np.where(amax > 0, np.frexp(amax)[1] - 1 + 127, 0) - down, 1)
    scale = np.exp2(byte - 127.0)
    codes = (blocks / scale).astype(np.float32).astype(dtype).astype(np.float64)
    return np.moveaxis((codes * scale).reshape(v.shape), -1, axis)


WIDE = False


def mx_kscale(k):
    if not WIDE:
        return np.ones(k)
    levels = np.array([10, -10, 5, -5, 0])
    if k % 512:
        return np.exp2(np.random.permutation(np.resize(levels, k // 32))).repeat(32)
    a = np.empty((k // 512, 16))
    for p in range(k // 512):
        a[p, :8] = np.random.permutation(np.resize(levels, 8))
        for g in range(8):
            far = levels[np.abs(levels - a[p, g]) >= 10]
            a[p, g + 8] = far[np.random.randint(len(far))]
    return np.exp2(a.ravel()).repeat(32)


BF16 = ml_dtypes.bfloat16


def bf(x):
    return np.asarray(x, np.float32).astype(BF16)


def f64(x):
    return np.asarray(x).astype(np.float64)


E2M1 = np.array([0.0, 0.5, 1.0, 1.5, 2.0, 3.0, 4.0, 6.0, -0.0, -0.5, -1.0, -1.5, -2.0, -3.0, -4.0, -6.0])


def pack_weight(w, fmt):
    k, n = w.shape
    w = f64(bf(w)).reshape(k // 32, 32, n)
    amax = np.abs(w).max(1)
    if fmt == "e4m3":
        byte = np.frexp(amax)[1] - 1 + 127 - 7
    else:
        mant, ex = np.frexp(amax / 6.0)
        byte = np.where(mant > 0.5, ex, ex - 1) + 127
    byte = np.clip(np.where(amax > 0, byte, 1), 1, 254)
    scaled = (w * np.exp2(127.0 - byte)[:, None, :]).reshape(k, n).astype(np.float32)
    by_word = np.ascontiguousarray(scaled.reshape(k // 512, 128, 4, n).transpose(0, 1, 3, 2))
    if fmt == "e4m3":
        words = by_word.astype(ml_dtypes.float8_e4m3fn).view(np.uint8)
    else:
        c = by_word.astype(ml_dtypes.float4_e2m1fn).view(np.uint8) & 0xF
        words = c[..., 0::2] | (c[..., 1::2] << 4)
    return np.ascontiguousarray(words), np.ascontiguousarray(byte.astype(np.uint8).reshape(k // 512, 16, n))


def unpack_weight(words, scales, fmt):
    g, p, n, _ = words.shape
    if fmt == "e4m3":
        vals = np.ascontiguousarray(words).view(ml_dtypes.float8_e4m3fn).astype(np.float64)
    else:
        nib = np.empty((g, p, n, 4), np.uint8)
        nib[..., 0::2] = words & 0xF
        nib[..., 1::2] = words >> 4
        vals = E2M1[nib]
    vals = vals * np.repeat(np.exp2(scales.astype(np.float64) - 127.0), 8, axis=1)[..., None]
    return vals.transpose(0, 1, 3, 2).reshape(g * 512, n)
def pack4(w):
    words, scales = pack_weight(w, "e2m1")
    return words.reshape(words.shape[0], 128, -1), scales


def unpack4(words, scales):
    return unpack_weight(words.reshape(words.shape[0], 128, -1, 2), scales, "e2m1")


B, S, D, NH = 2, 512, 1024, 8
SCALE = np.sqrt(D // NH)


def draw0():
    s, t = mx_kscale(D), mx_kscale(D)
    x = bf(np.random.standard_normal((B, S, D)) * s)
    wq = np.random.standard_normal((D, D)) * 0.84 / np.sqrt(D) / s[None, :] * t[:, None]
    wk = np.random.standard_normal((D, D)) * 0.84 / np.sqrt(D) / s[None, :] / t[:, None]
    wq_words, wq_scales = pack4(wq.T)
    wk_words, wk_scales = pack4(wk.T)
    return {"x": x,
            "wq_words": wq_words, "wq_scales": wq_scales,
            "wk_words": wk_words, "wk_scales": wk_scales}


def core(x, wq_words, wq_scales, wk_words, wk_scales):
    xq = mxq(f64(x), 2, "e4m3")
    q = xq @ unpack4(wq_words, wq_scales)
    k = xq @ unpack4(wk_words, wk_scales)
    sc = (mxq(q, 2, "e4m3") @ mxq(k, 2, "e4m3").transpose(0, 2, 1)) / SCALE
    e = np.exp(sc - sc.max(-1, keepdims=True))
    return e / e.sum(-1, keepdims=True)


def e4m3fn_bytes(y):
    return np.clip(np.asarray(y, np.float64), -448.0, 448.0).astype(np.float32).astype(ml_dtypes.float8_e4m3fn).view(np.uint8)


def e4m3fn_values(b):
    return np.asarray(b, np.uint8).view(ml_dtypes.float8_e4m3fn).astype(np.float64)


def setup_inputs():
    d = draw0()
    x0 = np.asarray(d['x']).astype(np.float64)
    s = (np.max(np.abs(x0), axis=(0, 1), keepdims=True) / 448.0).astype(np.float32)
    out = {}
    for k, v in d.items():
        if k == 'x':
            out['x_bytes'] = e4m3fn_bytes(x0 / s.astype(np.float64))
            out['x_scale'] = s
        else:
            out[k] = v
    return out


def reference(x_bytes, x_scale, wq_words, wq_scales, wk_words, wk_scales):
    return core(e4m3fn_values(x_bytes) * x_scale.astype(np.float64), wq_words, wq_scales, wk_words, wk_scales)

@@ -1,0 +1,308 @@
+import math
+from contextlib import ExitStack
+
+import concourse.mybir as mybir
+from concourse.masks import make_identity
+
+F32 = mybir.dt.float32
+BF16 = mybir.dt.bfloat16
+I32 = mybir.dt.int32
+U32 = mybir.dt.uint32
+U8 = mybir.dt.uint8
+FP8 = mybir.dt.float8_e4m3fn
+FP8X4 = mybir.dt.float8_e4m3fn_x4
+FP4X4 = mybir.dt.float4_e2m1fn_x4
+ACT = mybir.ActivationFunctionType
+ALU = mybir.AluOpType
+AX = mybir.AxisListType
+
+B, S, D = 2, 512, 1024
+P = 128
+TILES = B * S // P
+PER_BATCH = S // P
+PASSES = D // 512
+INV = 1.0 / math.sqrt(128.0)
+FLOPS = 2 * 2 * B * S * D * D + 2 * B * S * S * D
+
+SEQ = ["D","D","D","T0","T1","D","D","T2","K0","T3","K1","K2","Q1","T4","T5","Q0","T6","T7","K3","Q2","Q4","Q3","S0","K4","K6","S1","K5","S3","K7","S2","Q5","S4","Q6","S5","Q7","S6","S7"]
+CAST_V = (0,1,4,6,)
+EXIT_V = ()
+NORM_G = ()
+LAG_CAST = 4
+LAG_SCALE = 1
+LAG_QUANT = 0
+LAG_MAX = 0
+LAG_EXP = 2
+LAG_INV = 1
+LAG_NORM = 1
+XFIRST = 3
+PERM_Q = 8
+CAST_SPLIT = (0,)
+NORM_SPLIT = (7,)
+NORM_COLS = 320
+
+
+def tile_attentionnet_pa_w4_kernel(tc, x_bytes, x_scale, wq_words, wq_scales, wk_words, wk_scales, out):
+    nc = tc.nc
+    x_rows = x_bytes.rearrange("b s d -> (b s) d")
+    out_rows = out.rearrange("b s t -> (b s) t")
+
+    with ExitStack() as ctx:
+        keep = ctx.enter_context(tc.tile_pool(name="keep", bufs=1))
+        work = ctx.enter_context(tc.tile_pool(name="work", bufs=5))
+        soft = ctx.enter_context(tc.tile_pool(name="soft", bufs=4))
+        banks = ctx.enter_context(tc.psum_pool(name="banks", bufs=8))
+
+        warm = keep.tile([P, 1], F32, name="warm")
+        warm_out = keep.tile([P, 1], F32, name="warm_out")
+        zeros = keep.tile([P, 512], BF16, name="zeros")
+        dummy = banks.tile([P, 512], F32, name="bank")
+        ident = keep.tile([P, P], F32, name="ident")
+        scale_t = keep.tile([P, PASSES * 4], F32, name="scale_t")
+        xb = [keep.tile([P, D], U8, name="xb%d" % i) for i in range(TILES)]
+        raw = {m: keep.tile([P, 4096], U8, name="raw_" + m, align_bytes=64) for m in "KQ"}
+        raw_s = {m: keep.tile([P, 2048], U8, name="raws_" + m, align_bytes=64) for m in "KQ"}
+        wts = {m: keep.tile([P, 4096], U8, name="wts_" + m, align_bytes=64) for m in "KQ"}
+        wts_s = {m: keep.tile([P, 2048], U8, name="wtss_" + m, align_bytes=64) for m in "KQ"}
+        xc = [keep.tile([P, 256], U32, name="xc%d" % i, align_bytes=64) for i in range(TILES)]
+        xs = [keep.tile([P, 256], U8, name="xs%d" % i, align_bytes=64) for i in range(TILES)]
+        kc = [keep.tile([P, 1024], U32, name="kc%d" % i, align_bytes=64) for i in range(B)]
+        ks = [keep.tile([P, 1024], U8, name="ks%d" % i, align_bytes=64) for i in range(B)]
+        qc = [keep.tile([P, 256], U32, name="qc%d" % i, align_bytes=64) for i in range(TILES)]
+        qs = [keep.tile([P, 256], U8, name="qs%d" % i, align_bytes=64) for i in range(TILES)]
+
+        hbm_w = {"K": wk_words, "Q": wq_words}
+        hbm_s = {"K": wk_scales, "Q": wq_scales}
+
+        def load_x(i):
+            nc.sync.dma_start(out=xb[i][:], in_=x_rows[i * P : (i + 1) * P, :])
+
+        def load_w(m, h):
+            nc.sync.dma_start(
+                out=raw[m][:].bitcast(I32)[:, h * 512 : (h + 1) * 512].rearrange("p (g n) -> p g n", g=PASSES),
+                in_=hbm_w[m].bitcast(I32)[:, :, h * 256 : (h + 1) * 256].rearrange("g p n -> p g n"),
+            )
+
+        def load_s(m):
+            dst = raw_s[m][:].bitcast(I32).rearrange("p (g n) -> p g n", g=PASSES)
+            src = hbm_s[m].bitcast(I32)
+            for q in range(4):
+                nc.sync.dma_start(out=dst[32 * q : 32 * q + 4], in_=src[:, 4 * q : 4 * q + 4, :].rearrange("g r n -> r g n"))
+
+        def permute(m, h):
+            half = slice(h * 512, (h + 1) * 512)
+            nc.vector.tensor_copy(
+                out=wts[m][:].bitcast(I32)[:, half].rearrange("p (t c w) -> p t c w", t=4, w=4),
+                in_=raw[m][:].bitcast(I32)[:, half].rearrange("p (c t w) -> p t c w", t=4, w=4),
+            )
+
+        def permute_s(m, h):
+            src = raw_s[m][:].bitcast(I32)
+            dst = wts_s[m][:].bitcast(I32)
+            for g in range(PASSES):
+                nc.gpsimd.tensor_copy(
+                    out=dst[:, h * 256 + g * 128 : h * 256 + (g + 1) * 128].rearrange("p (t c w) -> p t c w", t=4, w=2),
+                    in_=src[:, g * 256 + h * 128 : g * 256 + (h + 1) * 128].rearrange("p (c t w) -> p t c w", t=4, w=2),
+                )
+
+        xbf = {}
+        xt = {}
+        xg = {}
+        yp = {}
+        yg = {}
+        sp = {}
+        ex = {}
+
+        def cast(i):
+            xbf[i] = work.tile([P, D], BF16, name="xbf", align_bytes=64)
+            src = xb[i][:].bitcast(FP8)
+            if i in CAST_SPLIT:
+                nc.vector.tensor_copy(out=xbf[i][:, 0:512], in_=xb[i][:, 0:512].bitcast(FP8))
+                nc.scalar.copy(xbf[i][:, 512:1024], xb[i][:, 512:1024].bitcast(FP8))
+            elif i in CAST_V:
+                nc.vector.tensor_copy(out=xbf[i][:], in_=src)
+            else:
+                nc.scalar.copy(xbf[i][:], src)
+
+        def turn(i):
+            xt[i] = banks.tile([P, 512], F32, name="bank")
+            words = xbf[i][:].bitcast(F32)
+            for g in range(PASSES):
+                for u in range(2):
+                    nc.tensor.transpose(
+                        xt[i][:, g * 256 + u * 128 : g * 256 + u * 128 + 128],
+                        words[:, 256 * g + u : 256 * (g + 1) : 2],
+                        ident[:],
+                    )
+
+        def scale(i, g):
+            if g == 0:
+                xg[i] = work.tile([P, 1024], BF16, name="xg", align_bytes=64)
+            nc.vector.tensor_tensor(
+                out=xg[i][:, g * 512 : (g + 1) * 512].rearrange("p (r u e) -> p r u e", u=2, e=2),
+                in0=xt[i][:, g * 256 : (g + 1) * 256].bitcast(BF16).rearrange("p (u r e) -> p r u e", u=2, e=2),
+                in1=scale_t[:, g * 4 : (g + 1) * 4].rearrange("p (u e) -> p u e", e=2).unsqueeze(1).to_broadcast([P, P, 2, 2]),
+                op=ALU.mult,
+            )
+
+        def quant_x(i):
+            for g in range(PASSES):
+                cols = slice(g * P, (g + 1) * P)
+                nc.vector.quantize_mx(out=xc[i][:, cols].bitcast(FP8X4), scales=xs[i][:, cols], in_=xg[i][:, g * 512 : (g + 1) * 512])
+
+        def project(m, i, h):
+            yp[m, i, h] = banks.tile([P, 512], F32, name="bank")
+            for t in range(4):
+                for g in range(PASSES):
+                    plane = h * 1024 + g * 512
+                    nc.tensor.matmul_mx(
+                        out=yp[m, i, h][:, t * P : (t + 1) * P],
+                        lhsT=wts[m][:, h * 2048 + t * 512 + g * 256 : h * 2048 + t * 512 + (g + 1) * 256].bitcast(FP4X4),
+                        lhsT_scale=wts_s[m][:, plane + t * 128 : plane + (t + 1) * 128],
+                        rhs=xc[i][:, g * P : (g + 1) * P].bitcast(FP8X4),
+                        rhs_scale=xs[i][:, g * P : (g + 1) * P],
+                        start=(g == 0),
+                        stop=(g == PASSES - 1),
+                    )
+
+        def leave(m, i, h):
+            if h == 0:
+                yg[m, i] = work.tile([P, 1024], BF16, name="yg", align_bytes=64)
+            dst = yg[m, i][:, h * 512 : (h + 1) * 512].rearrange("p (n t) -> p n t", t=4)
+            bank = yp[m, i, h][:].rearrange("p (t n) -> p n t", t=4)
+            if (m + str(i), h) in EXIT_V:
+                nc.vector.tensor_copy(out=dst, in_=bank)
+            else:
+                nc.scalar.copy(dst, bank)
+
+        def quant_y(m, i):
+            b, j = divmod(i, PER_BATCH)
+            if m == "Q":
+                nc.vector.quantize_mx(out=qc[i][:].bitcast(FP8X4), scales=qs[i][:], in_=yg[m, i][:])
+            else:
+                for h in range(2):
+                    cols = slice(h * S + j * P, h * S + (j + 1) * P)
+                    nc.vector.quantize_mx(out=kc[b][:, cols].bitcast(FP8X4), scales=ks[b][:, cols], in_=yg[m, i][:, h * 512 : (h + 1) * 512])
+
+        def score(i):
+            b = i // PER_BATCH
+            sp[i] = banks.tile([P, S], F32, name="bank")
+            for h in range(2):
+                nc.tensor.matmul_mx(
+                    out=sp[i][:],
+                    lhsT=qc[i][:, h * P : (h + 1) * P].bitcast(FP8X4),
+                    lhsT_scale=qs[i][:, h * P : (h + 1) * P],
+                    rhs=kc[b][:, h * S : (h + 1) * S].bitcast(FP8X4),
+                    rhs_scale=ks[b][:, h * S : (h + 1) * S],
+                    start=(h == 0),
+                    stop=(h == 1),
+                )
+
+        def row_max(i):
+            mx = soft.tile([P, 1], F32, name="mx")
+            nb = soft.tile([P, 1], F32, name="nb")
+            nc.vector.tensor_reduce(out=mx[:], in_=sp[i][:], axis=AX.X, op=ALU.max)
+            ex[i] = [mx, nb]
+
+        def exps(i):
+            mx, nb = ex[i]
+            nc.scalar.mul(nb[:], mx[:], -INV)
+            e = soft.tile([P, S], F32, name="e")
+            sm = soft.tile([P, 1], F32, name="sm")
+            nc.scalar.activation(out=e[:], in_=sp[i][:], func=ACT.Exp, bias=nb[:], scale=INV, accum_out=sm[:])
+            ex[i] = [e, sm]
+
+        def invert(i):
+            e, sm = ex[i]
+            rc = soft.tile([P, 1], F32, name="rc")
+            nc.vector.reciprocal(rc[:], sm[:])
+            ex[i] = (e, rc)
+
+        def finish(i):
+            e, rc = ex[i]
+            o = soft.tile([P, S], F32, name="o")
+            if i in NORM_SPLIT:
+                lo, hi = slice(0, NORM_COLS), slice(NORM_COLS, S)
+                nc.scalar.activation(out=o[:, hi], in_=e[:, hi], func=ACT.Copy, scale=rc[:])
+                nc.vector.tensor_scalar(out=o[:, lo], in0=e[:, lo], scalar1=rc[:], scalar2=None, op0=ALU.mult)
+                nc.scalar.dma_start(out=out_rows[i * P : (i + 1) * P, hi], in_=o[:, hi])
+                nc.sync.dma_start(out=out_rows[i * P : (i + 1) * P, lo], in_=o[:, lo])
+                return
+            if i in NORM_G:
+                nc.gpsimd.tensor_scalar(out=o[:], in0=e[:], scalar1=rc[:], scalar2=0.0, op0=ALU.mult, op1=ALU.add)
+            else:
+                nc.vector.tensor_scalar(out=o[:], in0=e[:], scalar1=rc[:], scalar2=None, op0=ALU.mult)
+            nc.sync.dma_start(out=out_rows[i * P : (i + 1) * P, :], in_=o[:])
+
+        ctx.enter_context(tc.manual_schedule())
+        make_identity(nc, ident[:])
+        nc.vector.memset(warm[:], 0.0)
+        nc.scalar.activation(out=warm_out[:], in_=warm[:], func=ACT.Exp)
+        nc.vector.memset(raw_s["K"][:].bitcast(I32), 0)
+        nc.vector.memset(zeros[:], 0.0)
+        nc.vector.memset(raw_s["Q"][:].bitcast(I32), 0)
+        load_x(0)
+        nc.scalar.dma_start(out=scale_t[:].rearrange("p (g t) -> p g t", t=4), in_=x_scale.rearrange("a b (g p t) -> p (a b g) t", p=P, t=4))
+        for i in range(1, XFIRST):
+            load_x(i)
+        load_s("K")
+        load_w("K", 0)
+        load_w("K", 1)
+        load_x(XFIRST)
+        load_w("Q", 0)
+        load_w("Q", 1)
+        load_s("Q")
+        for i in range(XFIRST + 1, TILES):
+            load_x(i)
+        for m in "KQ":
+            for h in range(2):
+                permute_s(m, h)
+
+        pending = {}
+
+        def later(n, fn, *args):
+            pending.setdefault(n, []).append((fn, args))
+
+        for n, op in enumerate(SEQ):
+            kind, i = op[0], int(op[1:] or 0)
+            if kind == "D":
+                continue
+            if kind == "T":
+                later(max(n - LAG_CAST, -1), cast, i)
+                later(n + LAG_SCALE, scale, i, 0)
+                later(n + LAG_SCALE, scale, i, 1)
+                if i == 0:
+                    later(n + LAG_SCALE, permute, "K", 0)
+                later(n + LAG_SCALE, quant_x, i)
+                if i == 0:
+                    later(n + LAG_SCALE, permute, "K", 1)
+            elif kind == "S":
+                later(n + LAG_MAX, row_max, i)
+                later(n + LAG_MAX + LAG_EXP, exps, i)
+                later(n + LAG_MAX + LAG_EXP + LAG_INV, invert, i)
+                later(n + LAG_MAX + LAG_EXP + LAG_INV + LAG_NORM, finish, i)
+            else:
+                later(n + LAG_QUANT, quant_y, kind, i)
+
+        def run_pending(n):
+            for fn, args in pending.get(n, []):
+                fn(*args)
+
+        later(PERM_Q, permute, "Q", 0)
+        later(PERM_Q, permute, "Q", 1)
+        run_pending(-1)
+        for n, op in enumerate(SEQ):
+            kind, i = op[0], int(op[1:] or 0)
+            if kind == "D":
+                nc.tensor.matmul(dummy[:], zeros[:, 0:P], zeros[:], start=True, stop=True)
+            elif kind == "T":
+                turn(i)
+            elif kind == "S":
+                score(i)
+            else:
+                for h in range(2):
+                    project(kind, i, h)
+                    leave(kind, i, h)
+            run_pending(n)
+        for n in range(len(SEQ), len(SEQ) + 9):
+            run_pending(n)

@@ -14,7 +14,6 @@ FP8X4 = mybir.dt.float8_e4m3fn_x4
 FP4X4 = mybir.dt.float4_e2m1fn_x4
 ACT = mybir.ActivationFunctionType
 ALU = mybir.AluOpType
-AX = mybir.AxisListType
 
 B, S, D = 2, 512, 1024
 P = 128
@@ -23,23 +22,8 @@ PER_BATCH = S // P
 PASSES = D // 512
 INV = 1.0 / math.sqrt(128.0)
 FLOPS = 2 * 2 * B * S * D * D + 2 * B * S * S * D
-
-SEQ = ["D","D","D","T0","T1","D","D","T2","K0","T3","K1","K2","Q1","T4","T5","Q0","T6","T7","K3","Q2","Q4","Q3","S0","K4","K6","S1","K5","S3","K7","S2","Q5","S4","Q6","S5","Q7","S6","S7"]
-CAST_V = (0,1,4,6,)
-EXIT_V = ()
-NORM_G = ()
-LAG_CAST = 4
-LAG_SCALE = 1
-LAG_QUANT = 0
-LAG_MAX = 0
-LAG_EXP = 2
-LAG_INV = 1
-LAG_NORM = 1
-XFIRST = 3
-PERM_Q = 8
-CAST_SPLIT = (0,)
-NORM_SPLIT = (7,)
-NORM_COLS = 320
+LEAD_WIDEN = 6
+ON_VECTOR = [("Q", 4, 0), ("Q", 6, 1)]
 
 
 def tile_attentionnet_pa_w4_kernel(tc, x_bytes, x_scale, wq_words, wq_scales, wk_words, wk_scales, out):
@@ -49,37 +33,49 @@ def tile_attentionnet_pa_w4_kernel(tc, x_bytes, x_scale, wq_words, wq_scales, wk
 
     with ExitStack() as ctx:
         keep = ctx.enter_context(tc.tile_pool(name="keep", bufs=1))
-        work = ctx.enter_context(tc.tile_pool(name="work", bufs=5))
-        soft = ctx.enter_context(tc.tile_pool(name="soft", bufs=4))
         banks = ctx.enter_context(tc.psum_pool(name="banks", bufs=8))
 
-        warm = keep.tile([P, 1], F32, name="warm")
-        warm_out = keep.tile([P, 1], F32, name="warm_out")
-        zeros = keep.tile([P, 512], BF16, name="zeros")
-        dummy = banks.tile([P, 512], F32, name="bank")
+        def tiles(name, keys, shape, dtype):
+            return {k: keep.tile(shape, dtype, name="%s_%s" % (name, k), align_bytes=64) for k in keys}
+
+        every = range(TILES)
+        both = ["K%d" % i for i in every] + ["Q%d" % i for i in every]
         ident = keep.tile([P, P], F32, name="ident")
-        scale_t = keep.tile([P, PASSES * 4], F32, name="scale_t")
-        xb = [keep.tile([P, D], U8, name="xb%d" % i) for i in range(TILES)]
-        raw = {m: keep.tile([P, 4096], U8, name="raw_" + m, align_bytes=64) for m in "KQ"}
-        raw_s = {m: keep.tile([P, 2048], U8, name="raws_" + m, align_bytes=64) for m in "KQ"}
-        wts = {m: keep.tile([P, 4096], U8, name="wts_" + m, align_bytes=64) for m in "KQ"}
-        wts_s = {m: keep.tile([P, 2048], U8, name="wtss_" + m, align_bytes=64) for m in "KQ"}
-        xc = [keep.tile([P, 256], U32, name="xc%d" % i, align_bytes=64) for i in range(TILES)]
-        xs = [keep.tile([P, 256], U8, name="xs%d" % i, align_bytes=64) for i in range(TILES)]
-        kc = [keep.tile([P, 1024], U32, name="kc%d" % i, align_bytes=64) for i in range(B)]
-        ks = [keep.tile([P, 1024], U8, name="ks%d" % i, align_bytes=64) for i in range(B)]
-        qc = [keep.tile([P, 256], U32, name="qc%d" % i, align_bytes=64) for i in range(TILES)]
-        qs = [keep.tile([P, 256], U8, name="qs%d" % i, align_bytes=64) for i in range(TILES)]
+        scale_k = keep.tile([P, PASSES * 4], F32, name="scale_k")
+        scale_row = tiles("scale_row", range(PASSES), [P, 512], F32)
+        xb = tiles("xb", every, [P, D], U8)
+        raw = tiles("raw", ["K0", "K1", "Q0", "Q1"], [P, 2048], U8)
+        raw_s = tiles("raw_s", "KQ", [P, 2048], U8)
+        wts = tiles("wts", ["K0", "K1", "Q0", "Q1"], [P, 2048], U8)
+        wts_s = tiles("wts_s", ["K0", "K1", "Q0", "Q1"], [P, 1024], U8)
+        xw = tiles("xw", every, [P, D], BF16)
+        xg = tiles("xg", every, [P, D], BF16)
+        xc = tiles("xc", every, [P, 256], U32)
+        xs = tiles("xs", every, [P, 256], U8)
+        yg = tiles("yg", both, [P, D], BF16)
+        kc = tiles("kc", range(B), [P, 1024], U32)
+        ks = tiles("ks", range(B), [P, 1024], U8)
+        qc = tiles("qc", every, [P, 256], U32)
+        qs = tiles("qs", every, [P, 256], U8)
+        neg = tiles("neg", every, [P, S], F32)
+        low = tiles("low", every, [P, 1], F32)
+        ex = tiles("ex", every, [P, S], F32)
+        total = tiles("total", every, [P, 1], F32)
+        inv = tiles("inv", every, [P, 1], F32)
+        res = tiles("res", every, [P, S], F32)
 
         hbm_w = {"K": wk_words, "Q": wq_words}
         hbm_s = {"K": wk_scales, "Q": wq_scales}
+        turned = {}
+        scores = {}
+        projected = {}
 
         def load_x(i):
             nc.sync.dma_start(out=xb[i][:], in_=x_rows[i * P : (i + 1) * P, :])
 
         def load_w(m, h):
             nc.sync.dma_start(
-                out=raw[m][:].bitcast(I32)[:, h * 512 : (h + 1) * 512].rearrange("p (g n) -> p g n", g=PASSES),
+                out=raw[m + str(h)][:].bitcast(I32).rearrange("p (g n) -> p g n", g=PASSES),
                 in_=hbm_w[m].bitcast(I32)[:, :, h * 256 : (h + 1) * 256].rearrange("g p n -> p g n"),
             )
 
@@ -89,107 +85,96 @@ def tile_attentionnet_pa_w4_kernel(tc, x_bytes, x_scale, wq_words, wq_scales, wk
             for q in range(4):
                 nc.sync.dma_start(out=dst[32 * q : 32 * q + 4], in_=src[:, 4 * q : 4 * q + 4, :].rearrange("g r n -> r g n"))
 
-        def permute(m, h):
-            half = slice(h * 512, (h + 1) * 512)
+        def permute_w(m, h):
             nc.vector.tensor_copy(
-                out=wts[m][:].bitcast(I32)[:, half].rearrange("p (t c w) -> p t c w", t=4, w=4),
-                in_=raw[m][:].bitcast(I32)[:, half].rearrange("p (c t w) -> p t c w", t=4, w=4),
+                out=wts[m + str(h)][:].bitcast(I32).rearrange("p (t c w) -> p t c w", t=4, w=4),
+                in_=raw[m + str(h)][:].bitcast(I32).rearrange("p (c t w) -> p t c w", t=4, w=4),
             )
 
         def permute_s(m, h):
-            src = raw_s[m][:].bitcast(I32)
-            dst = wts_s[m][:].bitcast(I32)
-            for g in range(PASSES):
-                nc.gpsimd.tensor_copy(
-                    out=dst[:, h * 256 + g * 128 : h * 256 + (g + 1) * 128].rearrange("p (t c w) -> p t c w", t=4, w=2),
-                    in_=src[:, g * 256 + h * 128 : g * 256 + (h + 1) * 128].rearrange("p (c t w) -> p t c w", t=4, w=2),
+            src = raw_s[m][:].bitcast(I32).rearrange("p (g h c t w) -> p h g t c w", g=PASSES, h=2, t=4, w=2)
+            nc.vector.tensor_copy(
+                out=wts_s[m + str(h)][:].bitcast(I32).rearrange("p (g t c w) -> p g t c w", g=PASSES, t=4, w=2),
+                in_=src[:, h],
+            )
+
+        def turn(i, g):
+            if g == 0:
+                turned[i] = banks.tile([P, 512], F32, name="bank")
+            words = xw[i][:].bitcast(F32)
+            for u in range(2):
+                nc.tensor.transpose(
+                    turned[i][:, g * 256 + u * P : g * 256 + (u + 1) * P],
+                    words[:, 256 * g + u : 256 * (g + 1) : 2],
+                    ident[:],
                 )
 
-        xbf = {}
-        xt = {}
-        xg = {}
-        yp = {}
-        yg = {}
-        sp = {}
-        ex = {}
-
-        def cast(i):
-            xbf[i] = work.tile([P, D], BF16, name="xbf", align_bytes=64)
-            src = xb[i][:].bitcast(FP8)
-            if i in CAST_SPLIT:
-                nc.vector.tensor_copy(out=xbf[i][:, 0:512], in_=xb[i][:, 0:512].bitcast(FP8))
-                nc.scalar.copy(xbf[i][:, 512:1024], xb[i][:, 512:1024].bitcast(FP8))
-            elif i in CAST_V:
-                nc.vector.tensor_copy(out=xbf[i][:], in_=src)
-            else:
-                nc.scalar.copy(xbf[i][:], src)
-
-        def turn(i):
-            xt[i] = banks.tile([P, 512], F32, name="bank")
-            words = xbf[i][:].bitcast(F32)
-            for g in range(PASSES):
-                for u in range(2):
-                    nc.tensor.transpose(
-                        xt[i][:, g * 256 + u * 128 : g * 256 + u * 128 + 128],
-                        words[:, 256 * g + u : 256 * (g + 1) : 2],
-                        ident[:],
-                    )
-
-        def scale(i, g):
-            if g == 0:
-                xg[i] = work.tile([P, 1024], BF16, name="xg", align_bytes=64)
+        def scale_turned(i, g, bank):
             nc.vector.tensor_tensor(
                 out=xg[i][:, g * 512 : (g + 1) * 512].rearrange("p (r u e) -> p r u e", u=2, e=2),
-                in0=xt[i][:, g * 256 : (g + 1) * 256].bitcast(BF16).rearrange("p (u r e) -> p r u e", u=2, e=2),
-                in1=scale_t[:, g * 4 : (g + 1) * 4].rearrange("p (u e) -> p u e", e=2).unsqueeze(1).to_broadcast([P, P, 2, 2]),
+                in0=bank.bitcast(BF16).rearrange("p (u r e) -> p r u e", u=2, e=2),
+                in1=scale_k[:, g * 4 : (g + 1) * 4].rearrange("p (u e) -> p u e", e=2).unsqueeze(1).to_broadcast([P, P, 2, 2]),
                 op=ALU.mult,
             )
 
+        def spread_scales(g):
+            bank = banks.tile([P, 512], F32, name="bank")
+            for t in range(4):
+                col = scale_k[:, g * 4 + t : g * 4 + t + 1].to_broadcast([P, P])
+                nc.tensor.transpose(bank[:, t * P : (t + 1) * P], col, ident[:])
+            nc.scalar.copy(scale_row[g][:].rearrange("p (n t) -> p n t", t=4), bank[:].rearrange("p (t n) -> p n t", t=4))
+
+        def widen(i, g):
+            cols = slice(g * 512, (g + 1) * 512)
+            nc.vector.tensor_tensor(out=xw[i][:, cols], in0=xb[i][:, cols].bitcast(FP8), in1=scale_row[g][:], op=ALU.mult)
+
+        def leave_turned(i):
+            nc.scalar.copy(
+                xg[i][:].bitcast(F32).rearrange("p (g r u) -> p g r u", g=PASSES, u=2),
+                turned[i][:].rearrange("p (g u r) -> p g r u", g=PASSES, u=2),
+            )
+
         def quant_x(i):
-            for g in range(PASSES):
-                cols = slice(g * P, (g + 1) * P)
-                nc.vector.quantize_mx(out=xc[i][:, cols].bitcast(FP8X4), scales=xs[i][:, cols], in_=xg[i][:, g * 512 : (g + 1) * 512])
+            nc.vector.quantize_mx(out=xc[i][:].bitcast(FP8X4), scales=xs[i][:], in_=xg[i][:])
 
         def project(m, i, h):
-            yp[m, i, h] = banks.tile([P, 512], F32, name="bank")
+            bank = banks.tile([P, 512], F32, name="bank")
             for t in range(4):
                 for g in range(PASSES):
-                    plane = h * 1024 + g * 512
                     nc.tensor.matmul_mx(
-                        out=yp[m, i, h][:, t * P : (t + 1) * P],
-                        lhsT=wts[m][:, h * 2048 + t * 512 + g * 256 : h * 2048 + t * 512 + (g + 1) * 256].bitcast(FP4X4),
-                        lhsT_scale=wts_s[m][:, plane + t * 128 : plane + (t + 1) * 128],
+                        out=bank[:, t * P : (t + 1) * P],
+                        lhsT=wts[m + str(h)][:, t * 512 + g * 256 : t * 512 + (g + 1) * 256].bitcast(FP4X4),
+                        lhsT_scale=wts_s[m + str(h)][:, g * 512 + t * P : g * 512 + (t + 1) * P],
                         rhs=xc[i][:, g * P : (g + 1) * P].bitcast(FP8X4),
                         rhs_scale=xs[i][:, g * P : (g + 1) * P],
                         start=(g == 0),
                         stop=(g == PASSES - 1),
                     )
+            projected[m, i, h] = bank
 
         def leave(m, i, h):
-            if h == 0:
-                yg[m, i] = work.tile([P, 1024], BF16, name="yg", align_bytes=64)
-            dst = yg[m, i][:, h * 512 : (h + 1) * 512].rearrange("p (n t) -> p n t", t=4)
-            bank = yp[m, i, h][:].rearrange("p (t n) -> p n t", t=4)
-            if (m + str(i), h) in EXIT_V:
-                nc.vector.tensor_copy(out=dst, in_=bank)
+            dst = yg[m + str(i)][:, h * 512 : (h + 1) * 512].rearrange("p (n t) -> p n t", t=4)
+            src = projected[m, i, h][:].rearrange("p (t n) -> p n t", t=4)
+            if (m, i, h) in ON_VECTOR:
+                nc.vector.tensor_copy(out=dst, in_=src)
             else:
-                nc.scalar.copy(dst, bank)
+                nc.scalar.copy(dst, src)
 
-        def quant_y(m, i):
+        def quant_k(i, h):
             b, j = divmod(i, PER_BATCH)
-            if m == "Q":
-                nc.vector.quantize_mx(out=qc[i][:].bitcast(FP8X4), scales=qs[i][:], in_=yg[m, i][:])
-            else:
-                for h in range(2):
-                    cols = slice(h * S + j * P, h * S + (j + 1) * P)
-                    nc.vector.quantize_mx(out=kc[b][:, cols].bitcast(FP8X4), scales=ks[b][:, cols], in_=yg[m, i][:, h * 512 : (h + 1) * 512])
+            cols = slice(h * S + j * P, h * S + (j + 1) * P)
+            nc.vector.quantize_mx(out=kc[b][:, cols].bitcast(FP8X4), scales=ks[b][:, cols], in_=yg["K%d" % i][:, h * 512 : (h + 1) * 512])
+
+        def quant_q(i, h):
+            cols = slice(h * P, (h + 1) * P)
+            nc.vector.quantize_mx(out=qc[i][:, cols].bitcast(FP8X4), scales=qs[i][:, cols], in_=yg["Q%d" % i][:, h * 512 : (h + 1) * 512])
 
         def score(i):
             b = i // PER_BATCH
-            sp[i] = banks.tile([P, S], F32, name="bank")
+            scores[i] = banks.tile([P, S], F32, name="bank")
             for h in range(2):
                 nc.tensor.matmul_mx(
-                    out=sp[i][:],
+                    out=scores[i][:],
                     lhsT=qc[i][:, h * P : (h + 1) * P].bitcast(FP8X4),
                     lhsT_scale=qs[i][:, h * P : (h + 1) * P],
                     rhs=kc[b][:, h * S : (h + 1) * S].bitcast(FP8X4),
@@ -198,111 +183,126 @@ def tile_attentionnet_pa_w4_kernel(tc, x_bytes, x_scale, wq_words, wq_scales, wk
                     stop=(h == 1),
                 )
 
-        def row_max(i):
-            mx = soft.tile([P, 1], F32, name="mx")
-            nb = soft.tile([P, 1], F32, name="nb")
-            nc.vector.tensor_reduce(out=mx[:], in_=sp[i][:], axis=AX.X, op=ALU.max)
-            ex[i] = [mx, nb]
+        def row_min(i):
+            nc.vector.tensor_scalar(out=neg[i][:], in0=scores[i][:], scalar1=-INV, scalar2=None, op0=ALU.mult, op1=ALU.min, accum_out=low[i][:])
 
         def exps(i):
-            mx, nb = ex[i]
-            nc.scalar.mul(nb[:], mx[:], -INV)
-            e = soft.tile([P, S], F32, name="e")
-            sm = soft.tile([P, 1], F32, name="sm")
-            nc.scalar.activation(out=e[:], in_=sp[i][:], func=ACT.Exp, bias=nb[:], scale=INV, accum_out=sm[:])
-            ex[i] = [e, sm]
+            nc.scalar.activation(out=ex[i][:], in_=neg[i][:], func=ACT.Exp, bias=low[i][:], scale=-1.0, accum_out=total[i][:])
 
         def invert(i):
-            e, sm = ex[i]
-            rc = soft.tile([P, 1], F32, name="rc")
-            nc.vector.reciprocal(rc[:], sm[:])
-            ex[i] = (e, rc)
+            nc.vector.reciprocal(inv[i][:], total[i][:])
 
         def finish(i):
-            e, rc = ex[i]
-            o = soft.tile([P, S], F32, name="o")
-            if i in NORM_SPLIT:
-                lo, hi = slice(0, NORM_COLS), slice(NORM_COLS, S)
-                nc.scalar.activation(out=o[:, hi], in_=e[:, hi], func=ACT.Copy, scale=rc[:])
-                nc.vector.tensor_scalar(out=o[:, lo], in0=e[:, lo], scalar1=rc[:], scalar2=None, op0=ALU.mult)
-                nc.scalar.dma_start(out=out_rows[i * P : (i + 1) * P, hi], in_=o[:, hi])
-                nc.sync.dma_start(out=out_rows[i * P : (i + 1) * P, lo], in_=o[:, lo])
-                return
-            if i in NORM_G:
-                nc.gpsimd.tensor_scalar(out=o[:], in0=e[:], scalar1=rc[:], scalar2=0.0, op0=ALU.mult, op1=ALU.add)
-            else:
-                nc.vector.tensor_scalar(out=o[:], in0=e[:], scalar1=rc[:], scalar2=None, op0=ALU.mult)
-            nc.sync.dma_start(out=out_rows[i * P : (i + 1) * P, :], in_=o[:])
+            nc.vector.tensor_scalar(out=res[i][:], in0=ex[i][:], scalar1=inv[i][:], scalar2=None, op0=ALU.mult)
+            nc.sync.dma_start(out=out_rows[i * P : (i + 1) * P, :], in_=res[i][:])
 
         ctx.enter_context(tc.manual_schedule())
+
         make_identity(nc, ident[:])
-        nc.vector.memset(warm[:], 0.0)
-        nc.scalar.activation(out=warm_out[:], in_=warm[:], func=ACT.Exp)
-        nc.vector.memset(raw_s["K"][:].bitcast(I32), 0)
-        nc.vector.memset(zeros[:], 0.0)
-        nc.vector.memset(raw_s["Q"][:].bitcast(I32), 0)
-        load_x(0)
-        nc.scalar.dma_start(out=scale_t[:].rearrange("p (g t) -> p g t", t=4), in_=x_scale.rearrange("a b (g p t) -> p (a b g) t", p=P, t=4))
-        for i in range(1, XFIRST):
-            load_x(i)
-        load_s("K")
-        load_w("K", 0)
-        load_w("K", 1)
-        load_x(XFIRST)
-        load_w("Q", 0)
-        load_w("Q", 1)
-        load_s("Q")
-        for i in range(XFIRST + 1, TILES):
-            load_x(i)
         for m in "KQ":
-            for h in range(2):
-                permute_s(m, h)
+            nc.vector.memset(raw_s[m][:].bitcast(I32), 0)
+        load_x(0)
+        nc.scalar.dma_start(out=scale_k[:].rearrange("p (g t) -> p g t", t=4), in_=x_scale.rearrange("a b (g p t) -> p (a b g) t", p=P, t=4))
+        load_w("K", 0)
+        load_s("K")
+        load_w("K", 1)
+        load_x(1)
+        load_w("Q", 0)
+        load_s("Q")
+        load_w("Q", 1)
+        for i in range(2, TILES):
+            load_x(i)
 
-        pending = {}
+        nc.vector.tensor_copy(out=xw[0][:, 0:512], in_=xb[0][:, 0:512].bitcast(FP8))
+        nc.scalar.activation(out=xw[0][:, 512:1024], in_=xb[0][:, 512:1024].bitcast(FP8), func=ACT.Copy)
+        first = []
+        words = xw[0][:].bitcast(F32)
+        for g in range(PASSES):
+            bank = banks.tile([P, 512], F32, name="bank")
+            for u in range(2):
+                nc.tensor.transpose(bank[:, u * P : (u + 1) * P], words[:, 256 * g + u : 256 * (g + 1) : 2], ident[:])
+            first.append(bank)
+        for g in range(PASSES):
+            spread_scales(g)
+        permute_w("K", 0)
+        scale_turned(0, 0, first[0][:, 0:256])
+        permute_s("K", 0)
+        scale_turned(0, 1, first[1][:, 0:256])
+        for g in range(PASSES):
+            cols = slice(g * P, (g + 1) * P)
+            nc.vector.quantize_mx(out=xc[0][:, cols].bitcast(FP8X4), scales=xs[0][:, cols], in_=xg[0][:, g * 512 : (g + 1) * 512])
+        permute_w("K", 1)
+        permute_s("K", 1)
+        for g in range(PASSES):
+            widen(1, g)
+        for h in range(2):
+            permute_w("Q", h)
+            permute_s("Q", h)
 
-        def later(n, fn, *args):
-            pending.setdefault(n, []).append((fn, args))
+        def halves(m, i):
+            return [(m, i, 0), (m, i, 1)]
 
-        for n, op in enumerate(SEQ):
-            kind, i = op[0], int(op[1:] or 0)
-            if kind == "D":
-                continue
+        def one(kind, i):
+            return [(kind, i, 0)]
+
+        steps = halves("K", 0) + one("T", 1) + halves("Q", 0) + one("T", 2)
+        steps += halves("K", 1) + halves("Q", 1) + one("T", 3) + one("T", 4)
+        steps += halves("K", 2) + halves("K", 3) + halves("Q", 2) + one("T", 5) + one("T", 6)
+        steps += halves("Q", 3) + one("S", 0) + one("T", 7)
+        for i in range(PER_BATCH, TILES - 1):
+            steps += halves("K", i) + one("S", i - PER_BATCH + 1)
+        steps += halves("K", 7) + halves("Q", 4) + halves("Q", 5) + one("S", 4) + halves("Q", 6) + halves("Q", 7)
+
+        later = {}
+
+        def after(n, rank, fn, *args):
+            later.setdefault(n, []).append((rank, len(later.get(n, [])), fn, args))
+
+        for n, (kind, i, h) in enumerate(steps):
             if kind == "T":
-                later(max(n - LAG_CAST, -1), cast, i)
-                later(n + LAG_SCALE, scale, i, 0)
-                later(n + LAG_SCALE, scale, i, 1)
-                if i == 0:
-                    later(n + LAG_SCALE, permute, "K", 0)
-                later(n + LAG_SCALE, quant_x, i)
-                if i == 0:
-                    later(n + LAG_SCALE, permute, "K", 1)
+                if i > 1:
+                    for g in range(PASSES):
+                        after(max(n - LEAD_WIDEN, 0) + g, 4, widen, i, g)
+                after(n + 1, 2, quant_x, i)
             elif kind == "S":
-                later(n + LAG_MAX, row_max, i)
-                later(n + LAG_MAX + LAG_EXP, exps, i)
-                later(n + LAG_MAX + LAG_EXP + LAG_INV, invert, i)
-                later(n + LAG_MAX + LAG_EXP + LAG_INV + LAG_NORM, finish, i)
+                after(n, 0, row_min, i)
+                lag = 1 if i == PER_BATCH else 2
+                after(n + lag, 0, exps, i)
+                after(n + 2 * lag, 3, invert, i)
+                after(n + 2 * lag + 1, 1, finish, i)
+            elif kind == "K":
+                after(n + 1, 2, quant_k, i, h)
             else:
-                later(n + LAG_QUANT, quant_y, kind, i)
+                after(n + 1, 2, quant_q, i, h)
 
-        def run_pending(n):
-            for fn, args in pending.get(n, []):
+        def run_later(n):
+            for rank, order, fn, args in sorted(later.get(n, []), key=lambda e: e[:2]):
                 fn(*args)
 
-        later(PERM_Q, permute, "Q", 0)
-        later(PERM_Q, permute, "Q", 1)
-        run_pending(-1)
-        for n, op in enumerate(SEQ):
-            kind, i = op[0], int(op[1:] or 0)
-            if kind == "D":
-                nc.tensor.matmul(dummy[:], zeros[:, 0:P], zeros[:], start=True, stop=True)
-            elif kind == "T":
-                turn(i)
+        for n, (kind, i, h) in enumerate(steps):
+            if kind == "T":
+                for g in range(PASSES):
+                    turn(i, g)
+                leave_turned(i)
             elif kind == "S":
                 score(i)
             else:
-                for h in range(2):
-                    project(kind, i, h)
-                    leave(kind, i, h)
-            run_pending(n)
-        for n in range(len(SEQ), len(SEQ) + 9):
-            run_pending(n)
+                project(kind, i, h)
+                leave(kind, i, h)
+            run_later(n)
+
+        tail = range(TILES - 3, TILES)
+        score(tail[0])
+        row_min(tail[0])
+        run_later(len(steps))
+        for i in tail[1:]:
+            score(i)
+            row_min(i)
+        for i in tail:
+            exps(i)
+        invert(tail[0])
+        invert(tail[1])
+        finish(tail[0])
+        finish(tail[1])
+        invert(tail[2])
+        finish(tail[2])

@@ -22,8 +22,7 @@ PER_BATCH = S // P
 PASSES = D // 512
 INV = 1.0 / math.sqrt(128.0)
 FLOPS = 2 * 2 * B * S * D * D + 2 * B * S * S * D
-LEAD_WIDEN = 6
-ON_VECTOR = [("Q", 4, 0), ("Q", 6, 1)]
+SPLIT = 320
 
 
 def tile_attentionnet_pa_w4_kernel(tc, x_bytes, x_scale, wq_words, wq_scales, wk_words, wk_scales, out):
@@ -39,24 +38,25 @@ def tile_attentionnet_pa_w4_kernel(tc, x_bytes, x_scale, wq_words, wq_scales, wk
             return {k: keep.tile(shape, dtype, name="%s_%s" % (name, k), align_bytes=64) for k in keys}
 
         every = range(TILES)
-        both = ["K%d" % i for i in every] + ["Q%d" % i for i in every]
+        halves = ["K0", "K1", "Q0", "Q1"]
         ident = keep.tile([P, P], F32, name="ident")
         scale_k = keep.tile([P, PASSES * 4], F32, name="scale_k")
-        scale_row = tiles("scale_row", range(PASSES), [P, 512], F32)
+        scale_row = keep.tile([P, D], F32, name="scale_row")
         xb = tiles("xb", every, [P, D], U8)
-        raw = tiles("raw", ["K0", "K1", "Q0", "Q1"], [P, 2048], U8)
+        raw = tiles("raw", halves, [P, 2048], U8)
         raw_s = tiles("raw_s", "KQ", [P, 2048], U8)
-        wts = tiles("wts", ["K0", "K1", "Q0", "Q1"], [P, 2048], U8)
-        wts_s = tiles("wts_s", ["K0", "K1", "Q0", "Q1"], [P, 1024], U8)
+        wts = tiles("wts", halves, [P, 2048], U8)
+        wts_s = tiles("wts_s", "KQ", [P, 2048], U8)
         xw = tiles("xw", every, [P, D], BF16)
-        xg = tiles("xg", every, [P, D], BF16)
-        xc = tiles("xc", every, [P, 256], U32)
-        xs = tiles("xs", every, [P, 256], U8)
-        yg = tiles("yg", both, [P, D], BF16)
-        kc = tiles("kc", range(B), [P, 1024], U32)
-        ks = tiles("ks", range(B), [P, 1024], U8)
-        qc = tiles("qc", every, [P, 256], U32)
-        qs = tiles("qs", every, [P, 256], U8)
+        xg = tiles("xg", range(TILES // 2), [P, 2 * D], BF16)
+        xc = tiles("xc", range(TILES // 2), [P, 512], U32)
+        xs = tiles("xs", range(TILES // 2), [P, 512], U8)
+        yk = tiles("yk", range(2 * B), [P, 4 * S], BF16)
+        kc = tiles("kc", range(2 * B), [P, S], U32)
+        ks = tiles("ks", range(2 * B), [P, S], U8)
+        yq = tiles("yq", range(TILES // 2), [P, 2 * D], BF16)
+        qc = tiles("qc", range(TILES // 2), [P, 512], U32)
+        qs = tiles("qs", range(TILES // 2), [P, 512], U8)
         neg = tiles("neg", every, [P, S], F32)
         low = tiles("low", every, [P, 1], F32)
         ex = tiles("ex", every, [P, S], F32)
@@ -68,7 +68,6 @@ def tile_attentionnet_pa_w4_kernel(tc, x_bytes, x_scale, wq_words, wq_scales, wk
         hbm_s = {"K": wk_scales, "Q": wq_scales}
         turned = {}
         scores = {}
-        projected = {}
 
         def load_x(i):
             nc.sync.dma_start(out=xb[i][:], in_=x_rows[i * P : (i + 1) * P, :])
@@ -91,94 +90,99 @@ def tile_attentionnet_pa_w4_kernel(tc, x_bytes, x_scale, wq_words, wq_scales, wk
                 in_=raw[m + str(h)][:].bitcast(I32).rearrange("p (c t w) -> p t c w", t=4, w=4),
             )
 
-        def permute_s(m, h):
-            src = raw_s[m][:].bitcast(I32).rearrange("p (g h c t w) -> p h g t c w", g=PASSES, h=2, t=4, w=2)
+        def permute_s(m):
             nc.vector.tensor_copy(
-                out=wts_s[m + str(h)][:].bitcast(I32).rearrange("p (g t c w) -> p g t c w", g=PASSES, t=4, w=2),
-                in_=src[:, h],
+                out=wts_s[m][:].bitcast(I32).rearrange("p (a t c w) -> p a t c w", a=4, t=4, w=2),
+                in_=raw_s[m][:].bitcast(I32).rearrange("p (a c t w) -> p a t c w", a=4, t=4, w=2),
             )
 
-        def turn(i, g):
-            if g == 0:
-                turned[i] = banks.tile([P, 512], F32, name="bank")
+        def quantize(codes, scales, values, first, count):
+            cols = slice(first * P, (first + count) * P)
+            nc.vector.quantize_mx(out=codes[:, cols].bitcast(FP8X4), scales=scales[:, cols], in_=values[:, first * 512 : (first + count) * 512])
+
+        def cast(i):
+            nc.scalar.activation(out=xw[i][:], in_=xb[i][:].bitcast(FP8), func=ACT.Copy)
+
+        def widen(i):
+            nc.vector.tensor_tensor(out=xw[i][:], in0=xb[i][:].bitcast(FP8), in1=scale_row[:], op=ALU.mult)
+
+        def turn(i):
+            turned[i] = banks.tile([P, 512], F32, name="bank")
             words = xw[i][:].bitcast(F32)
             for u in range(2):
-                nc.tensor.transpose(
-                    turned[i][:, g * 256 + u * P : g * 256 + (u + 1) * P],
-                    words[:, 256 * g + u : 256 * (g + 1) : 2],
-                    ident[:],
-                )
+                for g in range(PASSES):
+                    src = words[:, 256 * g + u : 256 * (g + 1) : 2]
+                    nc.tensor.transpose(turned[i][:, u * 256 + g * P : u * 256 + (g + 1) * P], src, ident[:])
 
-        def scale_turned(i, g, bank):
+        def x_values(i):
+            return xg[i // 2][:, (i % 2) * D : (i % 2 + 1) * D]
+
+        def scale_turned(i):
             nc.vector.tensor_tensor(
-                out=xg[i][:, g * 512 : (g + 1) * 512].rearrange("p (r u e) -> p r u e", u=2, e=2),
-                in0=bank.bitcast(BF16).rearrange("p (u r e) -> p r u e", u=2, e=2),
-                in1=scale_k[:, g * 4 : (g + 1) * 4].rearrange("p (u e) -> p u e", e=2).unsqueeze(1).to_broadcast([P, P, 2, 2]),
+                out=x_values(i).rearrange("p (g r u e) -> p g r u e", g=PASSES, u=2, e=2),
+                in0=turned[i][:].bitcast(BF16).rearrange("p (u g r e) -> p g r u e", g=PASSES, u=2, e=2),
+                in1=scale_k[:].rearrange("p (g u e) -> p g u e", u=2, e=2).unsqueeze(2).to_broadcast([P, PASSES, P, 2, 2]),
                 op=ALU.mult,
             )
 
-        def spread_scales(g):
-            bank = banks.tile([P, 512], F32, name="bank")
-            for t in range(4):
-                col = scale_k[:, g * 4 + t : g * 4 + t + 1].to_broadcast([P, P])
-                nc.tensor.transpose(bank[:, t * P : (t + 1) * P], col, ident[:])
-            nc.scalar.copy(scale_row[g][:].rearrange("p (n t) -> p n t", t=4), bank[:].rearrange("p (t n) -> p n t", t=4))
-
-        def widen(i, g):
-            cols = slice(g * 512, (g + 1) * 512)
-            nc.vector.tensor_tensor(out=xw[i][:, cols], in0=xb[i][:, cols].bitcast(FP8), in1=scale_row[g][:], op=ALU.mult)
-
         def leave_turned(i):
             nc.scalar.copy(
-                xg[i][:].bitcast(F32).rearrange("p (g r u) -> p g r u", g=PASSES, u=2),
-                turned[i][:].rearrange("p (g u r) -> p g r u", g=PASSES, u=2),
+                x_values(i).bitcast(F32).rearrange("p (r u) -> p r u", u=2),
+                turned[i][:].rearrange("p (u r) -> p r u", u=2),
             )
 
-        def quant_x(i):
-            nc.vector.quantize_mx(out=xc[i][:].bitcast(FP8X4), scales=xs[i][:], in_=xg[i][:])
+        def quant_x(i, count=1):
+            quantize(xc[i // 2], xs[i // 2], xg[i // 2], 2 * (i % 2), 2 * count)
 
-        def project(m, i, h):
+        def project(m, i, h, on_vector=False):
             bank = banks.tile([P, 512], F32, name="bank")
             for t in range(4):
                 for g in range(PASSES):
+                    cols = slice((2 * (i % 2) + g) * P, (2 * (i % 2) + g + 1) * P)
+                    plane = (2 * g + h) * 512 + t * P
                     nc.tensor.matmul_mx(
                         out=bank[:, t * P : (t + 1) * P],
                         lhsT=wts[m + str(h)][:, t * 512 + g * 256 : t * 512 + (g + 1) * 256].bitcast(FP4X4),
-                        lhsT_scale=wts_s[m + str(h)][:, g * 512 + t * P : g * 512 + (t + 1) * P],
-                        rhs=xc[i][:, g * P : (g + 1) * P].bitcast(FP8X4),
-                        rhs_scale=xs[i][:, g * P : (g + 1) * P],
+                        lhsT_scale=wts_s[m][:, plane : plane + P],
+                        rhs=xc[i // 2][:, cols].bitcast(FP8X4),
+                        rhs_scale=xs[i // 2][:, cols],
                         start=(g == 0),
                         stop=(g == PASSES - 1),
                     )
-            projected[m, i, h] = bank
-
-        def leave(m, i, h):
-            dst = yg[m + str(i)][:, h * 512 : (h + 1) * 512].rearrange("p (n t) -> p n t", t=4)
-            src = projected[m, i, h][:].rearrange("p (t n) -> p n t", t=4)
-            if (m, i, h) in ON_VECTOR:
+            b, j = divmod(i, PER_BATCH)
+            if m == "K":
+                dst = yk[2 * b + h][:, j * 512 : (j + 1) * 512]
+            else:
+                dst = yq[i // 2][:, (2 * (i % 2) + h) * 512 : (2 * (i % 2) + h + 1) * 512]
+            dst = dst.rearrange("p (n t) -> p n t", t=4)
+            src = bank[:].rearrange("p (t n) -> p n t", t=4)
+            if on_vector:
                 nc.vector.tensor_copy(out=dst, in_=src)
             else:
                 nc.scalar.copy(dst, src)
 
-        def quant_k(i, h):
-            b, j = divmod(i, PER_BATCH)
-            cols = slice(h * S + j * P, h * S + (j + 1) * P)
-            nc.vector.quantize_mx(out=kc[b][:, cols].bitcast(FP8X4), scales=ks[b][:, cols], in_=yg["K%d" % i][:, h * 512 : (h + 1) * 512])
+        def project_both(m, i):
+            for h in range(2):
+                project(m, i, h)
 
-        def quant_q(i, h):
-            cols = slice(h * P, (h + 1) * P)
-            nc.vector.quantize_mx(out=qc[i][:, cols].bitcast(FP8X4), scales=qs[i][:, cols], in_=yg["Q%d" % i][:, h * 512 : (h + 1) * 512])
+        def quant_k(i, h):
+            n = 2 * (i // PER_BATCH) + h
+            quantize(kc[n], ks[n], yk[n], i % PER_BATCH, 2)
+
+        def quant_q(i, first, count):
+            quantize(qc[i // 2], qs[i // 2], yq[i // 2], 2 * (i % 2) + first, count)
 
         def score(i):
             b = i // PER_BATCH
             scores[i] = banks.tile([P, S], F32, name="bank")
             for h in range(2):
+                cols = slice((2 * (i % 2) + h) * P, (2 * (i % 2) + h + 1) * P)
                 nc.tensor.matmul_mx(
                     out=scores[i][:],
-                    lhsT=qc[i][:, h * P : (h + 1) * P].bitcast(FP8X4),
-                    lhsT_scale=qs[i][:, h * P : (h + 1) * P],
-                    rhs=kc[b][:, h * S : (h + 1) * S].bitcast(FP8X4),
-                    rhs_scale=ks[b][:, h * S : (h + 1) * S],
+                    lhsT=qc[i // 2][:, cols].bitcast(FP8X4),
+                    lhsT_scale=qs[i // 2][:, cols],
+                    rhs=kc[2 * b + h][:].bitcast(FP8X4),
+                    rhs_scale=ks[2 * b + h][:],
                     start=(h == 0),
                     stop=(h == 1),
                 )
@@ -203,18 +207,21 @@ def tile_attentionnet_pa_w4_kernel(tc, x_bytes, x_scale, wq_words, wq_scales, wk
             nc.vector.memset(raw_s[m][:].bitcast(I32), 0)
         load_x(0)
         nc.scalar.dma_start(out=scale_k[:].rearrange("p (g t) -> p g t", t=4), in_=x_scale.rearrange("a b (g p t) -> p (a b g) t", p=P, t=4))
+        load_x(1)
         load_w("K", 0)
+        load_x(2)
         load_s("K")
         load_w("K", 1)
-        load_x(1)
+        load_x(3)
         load_w("Q", 0)
         load_s("Q")
         load_w("Q", 1)
-        for i in range(2, TILES):
+        nc.sync.dma_start(out=scale_row[:], in_=x_scale.rearrange("a b k -> (a b k)").partition_broadcast(P))
+        for i in range(4, TILES):
             load_x(i)
 
         nc.vector.tensor_copy(out=xw[0][:, 0:512], in_=xb[0][:, 0:512].bitcast(FP8))
-        nc.scalar.activation(out=xw[0][:, 512:1024], in_=xb[0][:, 512:1024].bitcast(FP8), func=ACT.Copy)
+        nc.scalar.activation(out=xw[0][:, 512:D], in_=xb[0][:, 512:D].bitcast(FP8), func=ACT.Copy)
         first = []
         words = xw[0][:].bitcast(F32)
         for g in range(PASSES):
@@ -222,87 +229,117 @@ def tile_attentionnet_pa_w4_kernel(tc, x_bytes, x_scale, wq_words, wq_scales, wk
             for u in range(2):
                 nc.tensor.transpose(bank[:, u * P : (u + 1) * P], words[:, 256 * g + u : 256 * (g + 1) : 2], ident[:])
             first.append(bank)
-        for g in range(PASSES):
-            spread_scales(g)
+        for i in (1, 2):
+            cast(i)
+            turn(i)
+        cast(3)
         permute_w("K", 0)
-        scale_turned(0, 0, first[0][:, 0:256])
-        permute_s("K", 0)
-        scale_turned(0, 1, first[1][:, 0:256])
         for g in range(PASSES):
-            cols = slice(g * P, (g + 1) * P)
-            nc.vector.quantize_mx(out=xc[0][:, cols].bitcast(FP8X4), scales=xs[0][:, cols], in_=xg[0][:, g * 512 : (g + 1) * 512])
+            nc.vector.tensor_tensor(
+                out=xg[0][:, g * 512 : (g + 1) * 512].rearrange("p (r u e) -> p r u e", u=2, e=2),
+                in0=first[g][:, 0:256].bitcast(BF16).rearrange("p (u r e) -> p r u e", u=2, e=2),
+                in1=scale_k[:, g * 4 : (g + 1) * 4].rearrange("p (u e) -> p u e", e=2).unsqueeze(1).to_broadcast([P, P, 2, 2]),
+                op=ALU.mult,
+            )
+        permute_s("K")
+        for g in range(PASSES):
+            quantize(xc[0], xs[0], xg[0], g, 1)
         permute_w("K", 1)
-        permute_s("K", 1)
-        for g in range(PASSES):
-            widen(1, g)
+        scale_turned(1)
+        permute_w("Q", 0)
+        permute_s("Q")
+        permute_w("Q", 1)
+        quant_x(1)
+        scale_turned(2)
+
+        project_both("K", 0)
+        turn(3)
+        project_both("Q", 0)
+        project_both("K", 1)
+        scale_turned(3)
+        quant_x(2)
+        widen(4)
+        quant_x(3)
+        widen(5)
+        project_both("Q", 1)
+        project_both("K", 2)
+        for i in (4, 5):
+            turn(i)
+            leave_turned(i)
         for h in range(2):
-            permute_w("Q", h)
-            permute_s("Q", h)
+            quant_k(0, h)
+        widen(6)
+        quant_q(0, 0, 4)
+        project_both("K", 3)
+        quant_x(4, 2)
+        widen(7)
+        project_both("Q", 2)
+        for h in range(2):
+            quant_k(2, h)
+        project_both("Q", 3)
+        score(0)
+        for i in (6, 7):
+            turn(i)
+            leave_turned(i)
+        row_min(0)
+        quant_q(2, 0, 4)
 
-        def halves(m, i):
-            return [(m, i, 0), (m, i, 1)]
-
-        def one(kind, i):
-            return [(kind, i, 0)]
-
-        steps = halves("K", 0) + one("T", 1) + halves("Q", 0) + one("T", 2)
-        steps += halves("K", 1) + halves("Q", 1) + one("T", 3) + one("T", 4)
-        steps += halves("K", 2) + halves("K", 3) + halves("Q", 2) + one("T", 5) + one("T", 6)
-        steps += halves("Q", 3) + one("S", 0) + one("T", 7)
-        for i in range(PER_BATCH, TILES - 1):
-            steps += halves("K", i) + one("S", i - PER_BATCH + 1)
-        steps += halves("K", 7) + halves("Q", 4) + halves("Q", 5) + one("S", 4) + halves("Q", 6) + halves("Q", 7)
-
-        later = {}
-
-        def after(n, rank, fn, *args):
-            later.setdefault(n, []).append((rank, len(later.get(n, [])), fn, args))
-
-        for n, (kind, i, h) in enumerate(steps):
-            if kind == "T":
-                if i > 1:
-                    for g in range(PASSES):
-                        after(max(n - LEAD_WIDEN, 0) + g, 4, widen, i, g)
-                after(n + 1, 2, quant_x, i)
-            elif kind == "S":
-                after(n, 0, row_min, i)
-                lag = 1 if i == PER_BATCH else 2
-                after(n + lag, 0, exps, i)
-                after(n + 2 * lag, 3, invert, i)
-                after(n + 2 * lag + 1, 1, finish, i)
-            elif kind == "K":
-                after(n + 1, 2, quant_k, i, h)
+        for j in range(1, PER_BATCH):
+            i = PER_BATCH + j - 1
+            project_both("K", i)
+            exps(j - 1)
+            score(j)
+            if j == 1:
+                quant_x(6, 2)
             else:
-                after(n + 1, 2, quant_q, i, h)
+                invert(j - 2)
+            if j == 3:
+                for h in range(2):
+                    quant_k(PER_BATCH, h)
+            if j > 1:
+                finish(j - 2)
+            row_min(j)
+        project_both("K", 7)
+        exps(3)
+        invert(2)
+        quant_k(6, 0)
+        finish(2)
+        project("Q", 4, 0, on_vector=True)
+        project("Q", 4, 1)
+        quant_k(6, 1)
+        quant_q(4, 0, 1)
+        invert(3)
+        project_both("Q", 5)
+        quant_q(4, 1, 1)
+        finish(3)
+        score(4)
+        project("Q", 6, 0)
+        row_min(4)
+        exps(4)
+        quant_q(5, 0, 2)
+        project("Q", 6, 1, on_vector=True)
+        project_both("Q", 7)
+        invert(4)
+        quant_q(6, 0, 2)
+        finish(4)
+        quant_q(7, 0, 1)
 
-        def run_later(n):
-            for rank, order, fn, args in sorted(later.get(n, []), key=lambda e: e[:2]):
-                fn(*args)
-
-        for n, (kind, i, h) in enumerate(steps):
-            if kind == "T":
-                for g in range(PASSES):
-                    turn(i, g)
-                leave_turned(i)
-            elif kind == "S":
-                score(i)
-            else:
-                project(kind, i, h)
-                leave(kind, i, h)
-            run_later(n)
-
-        tail = range(TILES - 3, TILES)
-        score(tail[0])
-        row_min(tail[0])
-        run_later(len(steps))
-        for i in tail[1:]:
+        score(5)
+        row_min(5)
+        quant_q(7, 1, 1)
+        for i in (6, 7):
             score(i)
             row_min(i)
-        for i in tail:
+        for i in (5, 6, 7):
             exps(i)
-        invert(tail[0])
-        invert(tail[1])
-        finish(tail[0])
-        finish(tail[1])
-        invert(tail[2])
-        finish(tail[2])
+        invert(5)
+        invert(6)
+        finish(5)
+        finish(6)
+        invert(7)
+        rows = slice((TILES - 1) * P, TILES * P)
+        left, right = slice(0, SPLIT), slice(SPLIT, S)
+        nc.vector.tensor_scalar(out=res[7][:, left], in0=ex[7][:, left], scalar1=inv[7][:], scalar2=None, op0=ALU.mult)
+        nc.scalar.activation(out=res[7][:, right], in_=ex[7][:, right], func=ACT.Copy, scale=inv[7][:])
+        nc.sync.dma_start(out=out_rows[rows, left], in_=res[7][:, left])
+        nc.scalar.dma_start(out=out_rows[rows, right], in_=res[7][:, right])

@@ -39,6 +39,8 @@ def tile_attentionnet_pa_w4_kernel(tc, x_bytes, x_scale, wq_words, wq_scales, wk
 
         every = range(TILES)
         halves = ["K0", "K1", "Q0", "Q1"]
+        zeros = keep.tile([P, 512], BF16, name="zeros")
+        idle_bank = banks.tile([P, 512], F32, name="bank")
         ident = keep.tile([P, P], F32, name="ident")
         scale_k = keep.tile([P, PASSES * 4], F32, name="scale_k")
         scale_row = keep.tile([P, D], F32, name="scale_row")
@@ -99,6 +101,10 @@ def tile_attentionnet_pa_w4_kernel(tc, x_bytes, x_scale, wq_words, wq_scales, wk
         def quantize(codes, scales, values, first, count):
             cols = slice(first * P, (first + count) * P)
             nc.vector.quantize_mx(out=codes[:, cols].bitcast(FP8X4), scales=scales[:, cols], in_=values[:, first * 512 : (first + count) * 512])
+
+        def warm_up(count):
+            for n in range(count):
+                nc.tensor.matmul(idle_bank[:], zeros[:, 0:P], zeros[:], start=True, stop=True)
 
         def cast(i):
             nc.scalar.activation(out=xw[i][:], in_=xb[i][:].bitcast(FP8), func=ACT.Copy)
@@ -203,8 +209,9 @@ def tile_attentionnet_pa_w4_kernel(tc, x_bytes, x_scale, wq_words, wq_scales, wk
         ctx.enter_context(tc.manual_schedule())
 
         make_identity(nc, ident[:])
-        for m in "KQ":
-            nc.vector.memset(raw_s[m][:].bitcast(I32), 0)
+        nc.vector.memset(raw_s["K"][:].bitcast(I32), 0)
+        nc.vector.memset(zeros[:], 0.0)
+        nc.vector.memset(raw_s["Q"][:].bitcast(I32), 0)
         load_x(0)
         nc.scalar.dma_start(out=scale_k[:].rearrange("p (g t) -> p g t", t=4), in_=x_scale.rearrange("a b (g p t) -> p (a b g) t", p=P, t=4))
         load_x(1)
@@ -220,6 +227,7 @@ def tile_attentionnet_pa_w4_kernel(tc, x_bytes, x_scale, wq_words, wq_scales, wk
         for i in range(4, TILES):
             load_x(i)
 
+        warm_up(3)
         nc.vector.tensor_copy(out=xw[0][:, 0:512], in_=xb[0][:, 0:512].bitcast(FP8))
         nc.scalar.activation(out=xw[0][:, 512:D], in_=xb[0][:, 512:D].bitcast(FP8), func=ACT.Copy)
         first = []
@@ -230,6 +238,7 @@ def tile_attentionnet_pa_w4_kernel(tc, x_bytes, x_scale, wq_words, wq_scales, wk
                 nc.tensor.transpose(bank[:, u * P : (u + 1) * P], words[:, 256 * g + u : 256 * (g + 1) : 2], ident[:])
             first.append(bank)
         for i in (1, 2):
+            warm_up(1)
             cast(i)
             turn(i)
         cast(3)

@@ -83,8 +83,8 @@ def tile_attentionnet_pa_w4_kernel(tc, x_bytes, x_scale, wq_words, wq_scales, wk
         def load_s(m):
             dst = raw_s[m][:].bitcast(I32).rearrange("p (g n) -> p g n", g=PASSES)
             src = hbm_s[m].bitcast(I32)
-            for q in range(4):
-                nc.sync.dma_start(out=dst[32 * q : 32 * q + 4], in_=src[:, 4 * q : 4 * q + 4, :].rearrange("g r n -> r g n"))
+            for r in range(4):
+                nc.sync.dma_start(out=dst[r:P:32], in_=src[:, r:16:4, :].rearrange("g q n -> q g n"))
 
         def permute_w(m, h):
             nc.vector.tensor_copy(
@@ -111,6 +111,16 @@ def tile_attentionnet_pa_w4_kernel(tc, x_bytes, x_scale, wq_words, wq_scales, wk
 
         def widen(i):
             nc.vector.tensor_tensor(out=xw[i][:], in0=xb[i][:].bitcast(FP8), in1=scale_row[:], op=ALU.mult)
+
+        def spread_scales(g):
+            bank = banks.tile([P, 512], F32, name="bank")
+            for t in range(4):
+                col = scale_k[:, g * 4 + t : g * 4 + t + 1].to_broadcast([P, P])
+                nc.tensor.transpose(bank[:, t * P : (t + 1) * P], col, ident[:])
+            return bank
+
+        def leave_spread(g, bank):
+            nc.scalar.copy(scale_row[:, g * 512 : (g + 1) * 512].rearrange("p (n t) -> p n t", t=4), bank[:].rearrange("p (t n) -> p n t", t=4))
 
         def turn(i):
             turned[i] = banks.tile([P, 512], F32, name="bank")
@@ -214,17 +224,15 @@ def tile_attentionnet_pa_w4_kernel(tc, x_bytes, x_scale, wq_words, wq_scales, wk
         nc.vector.memset(raw_s["Q"][:].bitcast(I32), 0)
         load_x(0)
         nc.scalar.dma_start(out=scale_k[:].rearrange("p (g t) -> p g t", t=4), in_=x_scale.rearrange("a b (g p t) -> p (a b g) t", p=P, t=4))
-        load_x(1)
-        load_w("K", 0)
-        load_x(2)
         load_s("K")
-        load_w("K", 1)
-        load_x(3)
-        load_w("Q", 0)
+        load_x(1)
+        for h in range(2):
+            load_w("K", h)
+        load_x(2)
         load_s("Q")
-        load_w("Q", 1)
-        nc.sync.dma_start(out=scale_row[:], in_=x_scale.rearrange("a b k -> (a b k)").partition_broadcast(P))
-        for i in range(4, TILES):
+        for h in range(2):
+            load_w("Q", h)
+        for i in range(3, TILES):
             load_x(i)
 
         warm_up(3)
@@ -237,12 +245,14 @@ def tile_attentionnet_pa_w4_kernel(tc, x_bytes, x_scale, wq_words, wq_scales, wk
             for u in range(2):
                 nc.tensor.transpose(bank[:, u * P : (u + 1) * P], words[:, 256 * g + u : 256 * (g + 1) : 2], ident[:])
             first.append(bank)
-        for i in (1, 2):
-            warm_up(1)
-            cast(i)
-            turn(i)
-        cast(3)
-        permute_w("K", 0)
+        spread = [spread_scales(g) for g in range(PASSES)]
+        warm_up(2)
+        cast(1)
+        turn(1)
+        leave_spread(0, spread[0])
+        cast(2)
+        leave_spread(1, spread[1])
+        permute_s("K")
         for g in range(PASSES):
             nc.vector.tensor_tensor(
                 out=xg[0][:, g * 512 : (g + 1) * 512].rearrange("p (r u e) -> p r u e", u=2, e=2),
@@ -250,46 +260,51 @@ def tile_attentionnet_pa_w4_kernel(tc, x_bytes, x_scale, wq_words, wq_scales, wk
                 in1=scale_k[:, g * 4 : (g + 1) * 4].rearrange("p (u e) -> p u e", e=2).unsqueeze(1).to_broadcast([P, P, 2, 2]),
                 op=ALU.mult,
             )
-        permute_s("K")
+            if g == 0:
+                permute_w("K", 0)
         for g in range(PASSES):
             quantize(xc[0], xs[0], xg[0], g, 1)
         permute_w("K", 1)
         scale_turned(1)
-        permute_w("Q", 0)
         permute_s("Q")
-        permute_w("Q", 1)
+        for h in range(2):
+            permute_w("Q", h)
         quant_x(1)
-        scale_turned(2)
 
         project_both("K", 0)
-        turn(3)
-        project_both("Q", 0)
-        project_both("K", 1)
-        scale_turned(3)
+        turn(2)
+        scale_turned(2)
+        widen(3)
         quant_x(2)
         widen(4)
-        quant_x(3)
-        widen(5)
+        project_both("Q", 0)
+        project_both("K", 1)
         project_both("Q", 1)
-        project_both("K", 2)
-        for i in (4, 5):
+        for i in (3, 4):
             turn(i)
             leave_turned(i)
         for h in range(2):
             quant_k(0, h)
+        widen(5)
+        quant_x(3)
+        project_both("K", 2)
         widen(6)
+        quant_x(4)
         quant_q(0, 0, 4)
         project_both("K", 3)
-        quant_x(4, 2)
         widen(7)
         project_both("Q", 2)
+        for i in (5, 6):
+            turn(i)
+            leave_turned(i)
         for h in range(2):
             quant_k(2, h)
         project_both("Q", 3)
+        quant_x(5)
+        quant_x(6)
         score(0)
-        for i in (6, 7):
-            turn(i)
-            leave_turned(i)
+        turn(7)
+        leave_turned(7)
         row_min(0)
         quant_q(2, 0, 4)
 
@@ -299,7 +314,7 @@ def tile_attentionnet_pa_w4_kernel(tc, x_bytes, x_scale, wq_words, wq_scales, wk
             exps(j - 1)
             score(j)
             if j == 1:
-                quant_x(6, 2)
+                quant_x(7)
             else:
                 invert(j - 2)
             if j == 3:

@@ -23,6 +23,7 @@ PASSES = D // 512
 INV = 1.0 / math.sqrt(128.0)
 FLOPS = 2 * 2 * B * S * D * D + 2 * B * S * S * D
 SPLIT = 320
+ON_SCALAR = (1, 2, 7)
 
 
 def tile_attentionnet_pa_w4_kernel(tc, x_bytes, x_scale, wq_words, wq_scales, wk_words, wk_scales, out):
@@ -43,7 +44,7 @@ def tile_attentionnet_pa_w4_kernel(tc, x_bytes, x_scale, wq_words, wq_scales, wk
         idle_bank = banks.tile([P, 512], F32, name="bank")
         ident = keep.tile([P, P], F32, name="ident")
         scale_k = keep.tile([P, PASSES * 4], F32, name="scale_k")
-        scale_row = keep.tile([P, D], F32, name="scale_row")
+        ones = keep.tile([P, 1], F32, name="ones")
         xb = tiles("xb", every, [P, D], U8)
         raw = tiles("raw", halves, [P, 2048], U8)
         raw_s = tiles("raw_s", "KQ", [P, 2048], U8)
@@ -110,24 +111,26 @@ def tile_attentionnet_pa_w4_kernel(tc, x_bytes, x_scale, wq_words, wq_scales, wk
             nc.scalar.activation(out=xw[i][:], in_=xb[i][:].bitcast(FP8), func=ACT.Copy)
 
         def widen(i):
-            nc.vector.tensor_tensor(out=xw[i][:], in0=xb[i][:].bitcast(FP8), in1=scale_row[:], op=ALU.mult)
-
-        def spread_scales(g):
-            bank = banks.tile([P, 512], F32, name="bank")
-            for t in range(4):
-                col = scale_k[:, g * 4 + t : g * 4 + t + 1].to_broadcast([P, P])
-                nc.tensor.transpose(bank[:, t * P : (t + 1) * P], col, ident[:])
-            return bank
-
-        def leave_spread(g, bank):
-            nc.scalar.copy(scale_row[:, g * 512 : (g + 1) * 512].rearrange("p (n t) -> p n t", t=4), bank[:].rearrange("p (t n) -> p n t", t=4))
+            if i in ON_SCALAR:
+                cast(i)
+                return
+            nc.vector.tensor_scalar(
+                out=xw[i][:].rearrange("p (u w e) -> p w u e", u=2, e=2),
+                in0=xb[i][:].bitcast(FP8).rearrange("p (w u e) -> p w u e", u=2, e=2),
+                scalar1=ones[:],
+                scalar2=None,
+                op0=ALU.mult,
+            )
 
         def turn(i):
             turned[i] = banks.tile([P, 512], F32, name="bank")
             words = xw[i][:].bitcast(F32)
             for u in range(2):
                 for g in range(PASSES):
-                    src = words[:, 256 * g + u : 256 * (g + 1) : 2]
+                    if i in ON_SCALAR:
+                        src = words[:, 256 * g + u : 256 * (g + 1) : 2]
+                    else:
+                        src = words[:, u * 256 + g * P : u * 256 + (g + 1) * P]
                     nc.tensor.transpose(turned[i][:, u * 256 + g * P : u * 256 + (g + 1) * P], src, ident[:])
 
         def x_values(i):
@@ -139,12 +142,6 @@ def tile_attentionnet_pa_w4_kernel(tc, x_bytes, x_scale, wq_words, wq_scales, wk
                 in0=turned[i][:].bitcast(BF16).rearrange("p (u g r e) -> p g r u e", g=PASSES, u=2, e=2),
                 in1=scale_k[:].rearrange("p (g u e) -> p g u e", u=2, e=2).unsqueeze(2).to_broadcast([P, PASSES, P, 2, 2]),
                 op=ALU.mult,
-            )
-
-        def leave_turned(i):
-            nc.scalar.copy(
-                x_values(i).bitcast(F32).rearrange("p (r u) -> p r u", u=2),
-                turned[i][:].rearrange("p (u r) -> p r u", u=2),
             )
 
         def quant_x(i, count=1):
@@ -219,6 +216,7 @@ def tile_attentionnet_pa_w4_kernel(tc, x_bytes, x_scale, wq_words, wq_scales, wk
         ctx.enter_context(tc.manual_schedule())
 
         make_identity(nc, ident[:])
+        nc.gpsimd.memset(ones[:], 1.0)
         nc.vector.memset(raw_s["K"][:].bitcast(I32), 0)
         nc.vector.memset(zeros[:], 0.0)
         nc.vector.memset(raw_s["Q"][:].bitcast(I32), 0)
@@ -245,13 +243,10 @@ def tile_attentionnet_pa_w4_kernel(tc, x_bytes, x_scale, wq_words, wq_scales, wk
             for u in range(2):
                 nc.tensor.transpose(bank[:, u * P : (u + 1) * P], words[:, 256 * g + u : 256 * (g + 1) : 2], ident[:])
             first.append(bank)
-        spread = [spread_scales(g) for g in range(PASSES)]
         warm_up(2)
         cast(1)
         turn(1)
-        leave_spread(0, spread[0])
         cast(2)
-        leave_spread(1, spread[1])
         permute_s("K")
         for g in range(PASSES):
             nc.vector.tensor_tensor(
@@ -275,37 +270,37 @@ def tile_attentionnet_pa_w4_kernel(tc, x_bytes, x_scale, wq_words, wq_scales, wk
         turn(2)
         scale_turned(2)
         widen(3)
-        quant_x(2)
         widen(4)
+        quant_x(2)
         project_both("Q", 0)
         project_both("K", 1)
-        project_both("Q", 1)
-        for i in (3, 4):
-            turn(i)
-            leave_turned(i)
-        for h in range(2):
-            quant_k(0, h)
+        turn(3)
+        turn(4)
+        scale_turned(3)
         widen(5)
         quant_x(3)
-        project_both("K", 2)
         widen(6)
+        project_both("Q", 1)
+        project_both("K", 2)
+        scale_turned(4)
+        for h in range(2):
+            quant_k(0, h)
         quant_x(4)
-        quant_q(0, 0, 4)
         project_both("K", 3)
         widen(7)
+        turn(5)
+        turn(6)
+        quant_q(0, 0, 4)
+        scale_turned(5)
         project_both("Q", 2)
-        for i in (5, 6):
-            turn(i)
-            leave_turned(i)
         for h in range(2):
             quant_k(2, h)
-        project_both("Q", 3)
         quant_x(5)
-        quant_x(6)
+        project_both("Q", 3)
         score(0)
-        turn(7)
-        leave_turned(7)
+        scale_turned(6)
         row_min(0)
+        quant_x(6)
         quant_q(2, 0, 4)
 
         for j in range(1, PER_BATCH):
@@ -314,7 +309,7 @@ def tile_attentionnet_pa_w4_kernel(tc, x_bytes, x_scale, wq_words, wq_scales, wk
             exps(j - 1)
             score(j)
             if j == 1:
-                quant_x(7)
+                turn(7)
             else:
                 invert(j - 2)
             if j == 3:
@@ -323,6 +318,10 @@ def tile_attentionnet_pa_w4_kernel(tc, x_bytes, x_scale, wq_words, wq_scales, wk
             if j > 1:
                 finish(j - 2)
             row_min(j)
+            if j == 1:
+                scale_turned(7)
+            if j == 2:
+                quant_x(7)
         project_both("K", 7)
         exps(3)
         invert(2)

@@ -38,6 +38,11 @@ def tile_attentionnet_pa_w4_kernel(tc, x_bytes, x_scale, wq_words, wq_scales, wk
         def tiles(name, keys, shape, dtype):
             return {k: keep.tile(shape, dtype, name="%s_%s" % (name, k), align_bytes=64) for k in keys}
 
+        def placed(name, keys, count, dtype, size, start):
+            first = start // size
+            made = {k: keep.tile([P, count + 256 // size], dtype, name="%s_%s" % (name, k), align_bytes=256) for k in keys}
+            return {k: made[k][:, first : first + count] for k in keys}
+
         every = range(TILES)
         halves = ["K0", "K1", "Q0", "Q1"]
         zeros = keep.tile([P, 512], BF16, name="zeros")
@@ -48,12 +53,12 @@ def tile_attentionnet_pa_w4_kernel(tc, x_bytes, x_scale, wq_words, wq_scales, wk
         xb = tiles("xb", every, [P, D], U8)
         raw = tiles("raw", halves, [P, 2048], U8)
         raw_s = tiles("raw_s", "KQ", [P, 2048], U8)
-        wts = tiles("wts", halves, [P, 2048], U8)
-        wts_s = tiles("wts_s", "KQ", [P, 2048], U8)
+        wts = placed("wts", halves, 2048, U8, 1, 0)
+        wts_s = placed("wts_s", "KQ", 2048, U8, 1, 64)
         xw = tiles("xw", every, [P, D], BF16)
         xg = tiles("xg", range(TILES // 2), [P, 2 * D], BF16)
-        xc = tiles("xc", range(TILES // 2), [P, 512], U32)
-        xs = tiles("xs", range(TILES // 2), [P, 512], U8)
+        xc = placed("xc", range(TILES // 2), 512, U32, 4, 128)
+        xs = placed("xs", range(TILES // 2), 512, U8, 1, 0)
         yk = tiles("yk", range(2 * B), [P, 4 * S], BF16)
         kc = tiles("kc", range(2 * B), [P, S], U32)
         ks = tiles("ks", range(2 * B), [P, S], U8)

@@ -36,12 +36,7 @@ def tile_attentionnet_pa_w4_kernel(tc, x_bytes, x_scale, wq_words, wq_scales, wk
         banks = ctx.enter_context(tc.psum_pool(name="banks", bufs=8))
 
         def tiles(name, keys, shape, dtype):
-            return {k: keep.tile(shape, dtype, name="%s_%s" % (name, k), align_bytes=64) for k in keys}
-
-        def placed(name, keys, count, dtype, size, start):
-            first = start // size
-            made = {k: keep.tile([P, count + 256 // size], dtype, name="%s_%s" % (name, k), align_bytes=256) for k in keys}
-            return {k: made[k][:, first : first + count] for k in keys}
+            return {k: keep.tile(shape, dtype, name="%s_%s" % (name, k), align_bytes=256) for k in keys}
 
         every = range(TILES)
         halves = ["K0", "K1", "Q0", "Q1"]
@@ -53,12 +48,12 @@ def tile_attentionnet_pa_w4_kernel(tc, x_bytes, x_scale, wq_words, wq_scales, wk
         xb = tiles("xb", every, [P, D], U8)
         raw = tiles("raw", halves, [P, 2048], U8)
         raw_s = tiles("raw_s", "KQ", [P, 2048], U8)
-        wts = placed("wts", halves, 2048, U8, 1, 0)
-        wts_s = placed("wts_s", "KQ", 2048, U8, 1, 64)
+        wts = tiles("wts", halves, [P, 2048], U8)
+        wts_s = tiles("wts_s", "KQ", [P, 2048], U8)
         xw = tiles("xw", every, [P, D], BF16)
         xg = tiles("xg", range(TILES // 2), [P, 2 * D], BF16)
-        xc = placed("xc", range(TILES // 2), 512, U32, 4, 128)
-        xs = placed("xs", range(TILES // 2), 512, U8, 1, 0)
+        xc = tiles("xc", range(TILES // 2), [P, 512], U32)
+        xs = tiles("xs", range(TILES // 2), [P, 512], U8)
         yk = tiles("yk", range(2 * B), [P, 4 * S], BF16)
         kc = tiles("kc", range(2 * B), [P, S], U32)
         ks = tiles("ks", range(2 * B), [P, S], U8)
@@ -260,8 +255,7 @@ def tile_attentionnet_pa_w4_kernel(tc, x_bytes, x_scale, wq_words, wq_scales, wk
                 in1=scale_k[:, g * 4 : (g + 1) * 4].rearrange("p (u e) -> p u e", e=2).unsqueeze(1).to_broadcast([P, P, 2, 2]),
                 op=ALU.mult,
             )
-            if g == 0:
-                permute_w("K", 0)
+        permute_w("K", 0)
         for g in range(PASSES):
             quantize(xc[0], xs[0], xg[0], g, 1)
         permute_w("K", 1)

@@ -49,7 +49,7 @@ def tile_attentionnet_pa_w4_kernel(tc, x_bytes, x_scale, wq_words, wq_scales, wk
         raw = tiles("raw", halves, [P, 2048], U8)
         raw_s = tiles("raw_s", "KQ", [P, 2048], U8)
         wts = tiles("wts", halves, [P, 2048], U8)
-        wts_s = tiles("wts_s", "KQ", [P, 2048], U8)
+        wts_s = tiles("wts_s", halves, [P, 1024], U8)
         xw = tiles("xw", every, [P, D], BF16)
         xg = tiles("xg", range(TILES // 2), [P, 2 * D], BF16)
         xc = tiles("xc", range(TILES // 2), [P, 512], U32)
@@ -93,10 +93,11 @@ def tile_attentionnet_pa_w4_kernel(tc, x_bytes, x_scale, wq_words, wq_scales, wk
                 in_=raw[m + str(h)][:].bitcast(I32).rearrange("p (c t w) -> p t c w", t=4, w=4),
             )
 
-        def permute_s(m):
+        def permute_s(m, h):
+            src = raw_s[m][:].bitcast(I32).rearrange("p (g h c t w) -> p h t g c w", g=PASSES, h=2, t=4, w=2)
             nc.vector.tensor_copy(
-                out=wts_s[m][:].bitcast(I32).rearrange("p (a t c w) -> p a t c w", a=4, t=4, w=2),
-                in_=raw_s[m][:].bitcast(I32).rearrange("p (a c t w) -> p a t c w", a=4, t=4, w=2),
+                out=wts_s[m + str(h)][:].bitcast(I32).rearrange("p (t g c w) -> p t g c w", g=PASSES, t=4, w=2),
+                in_=src[:, h],
             )
 
         def quantize(codes, scales, values, first, count):
@@ -136,11 +137,11 @@ def tile_attentionnet_pa_w4_kernel(tc, x_bytes, x_scale, wq_words, wq_scales, wk
         def x_values(i):
             return xg[i // 2][:, (i % 2) * D : (i % 2 + 1) * D]
 
-        def scale_turned(i):
+        def scale_turned(i, passes=slice(0, PASSES)):
             nc.vector.tensor_tensor(
-                out=x_values(i).rearrange("p (g r u e) -> p g r u e", g=PASSES, u=2, e=2),
-                in0=turned[i][:].bitcast(BF16).rearrange("p (u g r e) -> p g r u e", g=PASSES, u=2, e=2),
-                in1=scale_k[:].rearrange("p (g u e) -> p g u e", u=2, e=2).unsqueeze(2).to_broadcast([P, PASSES, P, 2, 2]),
+                out=x_values(i).rearrange("p (g r u e) -> p g r u e", g=PASSES, u=2, e=2)[:, passes],
+                in0=turned[i][:].bitcast(BF16).rearrange("p (u g r e) -> p g r u e", g=PASSES, u=2, e=2)[:, passes],
+                in1=scale_k[:].rearrange("p (g u e) -> p g u e", u=2, e=2).unsqueeze(2).to_broadcast([P, PASSES, P, 2, 2])[:, passes],
                 op=ALU.mult,
             )
 
@@ -152,11 +153,11 @@ def tile_attentionnet_pa_w4_kernel(tc, x_bytes, x_scale, wq_words, wq_scales, wk
             for t in range(4):
                 for g in range(PASSES):
                     cols = slice((2 * (i % 2) + g) * P, (2 * (i % 2) + g + 1) * P)
-                    plane = (2 * g + h) * 512 + t * P
+                    plane = (PASSES * t + g) * P
                     nc.tensor.matmul_mx(
                         out=bank[:, t * P : (t + 1) * P],
                         lhsT=wts[m + str(h)][:, t * 512 + g * 256 : t * 512 + (g + 1) * 256].bitcast(FP4X4),
-                        lhsT_scale=wts_s[m][:, plane : plane + P],
+                        lhsT_scale=wts_s[m + str(h)][:, plane : plane + P],
                         rhs=xc[i // 2][:, cols].bitcast(FP8X4),
                         rhs_scale=xs[i // 2][:, cols],
                         start=(g == 0),
@@ -247,7 +248,8 @@ def tile_attentionnet_pa_w4_kernel(tc, x_bytes, x_scale, wq_words, wq_scales, wk
         cast(1)
         turn(1)
         cast(2)
-        permute_s("K")
+        for h in range(2):
+            permute_s("K", h)
         for g in range(PASSES):
             nc.vector.tensor_tensor(
                 out=xg[0][:, g * 512 : (g + 1) * 512].rearrange("p (r u e) -> p r u e", u=2, e=2),
@@ -259,22 +261,24 @@ def tile_attentionnet_pa_w4_kernel(tc, x_bytes, x_scale, wq_words, wq_scales, wk
         for g in range(PASSES):
             quantize(xc[0], xs[0], xg[0], g, 1)
         permute_w("K", 1)
-        scale_turned(1)
-        permute_s("Q")
+        scale_turned(1, slice(0, 1))
         for h in range(2):
-            permute_w("Q", h)
+            permute_s("Q", h)
+        permute_w("Q", 0)
+        scale_turned(1, slice(1, 2))
+        permute_w("Q", 1)
         quant_x(1)
 
         project_both("K", 0)
         turn(2)
-        scale_turned(2)
         widen(3)
         widen(4)
-        quant_x(2)
+        scale_turned(2)
         project_both("Q", 0)
         project_both("K", 1)
         turn(3)
         turn(4)
+        quant_x(2)
         scale_turned(3)
         widen(5)
         quant_x(3)
@@ -311,6 +315,8 @@ def tile_attentionnet_pa_w4_kernel(tc, x_bytes, x_scale, wq_words, wq_scales, wk
                 turn(7)
             else:
                 invert(j - 2)
+            if j == 2:
+                quant_x(7)
             if j == 3:
                 for h in range(2):
                     quant_k(PER_BATCH, h)
@@ -319,8 +325,6 @@ def tile_attentionnet_pa_w4_kernel(tc, x_bytes, x_scale, wq_words, wq_scales, wk
             row_min(j)
             if j == 1:
                 scale_turned(7)
-            if j == 2:
-                quant_x(7)
         project_both("K", 7)
         exps(3)
         invert(2)

@@ -23,7 +23,8 @@ PASSES = D // 512
 INV = 1.0 / math.sqrt(128.0)
 FLOPS = 2 * 2 * B * S * D * D + 2 * B * S * S * D
 SPLIT = 320
-ON_SCALAR = (1, 2, 7)
+STEPPED = (1, 2)
+ON_SCALAR = (3, 7)
 
 
 def tile_attentionnet_pa_w4_kernel(tc, x_bytes, x_scale, wq_words, wq_scales, wk_words, wk_scales, out):
@@ -33,7 +34,8 @@ def tile_attentionnet_pa_w4_kernel(tc, x_bytes, x_scale, wq_words, wq_scales, wk
 
     with ExitStack() as ctx:
         keep = ctx.enter_context(tc.tile_pool(name="keep", bufs=1))
-        banks = ctx.enter_context(tc.psum_pool(name="banks", bufs=8))
+        banks = ctx.enter_context(tc.psum_pool(name="banks", bufs=4))
+        side = ctx.enter_context(tc.psum_pool(name="side", bufs=4))
 
         def tiles(name, keys, shape, dtype):
             return {k: keep.tile(shape, dtype, name="%s_%s" % (name, k), align_bytes=256) for k in keys}
@@ -51,6 +53,7 @@ def tile_attentionnet_pa_w4_kernel(tc, x_bytes, x_scale, wq_words, wq_scales, wk
         wts = tiles("wts", halves, [P, 2048], U8)
         wts_s = tiles("wts_s", halves, [P, 1024], U8)
         xw = tiles("xw", every, [P, D], BF16)
+        xv = tiles("xv", ON_SCALAR, [P, D], BF16)
         xg = tiles("xg", range(TILES // 2), [P, 2 * D], BF16)
         xc = tiles("xc", range(TILES // 2), [P, 512], U32)
         xs = tiles("xs", range(TILES // 2), [P, 512], U8)
@@ -109,12 +112,13 @@ def tile_attentionnet_pa_w4_kernel(tc, x_bytes, x_scale, wq_words, wq_scales, wk
                 nc.tensor.matmul(idle_bank[:], zeros[:, 0:P], zeros[:], start=True, stop=True)
 
         def cast(i):
-            nc.scalar.activation(out=xw[i][:], in_=xb[i][:].bitcast(FP8), func=ACT.Copy)
+            dst = xv[i] if i in ON_SCALAR else xw[i]
+            nc.scalar.activation(out=dst[:], in_=xb[i][:].bitcast(FP8), func=ACT.Copy)
+
+        def reorder(i):
+            nc.scalar.copy(xw[i][:].bitcast(U32).rearrange("p (u w) -> p u w", u=2), xv[i][:].bitcast(U32).rearrange("p (w u) -> p u w", u=2))
 
         def widen(i):
-            if i in ON_SCALAR:
-                cast(i)
-                return
             nc.vector.tensor_scalar(
                 out=xw[i][:].rearrange("p (u w e) -> p w u e", u=2, e=2),
                 in0=xb[i][:].bitcast(FP8).rearrange("p (w u e) -> p w u e", u=2, e=2),
@@ -124,11 +128,11 @@ def tile_attentionnet_pa_w4_kernel(tc, x_bytes, x_scale, wq_words, wq_scales, wk
             )
 
         def turn(i):
-            turned[i] = banks.tile([P, 512], F32, name="bank")
+            turned[i] = side.tile([P, 512], F32, name="side")
             words = xw[i][:].bitcast(F32)
             for u in range(2):
                 for g in range(PASSES):
-                    if i in ON_SCALAR:
+                    if i in STEPPED:
                         src = words[:, 256 * g + u : 256 * (g + 1) : 2]
                     else:
                         src = words[:, u * 256 + g * P : u * 256 + (g + 1) * P]
@@ -148,36 +152,38 @@ def tile_attentionnet_pa_w4_kernel(tc, x_bytes, x_scale, wq_words, wq_scales, wk
         def quant_x(i, count=1):
             quantize(xc[i // 2], xs[i // 2], xg[i // 2], 2 * (i % 2), 2 * count)
 
-        def project(m, i, h, on_vector=False):
-            bank = banks.tile([P, 512], F32, name="bank")
+        def project(m, group, h, on_vector=()):
+            held = {i: banks.tile([P, 512], F32, name="bank") for i in group}
             for t in range(4):
                 for g in range(PASSES):
-                    cols = slice((2 * (i % 2) + g) * P, (2 * (i % 2) + g + 1) * P)
                     plane = (PASSES * t + g) * P
-                    nc.tensor.matmul_mx(
-                        out=bank[:, t * P : (t + 1) * P],
-                        lhsT=wts[m + str(h)][:, t * 512 + g * 256 : t * 512 + (g + 1) * 256].bitcast(FP4X4),
-                        lhsT_scale=wts_s[m + str(h)][:, plane : plane + P],
-                        rhs=xc[i // 2][:, cols].bitcast(FP8X4),
-                        rhs_scale=xs[i // 2][:, cols],
-                        start=(g == 0),
-                        stop=(g == PASSES - 1),
-                    )
-            b, j = divmod(i, PER_BATCH)
-            if m == "K":
-                dst = yk[2 * b + h][:, j * 512 : (j + 1) * 512]
-            else:
-                dst = yq[i // 2][:, (2 * (i % 2) + h) * 512 : (2 * (i % 2) + h + 1) * 512]
-            dst = dst.rearrange("p (n t) -> p n t", t=4)
-            src = bank[:].rearrange("p (t n) -> p n t", t=4)
-            if on_vector:
-                nc.vector.tensor_copy(out=dst, in_=src)
-            else:
-                nc.scalar.copy(dst, src)
+                    for i in group:
+                        cols = slice((2 * (i % 2) + g) * P, (2 * (i % 2) + g + 1) * P)
+                        nc.tensor.matmul_mx(
+                            out=held[i][:, t * P : (t + 1) * P],
+                            lhsT=wts[m + str(h)][:, t * 512 + g * 256 : t * 512 + (g + 1) * 256].bitcast(FP4X4),
+                            lhsT_scale=wts_s[m + str(h)][:, plane : plane + P],
+                            rhs=xc[i // 2][:, cols].bitcast(FP8X4),
+                            rhs_scale=xs[i // 2][:, cols],
+                            start=(g == 0),
+                            stop=(g == PASSES - 1),
+                        )
+            for i in group:
+                b, j = divmod(i, PER_BATCH)
+                if m == "K":
+                    dst = yk[2 * b + h][:, j * 512 : (j + 1) * 512]
+                else:
+                    dst = yq[i // 2][:, (2 * (i % 2) + h) * 512 : (2 * (i % 2) + h + 1) * 512]
+                dst = dst.rearrange("p (n t) -> p n t", t=4)
+                src = held[i][:].rearrange("p (t n) -> p n t", t=4)
+                if i in on_vector:
+                    nc.vector.tensor_copy(out=dst, in_=src)
+                else:
+                    nc.scalar.copy(dst, src)
 
-        def project_both(m, i):
+        def project_both(m, group):
             for h in range(2):
-                project(m, i, h)
+                project(m, group, h)
 
         def quant_k(i, h):
             n = 2 * (i // PER_BATCH) + h
@@ -188,7 +194,7 @@ def tile_attentionnet_pa_w4_kernel(tc, x_bytes, x_scale, wq_words, wq_scales, wk
 
         def score(i):
             b = i // PER_BATCH
-            scores[i] = banks.tile([P, S], F32, name="bank")
+            scores[i] = side.tile([P, S], F32, name="side")
             for h in range(2):
                 cols = slice((2 * (i % 2) + h) * P, (2 * (i % 2) + h + 1) * P)
                 nc.tensor.matmul_mx(
@@ -223,33 +229,41 @@ def tile_attentionnet_pa_w4_kernel(tc, x_bytes, x_scale, wq_words, wq_scales, wk
         nc.vector.memset(raw_s["Q"][:].bitcast(I32), 0)
         load_x(0)
         nc.scalar.dma_start(out=scale_k[:].rearrange("p (g t) -> p g t", t=4), in_=x_scale.rearrange("a b (g p t) -> p (a b g) t", p=P, t=4))
-        load_s("K")
         load_x(1)
+        load_s("K")
+        load_x(2)
         for h in range(2):
             load_w("K", h)
-        load_x(2)
+        load_x(3)
         load_s("Q")
         for h in range(2):
             load_w("Q", h)
-        for i in range(3, TILES):
+        for i in range(4, TILES):
             load_x(i)
 
         warm_up(3)
-        nc.vector.tensor_copy(out=xw[0][:, 0:512], in_=xb[0][:, 0:512].bitcast(FP8))
-        nc.scalar.activation(out=xw[0][:, 512:D], in_=xb[0][:, 512:D].bitcast(FP8), func=ACT.Copy)
         first = []
-        words = xw[0][:].bitcast(F32)
         for g in range(PASSES):
-            bank = banks.tile([P, 512], F32, name="bank")
+            half = slice(g * 512, (g + 1) * 512)
+            nc.vector.tensor_scalar(
+                out=xw[0][:, half].rearrange("p (u w e) -> p w u e", u=2, e=2),
+                in0=xb[0][:, half].bitcast(FP8).rearrange("p (w u e) -> p w u e", u=2, e=2),
+                scalar1=ones[:],
+                scalar2=None,
+                op0=ALU.mult,
+            )
+            bank = side.tile([P, 512], F32, name="side")
+            words = xw[0][:, half].bitcast(F32)
             for u in range(2):
-                nc.tensor.transpose(bank[:, u * P : (u + 1) * P], words[:, 256 * g + u : 256 * (g + 1) : 2], ident[:])
+                nc.tensor.transpose(bank[:, u * P : (u + 1) * P], words[:, u * P : (u + 1) * P], ident[:])
             first.append(bank)
         warm_up(2)
         cast(1)
         turn(1)
+        warm_up(1)
         cast(2)
-        for h in range(2):
-            permute_s("K", h)
+        turn(2)
+        permute_s("K", 0)
         for g in range(PASSES):
             nc.vector.tensor_tensor(
                 out=xg[0][:, g * 512 : (g + 1) * 512].rearrange("p (r u e) -> p r u e", u=2, e=2),
@@ -260,59 +274,60 @@ def tile_attentionnet_pa_w4_kernel(tc, x_bytes, x_scale, wq_words, wq_scales, wk
         permute_w("K", 0)
         for g in range(PASSES):
             quantize(xc[0], xs[0], xg[0], g, 1)
+        permute_s("K", 1)
         permute_w("K", 1)
         scale_turned(1, slice(0, 1))
         for h in range(2):
             permute_s("Q", h)
-        permute_w("Q", 0)
+            permute_w("Q", h)
         scale_turned(1, slice(1, 2))
-        permute_w("Q", 1)
-        quant_x(1)
+        cast(3)
+        reorder(3)
 
-        project_both("K", 0)
-        turn(2)
-        widen(3)
-        widen(4)
+        project_both("K", (0,))
+        quant_x(1)
         scale_turned(2)
-        project_both("Q", 0)
-        project_both("K", 1)
+        widen(4)
+        quant_x(2)
+        widen(5)
+        widen(6)
+        project_both("Q", (0,))
+        project_both("K", (1,))
+        project_both("Q", (1,))
         turn(3)
         turn(4)
-        quant_x(2)
+        turn(5)
+        cast(7)
         scale_turned(3)
-        widen(5)
-        quant_x(3)
-        widen(6)
-        project_both("Q", 1)
-        project_both("K", 2)
-        scale_turned(4)
+        project_both("K", (2,))
         for h in range(2):
             quant_k(0, h)
-        quant_x(4)
-        project_both("K", 3)
-        widen(7)
-        turn(5)
-        turn(6)
+        quant_x(3)
+        scale_turned(4)
+        reorder(7)
+        project_both("Q", (2,))
         quant_q(0, 0, 4)
+        quant_x(4)
+        project_both("K", (3,))
         scale_turned(5)
-        project_both("Q", 2)
+        turn(6)
+        turn(7)
+        project_both("Q", (3,))
         for h in range(2):
             quant_k(2, h)
         quant_x(5)
-        project_both("Q", 3)
         score(0)
         scale_turned(6)
         row_min(0)
-        quant_x(6)
         quant_q(2, 0, 4)
 
         for j in range(1, PER_BATCH):
             i = PER_BATCH + j - 1
-            project_both("K", i)
+            project_both("K", (i,))
             exps(j - 1)
             score(j)
             if j == 1:
-                turn(7)
+                scale_turned(7)
             else:
                 invert(j - 2)
             if j == 2:
@@ -322,29 +337,29 @@ def tile_attentionnet_pa_w4_kernel(tc, x_bytes, x_scale, wq_words, wq_scales, wk
                     quant_k(PER_BATCH, h)
             if j > 1:
                 finish(j - 2)
-            row_min(j)
             if j == 1:
-                scale_turned(7)
-        project_both("K", 7)
+                quant_x(6)
+            row_min(j)
+        project_both("K", (7,))
         exps(3)
         invert(2)
         quant_k(6, 0)
         finish(2)
-        project("Q", 4, 0, on_vector=True)
-        project("Q", 4, 1)
+        project("Q", (4,), 0, on_vector=(4,))
+        project("Q", (4,), 1)
         quant_k(6, 1)
         quant_q(4, 0, 1)
         invert(3)
-        project_both("Q", 5)
+        project_both("Q", (5,))
         quant_q(4, 1, 1)
         finish(3)
         score(4)
-        project("Q", 6, 0)
+        project("Q", (6,), 0)
         row_min(4)
         exps(4)
         quant_q(5, 0, 2)
-        project("Q", 6, 1, on_vector=True)
-        project_both("Q", 7)
+        project("Q", (6,), 1, on_vector=(6,))
+        project_both("Q", (7,))
         invert(4)
         quant_q(6, 0, 2)
         finish(4)
@@ -358,10 +373,9 @@ def tile_attentionnet_pa_w4_kernel(tc, x_bytes, x_scale, wq_words, wq_scales, wk
             row_min(i)
         for i in (5, 6, 7):
             exps(i)
-        invert(5)
-        invert(6)
-        finish(5)
-        finish(6)
+        for i in (5, 6):
+            invert(i)
+            finish(i)
         invert(7)
         rows = slice((TILES - 1) * P, TILES * P)
         left, right = slice(0, SPLIT), slice(SPLIT, S)

@@ -56,7 +56,7 @@ def tile_attentionnet_pa_w4_kernel(tc, x_bytes, x_scale, wq_words, wq_scales, wk
         xv = tiles("xv", ON_SCALAR, [P, D], BF16)
         xg = tiles("xg", range(TILES // 2), [P, 2 * D], BF16)
         xc = tiles("xc", range(TILES // 2), [P, 512], U32)
-        xs = tiles("xs", range(TILES // 2), [P, 512], U8)
+        xs = {k: v[:, P:] for k, v in tiles("xs", range(TILES // 2), [P, 512 + P], U8).items()}
         yk = tiles("yk", range(2 * B), [P, 4 * S], BF16)
         kc = tiles("kc", range(2 * B), [P, S], U32)
         ks = tiles("ks", range(2 * B), [P, S], U8)
@@ -154,8 +154,8 @@ def tile_attentionnet_pa_w4_kernel(tc, x_bytes, x_scale, wq_words, wq_scales, wk
 
         def project(m, group, h, on_vector=()):
             held = {i: banks.tile([P, 512], F32, name="bank") for i in group}
-            for t in range(4):
-                for g in range(PASSES):
+            for g in range(PASSES):
+                for t in range(4):
                     plane = (PASSES * t + g) * P
                     for i in group:
                         cols = slice((2 * (i % 2) + g) * P, (2 * (i % 2) + g + 1) * P)
@@ -165,8 +165,8 @@ def tile_attentionnet_pa_w4_kernel(tc, x_bytes, x_scale, wq_words, wq_scales, wk
                             lhsT_scale=wts_s[m + str(h)][:, plane : plane + P],
                             rhs=xc[i // 2][:, cols].bitcast(FP8X4),
                             rhs_scale=xs[i // 2][:, cols],
-                            start=(g == 0),
-                            stop=(g == PASSES - 1),
+                            start=(g == 0 and t == 0),
+                            stop=(g == PASSES - 1 and t == 3),
                         )
             for i in group:
                 b, j = divmod(i, PER_BATCH)

@@ -25,6 +25,7 @@ FLOPS = 2 * 2 * B * S * D * D + 2 * B * S * S * D
 SPLIT = 320
 STEPPED = (1, 2)
 ON_SCALAR = (3, 7)
+ON_GPSIMD = ()
 
 
 def tile_attentionnet_pa_w4_kernel(tc, x_bytes, x_scale, wq_words, wq_scales, wk_words, wk_scales, out):
@@ -34,8 +35,18 @@ def tile_attentionnet_pa_w4_kernel(tc, x_bytes, x_scale, wq_words, wq_scales, wk
 
     with ExitStack() as ctx:
         keep = ctx.enter_context(tc.tile_pool(name="keep", bufs=1))
-        banks = ctx.enter_context(tc.psum_pool(name="banks", bufs=4))
-        side = ctx.enter_context(tc.psum_pool(name="side", bufs=4))
+        banks = ctx.enter_context(tc.psum_pool(name="banks", bufs=1))
+
+        free = list(range(8))
+        held = {}
+
+        def take(key):
+            number = free.pop(0)
+            held[key] = (number, banks.tile([P, 512], F32, name="bank%d" % number))
+            return held[key][1]
+
+        def give_back(key):
+            free.append(held[key][0])
 
         def tiles(name, keys, shape, dtype):
             return {k: keep.tile(shape, dtype, name="%s_%s" % (name, k), align_bytes=256) for k in keys}
@@ -43,7 +54,7 @@ def tile_attentionnet_pa_w4_kernel(tc, x_bytes, x_scale, wq_words, wq_scales, wk
         every = range(TILES)
         halves = ["K0", "K1", "Q0", "Q1"]
         zeros = keep.tile([P, 512], BF16, name="zeros")
-        idle_bank = banks.tile([P, 512], F32, name="bank")
+        idle_bank = take("idle")
         ident = keep.tile([P, P], F32, name="ident")
         scale_k = keep.tile([P, PASSES * 4], F32, name="scale_k")
         ones = keep.tile([P, 1], F32, name="ones")
@@ -51,12 +62,12 @@ def tile_attentionnet_pa_w4_kernel(tc, x_bytes, x_scale, wq_words, wq_scales, wk
         raw = tiles("raw", halves, [P, 2048], U8)
         raw_s = tiles("raw_s", "KQ", [P, 2048], U8)
         wts = tiles("wts", halves, [P, 2048], U8)
-        wts_s = tiles("wts_s", halves, [P, 1024], U8)
+        wts_s = tiles("wts_s", "KQ", [P, 2048], U8)
         xw = tiles("xw", every, [P, D], BF16)
         xv = tiles("xv", ON_SCALAR, [P, D], BF16)
         xg = tiles("xg", range(TILES // 2), [P, 2 * D], BF16)
         xc = tiles("xc", range(TILES // 2), [P, 512], U32)
-        xs = {k: v[:, P:] for k, v in tiles("xs", range(TILES // 2), [P, 512 + P], U8).items()}
+        xs = tiles("xs", range(TILES // 2), [P, 512], U8)
         yk = tiles("yk", range(2 * B), [P, 4 * S], BF16)
         kc = tiles("kc", range(2 * B), [P, S], U32)
         ks = tiles("ks", range(2 * B), [P, S], U8)
@@ -74,6 +85,7 @@ def tile_attentionnet_pa_w4_kernel(tc, x_bytes, x_scale, wq_words, wq_scales, wk
         hbm_s = {"K": wk_scales, "Q": wq_scales}
         turned = {}
         scores = {}
+        sums = {}
 
         def load_x(i):
             nc.sync.dma_start(out=xb[i][:], in_=x_rows[i * P : (i + 1) * P, :])
@@ -96,11 +108,10 @@ def tile_attentionnet_pa_w4_kernel(tc, x_bytes, x_scale, wq_words, wq_scales, wk
                 in_=raw[m + str(h)][:].bitcast(I32).rearrange("p (c t w) -> p t c w", t=4, w=4),
             )
 
-        def permute_s(m, h):
-            src = raw_s[m][:].bitcast(I32).rearrange("p (g h c t w) -> p h t g c w", g=PASSES, h=2, t=4, w=2)
+        def permute_s(m):
             nc.vector.tensor_copy(
-                out=wts_s[m + str(h)][:].bitcast(I32).rearrange("p (t g c w) -> p t g c w", g=PASSES, t=4, w=2),
-                in_=src[:, h],
+                out=wts_s[m][:].bitcast(I32).rearrange("p (t c w) -> p t c w", t=4, w=2),
+                in_=raw_s[m][:].bitcast(I32).rearrange("p (c t w) -> p t c w", t=4, w=2),
             )
 
         def quantize(codes, scales, values, first, count):
@@ -111,9 +122,9 @@ def tile_attentionnet_pa_w4_kernel(tc, x_bytes, x_scale, wq_words, wq_scales, wk
             for n in range(count):
                 nc.tensor.matmul(idle_bank[:], zeros[:, 0:P], zeros[:], start=True, stop=True)
 
-        def cast(i):
+        def cast(i, cols=slice(0, D)):
             dst = xv[i] if i in ON_SCALAR else xw[i]
-            nc.scalar.activation(out=dst[:], in_=xb[i][:].bitcast(FP8), func=ACT.Copy)
+            nc.scalar.activation(out=dst[:, cols], in_=xb[i][:, cols].bitcast(FP8), func=ACT.Copy)
 
         def reorder(i):
             nc.scalar.copy(xw[i][:].bitcast(U32).rearrange("p (u w) -> p u w", u=2), xv[i][:].bitcast(U32).rearrange("p (w u) -> p u w", u=2))
@@ -128,10 +139,10 @@ def tile_attentionnet_pa_w4_kernel(tc, x_bytes, x_scale, wq_words, wq_scales, wk
             )
 
         def turn(i):
-            turned[i] = side.tile([P, 512], F32, name="side")
+            turned[i] = take(("x", i))
             words = xw[i][:].bitcast(F32)
-            for u in range(2):
-                for g in range(PASSES):
+            for g in range(PASSES):
+                for u in range(2):
                     if i in STEPPED:
                         src = words[:, 256 * g + u : 256 * (g + 1) : 2]
                     else:
@@ -148,42 +159,50 @@ def tile_attentionnet_pa_w4_kernel(tc, x_bytes, x_scale, wq_words, wq_scales, wk
                 in1=scale_k[:].rearrange("p (g u e) -> p g u e", u=2, e=2).unsqueeze(2).to_broadcast([P, PASSES, P, 2, 2])[:, passes],
                 op=ALU.mult,
             )
+            if passes.stop == PASSES:
+                give_back(("x", i))
 
         def quant_x(i, count=1):
             quantize(xc[i // 2], xs[i // 2], xg[i // 2], 2 * (i % 2), 2 * count)
 
-        def project(m, group, h, on_vector=()):
-            held = {i: banks.tile([P, 512], F32, name="bank") for i in group}
-            for g in range(PASSES):
-                for t in range(4):
-                    plane = (PASSES * t + g) * P
-                    for i in group:
-                        cols = slice((2 * (i % 2) + g) * P, (2 * (i % 2) + g + 1) * P)
-                        nc.tensor.matmul_mx(
-                            out=held[i][:, t * P : (t + 1) * P],
-                            lhsT=wts[m + str(h)][:, t * 512 + g * 256 : t * 512 + (g + 1) * 256].bitcast(FP4X4),
-                            lhsT_scale=wts_s[m + str(h)][:, plane : plane + P],
-                            rhs=xc[i // 2][:, cols].bitcast(FP8X4),
-                            rhs_scale=xs[i // 2][:, cols],
-                            start=(g == 0 and t == 0),
-                            stop=(g == PASSES - 1 and t == 3),
-                        )
-            for i in group:
-                b, j = divmod(i, PER_BATCH)
-                if m == "K":
-                    dst = yk[2 * b + h][:, j * 512 : (j + 1) * 512]
-                else:
-                    dst = yq[i // 2][:, (2 * (i % 2) + h) * 512 : (2 * (i % 2) + h + 1) * 512]
-                dst = dst.rearrange("p (n t) -> p n t", t=4)
-                src = held[i][:].rearrange("p (t n) -> p n t", t=4)
-                if i in on_vector:
-                    nc.vector.tensor_copy(out=dst, in_=src)
-                else:
-                    nc.scalar.copy(dst, src)
+        def passes(m, i, h, g):
+            if g == 0:
+                sums[m, i, h] = take((m, i, h))
+            cols = slice((2 * (i % 2) + g) * P, (2 * (i % 2) + g + 1) * P)
+            for t in range(4):
+                plane = (4 * t + 2 * g + h) * P
+                nc.tensor.matmul_mx(
+                    out=sums[m, i, h][:, t * P : (t + 1) * P],
+                    lhsT=wts[m + str(h)][:, t * 512 + g * 256 : t * 512 + (g + 1) * 256].bitcast(FP4X4),
+                    lhsT_scale=wts_s[m][:, plane : plane + P],
+                    rhs=xc[i // 2][:, cols].bitcast(FP8X4),
+                    rhs_scale=xs[i // 2][:, cols],
+                    start=(g == 0 and t == 0),
+                    stop=(g == PASSES - 1 and t == 3),
+                )
 
-        def project_both(m, group):
+        def empty(m, i, h, on_vector=False):
+            b, j = divmod(i, PER_BATCH)
+            if m == "K":
+                dst = yk[2 * b + h][:, j * 512 : (j + 1) * 512]
+            else:
+                dst = yq[i // 2][:, (2 * (i % 2) + h) * 512 : (2 * (i % 2) + h + 1) * 512]
+            dst = dst.rearrange("p (n t) -> p n t", t=4)
+            src = sums[m, i, h][:].rearrange("p (t n) -> p n t", t=4)
+            if on_vector:
+                nc.vector.tensor_copy(out=dst, in_=src)
+            else:
+                nc.scalar.copy(dst, src)
+            give_back((m, i, h))
+
+        def project(m, i, h, on_vector=False):
+            for g in range(PASSES):
+                passes(m, i, h, g)
+            empty(m, i, h, on_vector)
+
+        def project_both(m, i):
             for h in range(2):
-                project(m, group, h)
+                project(m, i, h)
 
         def quant_k(i, h):
             n = 2 * (i // PER_BATCH) + h
@@ -194,7 +213,7 @@ def tile_attentionnet_pa_w4_kernel(tc, x_bytes, x_scale, wq_words, wq_scales, wk
 
         def score(i):
             b = i // PER_BATCH
-            scores[i] = side.tile([P, S], F32, name="side")
+            scores[i] = take(("s", i))
             for h in range(2):
                 cols = slice((2 * (i % 2) + h) * P, (2 * (i % 2) + h + 1) * P)
                 nc.tensor.matmul_mx(
@@ -209,6 +228,7 @@ def tile_attentionnet_pa_w4_kernel(tc, x_bytes, x_scale, wq_words, wq_scales, wk
 
         def row_min(i):
             nc.vector.tensor_scalar(out=neg[i][:], in0=scores[i][:], scalar1=-INV, scalar2=None, op0=ALU.mult, op1=ALU.min, accum_out=low[i][:])
+            give_back(("s", i))
 
         def exps(i):
             nc.scalar.activation(out=ex[i][:], in_=neg[i][:], func=ACT.Exp, bias=low[i][:], scale=-1.0, accum_out=total[i][:])
@@ -217,7 +237,10 @@ def tile_attentionnet_pa_w4_kernel(tc, x_bytes, x_scale, wq_words, wq_scales, wk
             nc.vector.reciprocal(inv[i][:], total[i][:])
 
         def finish(i):
-            nc.vector.tensor_scalar(out=res[i][:], in0=ex[i][:], scalar1=inv[i][:], scalar2=None, op0=ALU.mult)
+            if i in ON_GPSIMD:
+                nc.gpsimd.tensor_scalar(out=res[i][:], in0=ex[i][:], scalar1=inv[i][:], scalar2=1.0, op0=ALU.mult, op1=ALU.mult)
+            else:
+                nc.vector.tensor_scalar(out=res[i][:], in0=ex[i][:], scalar1=inv[i][:], scalar2=None, op0=ALU.mult)
             nc.sync.dma_start(out=out_rows[i * P : (i + 1) * P, :], in_=res[i][:])
 
         ctx.enter_context(tc.manual_schedule())
@@ -252,7 +275,7 @@ def tile_attentionnet_pa_w4_kernel(tc, x_bytes, x_scale, wq_words, wq_scales, wk
                 scalar2=None,
                 op0=ALU.mult,
             )
-            bank = side.tile([P, 512], F32, name="side")
+            bank = take(("first", g))
             words = xw[0][:, half].bitcast(F32)
             for u in range(2):
                 nc.tensor.transpose(bank[:, u * P : (u + 1) * P], words[:, u * P : (u + 1) * P], ident[:])
@@ -261,9 +284,11 @@ def tile_attentionnet_pa_w4_kernel(tc, x_bytes, x_scale, wq_words, wq_scales, wk
         cast(1)
         turn(1)
         warm_up(1)
-        cast(2)
+        for g in range(PASSES):
+            cast(2, slice(g * 512, (g + 1) * 512))
+        give_back("idle")
         turn(2)
-        permute_s("K", 0)
+        permute_s("K")
         for g in range(PASSES):
             nc.vector.tensor_tensor(
                 out=xg[0][:, g * 512 : (g + 1) * 512].rearrange("p (r u e) -> p r u e", u=2, e=2),
@@ -271,48 +296,55 @@ def tile_attentionnet_pa_w4_kernel(tc, x_bytes, x_scale, wq_words, wq_scales, wk
                 in1=scale_k[:, g * 4 : (g + 1) * 4].rearrange("p (u e) -> p u e", e=2).unsqueeze(1).to_broadcast([P, P, 2, 2]),
                 op=ALU.mult,
             )
+            give_back(("first", g))
         permute_w("K", 0)
         for g in range(PASSES):
             quantize(xc[0], xs[0], xg[0], g, 1)
-        permute_s("K", 1)
         permute_w("K", 1)
         scale_turned(1, slice(0, 1))
-        for h in range(2):
-            permute_s("Q", h)
-            permute_w("Q", h)
+        permute_s("Q")
+        quantize(xc[0], xs[0], xg[0], 2, 1)
+        permute_w("Q", 0)
         scale_turned(1, slice(1, 2))
+        permute_w("Q", 1)
+        quantize(xc[0], xs[0], xg[0], 3, 1)
         cast(3)
-        reorder(3)
 
-        project_both("K", (0,))
-        quant_x(1)
+
+        project_both("K", 0)
+        reorder(3)
+        for h in range(2):
+            passes("K", 1, h, 0)
+        project("Q", 0, 0)
+        for h in range(2):
+            passes("K", 1, h, 1)
+            empty("K", 1, h)
+        project("Q", 0, 1)
         scale_turned(2)
         widen(4)
         quant_x(2)
         widen(5)
         widen(6)
-        project_both("Q", (0,))
-        project_both("K", (1,))
-        project_both("Q", (1,))
+        project_both("Q", 1)
         turn(3)
         turn(4)
         turn(5)
         cast(7)
         scale_turned(3)
-        project_both("K", (2,))
+        project_both("K", 2)
         for h in range(2):
             quant_k(0, h)
         quant_x(3)
         scale_turned(4)
         reorder(7)
-        project_both("Q", (2,))
+        project_both("Q", 2)
         quant_q(0, 0, 4)
         quant_x(4)
-        project_both("K", (3,))
+        project_both("K", 3)
         scale_turned(5)
         turn(6)
         turn(7)
-        project_both("Q", (3,))
+        project_both("Q", 3)
         for h in range(2):
             quant_k(2, h)
         quant_x(5)
@@ -323,7 +355,7 @@ def tile_attentionnet_pa_w4_kernel(tc, x_bytes, x_scale, wq_words, wq_scales, wk
 
         for j in range(1, PER_BATCH):
             i = PER_BATCH + j - 1
-            project_both("K", (i,))
+            project_both("K", i)
             exps(j - 1)
             score(j)
             if j == 1:
@@ -340,26 +372,26 @@ def tile_attentionnet_pa_w4_kernel(tc, x_bytes, x_scale, wq_words, wq_scales, wk
             if j == 1:
                 quant_x(6)
             row_min(j)
-        project_both("K", (7,))
+        project_both("K", 7)
         exps(3)
         invert(2)
         quant_k(6, 0)
         finish(2)
-        project("Q", (4,), 0, on_vector=(4,))
-        project("Q", (4,), 1)
+        project("Q", 4, 0, on_vector=True)
+        project("Q", 4, 1)
         quant_k(6, 1)
         quant_q(4, 0, 1)
         invert(3)
-        project_both("Q", (5,))
+        project_both("Q", 5)
         quant_q(4, 1, 1)
         finish(3)
         score(4)
-        project("Q", (6,), 0)
+        project("Q", 6, 0)
         row_min(4)
         exps(4)
         quant_q(5, 0, 2)
-        project("Q", (6,), 1, on_vector=(6,))
-        project_both("Q", (7,))
+        project("Q", 6, 1, on_vector=True)
+        project_both("Q", 7)
         invert(4)
         quant_q(6, 0, 2)
         finish(4)

@@ -288,7 +288,6 @@ def tile_attentionnet_pa_w4_kernel(tc, x_bytes, x_scale, wq_words, wq_scales, wk
             cast(2, slice(g * 512, (g + 1) * 512))
         give_back("idle")
         turn(2)
-        permute_s("K")
         for g in range(PASSES):
             nc.vector.tensor_tensor(
                 out=xg[0][:, g * 512 : (g + 1) * 512].rearrange("p (r u e) -> p r u e", u=2, e=2),
@@ -297,29 +296,29 @@ def tile_attentionnet_pa_w4_kernel(tc, x_bytes, x_scale, wq_words, wq_scales, wk
                 op=ALU.mult,
             )
             give_back(("first", g))
+        permute_s("K")
         permute_w("K", 0)
         for g in range(PASSES):
             quantize(xc[0], xs[0], xg[0], g, 1)
-        permute_w("K", 1)
         scale_turned(1, slice(0, 1))
-        permute_s("Q")
-        quantize(xc[0], xs[0], xg[0], 2, 1)
-        permute_w("Q", 0)
+        permute_w("K", 1)
         scale_turned(1, slice(1, 2))
-        permute_w("Q", 1)
-        quantize(xc[0], xs[0], xg[0], 3, 1)
+        for g in range(PASSES):
+            quantize(xc[0], xs[0], xg[0], PASSES + g, 1)
+        permute_s("Q")
+        for h in range(2):
+            permute_w("Q", h)
         cast(3)
 
 
         project_both("K", 0)
         reorder(3)
+        for g in range(PASSES):
+            for h in range(2):
+                passes("K", 1, h, g)
         for h in range(2):
-            passes("K", 1, h, 0)
-        project("Q", 0, 0)
-        for h in range(2):
-            passes("K", 1, h, 1)
             empty("K", 1, h)
-        project("Q", 0, 1)
+        project_both("Q", 0)
         scale_turned(2)
         widen(4)
         quant_x(2)

@@ -108,8 +108,8 @@ def tile_attentionnet_pa_w4_kernel(tc, x_bytes, x_scale, wq_words, wq_scales, wk
                 in_=raw[m + str(h)][:].bitcast(I32).rearrange("p (c t w) -> p t c w", t=4, w=4),
             )
 
-        def permute_s(m):
-            nc.vector.tensor_copy(
+        def permute_s(m, engine):
+            engine.tensor_copy(
                 out=wts_s[m][:].bitcast(I32).rearrange("p (t c w) -> p t c w", t=4, w=2),
                 in_=raw_s[m][:].bitcast(I32).rearrange("p (c t w) -> p t c w", t=4, w=2),
             )
@@ -152,14 +152,14 @@ def tile_attentionnet_pa_w4_kernel(tc, x_bytes, x_scale, wq_words, wq_scales, wk
         def x_values(i):
             return xg[i // 2][:, (i % 2) * D : (i % 2 + 1) * D]
 
-        def scale_turned(i, passes=slice(0, PASSES)):
+        def scale_turned(i, passes=slice(0, PASSES), rows=slice(0, P)):
             nc.vector.tensor_tensor(
-                out=x_values(i).rearrange("p (g r u e) -> p g r u e", g=PASSES, u=2, e=2)[:, passes],
-                in0=turned[i][:].bitcast(BF16).rearrange("p (u g r e) -> p g r u e", g=PASSES, u=2, e=2)[:, passes],
-                in1=scale_k[:].rearrange("p (g u e) -> p g u e", u=2, e=2).unsqueeze(2).to_broadcast([P, PASSES, P, 2, 2])[:, passes],
+                out=x_values(i).rearrange("p (g r u e) -> p g r u e", g=PASSES, u=2, e=2)[:, passes, rows],
+                in0=turned[i][:].bitcast(BF16).rearrange("p (u g r e) -> p g r u e", g=PASSES, u=2, e=2)[:, passes, rows],
+                in1=scale_k[:].rearrange("p (g u e) -> p g u e", u=2, e=2).unsqueeze(2).to_broadcast([P, PASSES, P, 2, 2])[:, passes, rows],
                 op=ALU.mult,
             )
-            if passes.stop == PASSES:
+            if passes.stop == PASSES and rows.stop == P:
                 give_back(("x", i))
 
         def quant_x(i, count=1):
@@ -296,16 +296,17 @@ def tile_attentionnet_pa_w4_kernel(tc, x_bytes, x_scale, wq_words, wq_scales, wk
                 op=ALU.mult,
             )
             give_back(("first", g))
-        permute_s("K")
+        permute_s("K", nc.gpsimd)
         permute_w("K", 0)
         for g in range(PASSES):
             quantize(xc[0], xs[0], xg[0], g, 1)
-        scale_turned(1, slice(0, 1))
         permute_w("K", 1)
-        scale_turned(1, slice(1, 2))
-        for g in range(PASSES):
-            quantize(xc[0], xs[0], xg[0], PASSES + g, 1)
-        permute_s("Q")
+        scale_turned(1, slice(0, 1))
+        scale_turned(1, slice(1, 2), slice(0, P // 2))
+        quantize(xc[0], xs[0], xg[0], 2, 1)
+        scale_turned(1, slice(1, 2), slice(P // 2, P))
+        permute_s("Q", nc.vector)
+        quantize(xc[0], xs[0], xg[0], 3, 1)
         for h in range(2):
             permute_w("Q", h)
         cast(3)

@@ -25,7 +25,7 @@ FLOPS = 2 * 2 * B * S * D * D + 2 * B * S * S * D
 SPLIT = 320
 STEPPED = (1, 2)
 ON_SCALAR = (3, 7)
-ON_GPSIMD = ()
+ON_GPSIMD = (0, 1)
 
 
 def tile_attentionnet_pa_w4_kernel(tc, x_bytes, x_scale, wq_words, wq_scales, wk_words, wk_scales, out):
@@ -351,32 +351,33 @@ def tile_attentionnet_pa_w4_kernel(tc, x_bytes, x_scale, wq_words, wq_scales, wk
         score(0)
         scale_turned(6)
         row_min(0)
+        quant_x(6)
         quant_q(2, 0, 4)
 
-        for j in range(1, PER_BATCH):
-            i = PER_BATCH + j - 1
-            project_both("K", i)
-            exps(j - 1)
-            score(j)
-            if j == 1:
-                scale_turned(7)
-            else:
-                invert(j - 2)
-            if j == 2:
-                quant_x(7)
-            if j == 3:
-                for h in range(2):
-                    quant_k(PER_BATCH, h)
-            if j > 1:
-                finish(j - 2)
-            if j == 1:
-                quant_x(6)
-            row_min(j)
+        project_both("K", 4)
+        exps(0)
+        score(1)
+        row_min(1)
+        invert(0)
+        scale_turned(7)
+        finish(0)
+        project_both("K", 5)
+        exps(1)
+        score(2)
+        quant_x(7)
+        row_min(2)
+        project_both("K", 6)
+        exps(2)
+        score(3)
+        quant_k(4, 0)
+        invert(1)
+        quant_k(4, 1)
+        finish(1)
+        row_min(3)
         project_both("K", 7)
         exps(3)
         invert(2)
         quant_k(6, 0)
-        finish(2)
         project("Q", 4, 0, on_vector=True)
         project("Q", 4, 1)
         quant_k(6, 1)
@@ -384,7 +385,8 @@ def tile_attentionnet_pa_w4_kernel(tc, x_bytes, x_scale, wq_words, wq_scales, wk
         invert(3)
         project_both("Q", 5)
         quant_q(4, 1, 1)
-        finish(3)
+        for i in (2, 3):
+            finish(i)
         score(4)
         project("Q", 6, 0)
         row_min(4)

@@ -124,7 +124,7 @@ def tile_attentionnet_pa_w4_kernel(tc, x_bytes, x_scale, wq_words, wq_scales, wk
 
         def cast(i, cols=slice(0, D)):
             dst = xv[i] if i in ON_SCALAR else xw[i]
-            nc.scalar.activation(out=dst[:, cols], in_=xb[i][:, cols].bitcast(FP8), func=ACT.Copy)
+            nc.scalar.copy(dst[:, cols], xb[i][:, cols].bitcast(FP8))
 
         def reorder(i):
             nc.scalar.copy(xw[i][:].bitcast(U32).rearrange("p (u w) -> p u w", u=2), xv[i][:].bitcast(U32).rearrange("p (w u) -> p u w", u=2))
@@ -281,7 +281,8 @@ def tile_attentionnet_pa_w4_kernel(tc, x_bytes, x_scale, wq_words, wq_scales, wk
                 nc.tensor.transpose(bank[:, u * P : (u + 1) * P], words[:, u * P : (u + 1) * P], ident[:])
             first.append(bank)
         warm_up(2)
-        cast(1)
+        nc.scalar.activation(out=xw[1][:, 0:P], in_=xb[1][:, 0:P].bitcast(FP8), func=ACT.Copy)
+        cast(1, slice(P, D))
         turn(1)
         warm_up(1)
         for g in range(PASSES):
@@ -352,7 +353,7 @@ def tile_attentionnet_pa_w4_kernel(tc, x_bytes, x_scale, wq_words, wq_scales, wk
         scale_turned(6)
         row_min(0)
         quant_x(6)
-        quant_q(2, 0, 4)
+        quant_q(2, 0, 2)
 
         project_both("K", 4)
         exps(0)
@@ -364,6 +365,7 @@ def tile_attentionnet_pa_w4_kernel(tc, x_bytes, x_scale, wq_words, wq_scales, wk
         project_both("K", 5)
         exps(1)
         score(2)
+        quant_q(3, 0, 2)
         quant_x(7)
         row_min(2)
         project_both("K", 6)
@@ -393,23 +395,26 @@ def tile_attentionnet_pa_w4_kernel(tc, x_bytes, x_scale, wq_words, wq_scales, wk
         exps(4)
         quant_q(5, 0, 2)
         project("Q", 6, 1, on_vector=True)
-        project_both("Q", 7)
+        project("Q", 7, 0)
+        score(5)
+        project("Q", 7, 1)
         invert(4)
         quant_q(6, 0, 2)
-        finish(4)
-        quant_q(7, 0, 1)
-
-        score(5)
         row_min(5)
+        exps(5)
+        quant_q(7, 0, 1)
+        finish(4)
         quant_q(7, 1, 1)
         for i in (6, 7):
             score(i)
-            row_min(i)
-        for i in (5, 6, 7):
+        row_min(6)
+        invert(5)
+        row_min(7)
+        finish(5)
+        for i in (6, 7):
             exps(i)
-        for i in (5, 6):
-            invert(i)
-            finish(i)
+        invert(6)
+        finish(6)
         invert(7)
         rows = slice((TILES - 1) * P, TILES * P)
         left, right = slice(0, SPLIT), slice(SPLIT, S)

@@ -64,7 +64,7 @@ def tile_attentionnet_pa_w4_kernel(tc, x_bytes, x_scale, wq_words, wq_scales, wk
         wts = tiles("wts", halves, [P, 2048], U8)
         wts_s = tiles("wts_s", "KQ", [P, 2048], U8)
         xw = tiles("xw", every, [P, D], BF16)
-        xv = tiles("xv", ON_SCALAR, [P, D], BF16)
+        xv = tiles("xv", (3,), [P, D], BF16)
         xg = tiles("xg", range(TILES // 2), [P, 2 * D], BF16)
         xc = tiles("xc", range(TILES // 2), [P, 512], U32)
         xs = tiles("xs", range(TILES // 2), [P, 512], U8)
@@ -126,6 +126,10 @@ def tile_attentionnet_pa_w4_kernel(tc, x_bytes, x_scale, wq_words, wq_scales, wk
             dst = xv[i] if i in ON_SCALAR else xw[i]
             nc.scalar.copy(dst[:, cols], xb[i][:, cols].bitcast(FP8))
 
+        def cast_behind(i, done):
+            xv[i] = keep.tile([P, D], BF16, name=done, align_bytes=256)
+            nc.gpsimd.tensor_copy(out=xv[i][:], in_=xb[i][:].bitcast(FP8))
+
         def reorder(i):
             nc.scalar.copy(xw[i][:].bitcast(U32).rearrange("p (u w) -> p u w", u=2), xv[i][:].bitcast(U32).rearrange("p (w u) -> p u w", u=2))
 
@@ -161,6 +165,37 @@ def tile_attentionnet_pa_w4_kernel(tc, x_bytes, x_scale, wq_words, wq_scales, wk
             )
             if passes.stop == PASSES and rows.stop == P:
                 give_back(("x", i))
+
+        def turn_passes(i):
+            words = xw[i][:].bitcast(F32)
+            held_banks = []
+            for g in range(PASSES):
+                bank = take(("pass", i, g))
+                for u in range(2):
+                    nc.tensor.transpose(bank[:, u * P : (u + 1) * P], words[:, 256 * g + u : 256 * (g + 1) : 2], ident[:])
+                held_banks.append(bank)
+            return held_banks
+
+        def scale_pass(i, g, bank):
+            nc.vector.tensor_tensor(
+                out=x_values(i)[:, g * 512 : (g + 1) * 512].rearrange("p (r u e) -> p r u e", u=2, e=2),
+                in0=bank[:, 0:256].bitcast(BF16).rearrange("p (u r e) -> p r u e", u=2, e=2),
+                in1=scale_k[:, g * 4 : (g + 1) * 4].rearrange("p (u e) -> p u e", e=2).unsqueeze(1).to_broadcast([P, P, 2, 2]),
+                op=ALU.mult,
+            )
+            give_back(("pass", i, g))
+
+        def scale_slots(i, g, bank):
+            pairs = bank[:, 0:256].bitcast(BF16)
+            for t in range(4):
+                u, e = divmod(t, 2)
+                nc.scalar.activation(
+                    out=x_values(i)[:, g * 512 + t : (g + 1) * 512 : 4],
+                    in_=pairs[:, u * 256 + e : (u + 1) * 256 : 2],
+                    func=ACT.Copy,
+                    scale=scale_k[:, g * 4 + t : g * 4 + t + 1],
+                )
+            give_back(("pass", i, g))
 
         def quant_x(i, count=1):
             quantize(xc[i // 2], xs[i // 2], xg[i // 2], 2 * (i % 2), 2 * count)
@@ -280,15 +315,14 @@ def tile_attentionnet_pa_w4_kernel(tc, x_bytes, x_scale, wq_words, wq_scales, wk
             for u in range(2):
                 nc.tensor.transpose(bank[:, u * P : (u + 1) * P], words[:, u * P : (u + 1) * P], ident[:])
             first.append(bank)
-        warm_up(2)
         nc.scalar.activation(out=xw[1][:, 0:P], in_=xb[1][:, 0:P].bitcast(FP8), func=ACT.Copy)
         cast(1, slice(P, D))
-        turn(1)
-        warm_up(1)
+        second = turn_passes(1)
+        warm_up(2)
         for g in range(PASSES):
             cast(2, slice(g * 512, (g + 1) * 512))
-        give_back("idle")
         turn(2)
+        give_back("idle")
         for g in range(PASSES):
             nc.vector.tensor_tensor(
                 out=xg[0][:, g * 512 : (g + 1) * 512].rearrange("p (r u e) -> p r u e", u=2, e=2),
@@ -302,10 +336,9 @@ def tile_attentionnet_pa_w4_kernel(tc, x_bytes, x_scale, wq_words, wq_scales, wk
         for g in range(PASSES):
             quantize(xc[0], xs[0], xg[0], g, 1)
         permute_w("K", 1)
-        scale_turned(1, slice(0, 1))
-        scale_turned(1, slice(1, 2), slice(0, P // 2))
+        scale_pass(1, 0, second[0])
+        scale_slots(1, 1, second[1])
         quantize(xc[0], xs[0], xg[0], 2, 1)
-        scale_turned(1, slice(1, 2), slice(P // 2, P))
         permute_s("Q", nc.vector)
         quantize(xc[0], xs[0], xg[0], 3, 1)
         for h in range(2):
@@ -328,15 +361,16 @@ def tile_attentionnet_pa_w4_kernel(tc, x_bytes, x_scale, wq_words, wq_scales, wk
         widen(6)
         project_both("Q", 1)
         turn(3)
+        cast_behind(7, "xw_3")
         turn(4)
         turn(5)
-        cast(7)
         scale_turned(3)
         project_both("K", 2)
+        scale_turned(4, slice(0, 1))
+        quant_x(3)
         for h in range(2):
             quant_k(0, h)
-        quant_x(3)
-        scale_turned(4)
+        scale_turned(4, slice(1, 2))
         reorder(7)
         project_both("Q", 2)
         quant_q(0, 0, 4)
@@ -349,13 +383,14 @@ def tile_attentionnet_pa_w4_kernel(tc, x_bytes, x_scale, wq_words, wq_scales, wk
         for h in range(2):
             quant_k(2, h)
         quant_x(5)
+        project("K", 4, 0)
         score(0)
         scale_turned(6)
         row_min(0)
         quant_x(6)
         quant_q(2, 0, 2)
 
-        project_both("K", 4)
+        project("K", 4, 1)
         exps(0)
         score(1)
         row_min(1)

@@ -22,10 +22,11 @@ PER_BATCH = S // P
 PASSES = D // 512
 INV = 1.0 / math.sqrt(128.0)
 FLOPS = 2 * 2 * B * S * D * D + 2 * B * S * S * D
+BANKS = 8
 SPLIT = 320
 STEPPED = (1, 2)
-ON_SCALAR = (3, 7)
-ON_GPSIMD = (0, 1)
+REORDERED_ON_SCALAR, REORDERED_ON_GPSIMD = 3, 7
+NORMALISED_ON_GPSIMD = (0, 1)
 
 
 def tile_attentionnet_pa_w4_kernel(tc, x_bytes, x_scale, wq_words, wq_scales, wk_words, wk_scales, out):
@@ -37,7 +38,7 @@ def tile_attentionnet_pa_w4_kernel(tc, x_bytes, x_scale, wq_words, wq_scales, wk
         keep = ctx.enter_context(tc.tile_pool(name="keep", bufs=1))
         banks = ctx.enter_context(tc.psum_pool(name="banks", bufs=1))
 
-        free = list(range(8))
+        free = list(range(BANKS))
         held = {}
 
         def take(key):
@@ -64,7 +65,7 @@ def tile_attentionnet_pa_w4_kernel(tc, x_bytes, x_scale, wq_words, wq_scales, wk
         wts = tiles("wts", halves, [P, 2048], U8)
         wts_s = tiles("wts_s", "KQ", [P, 2048], U8)
         xw = tiles("xw", every, [P, D], BF16)
-        xv = tiles("xv", (3,), [P, D], BF16)
+        xv = tiles("xv", (REORDERED_ON_SCALAR,), [P, D], BF16)
         xg = tiles("xg", range(TILES // 2), [P, 2 * D], BF16)
         xc = tiles("xc", range(TILES // 2), [P, 512], U32)
         xs = tiles("xs", range(TILES // 2), [P, 512], U8)
@@ -84,6 +85,7 @@ def tile_attentionnet_pa_w4_kernel(tc, x_bytes, x_scale, wq_words, wq_scales, wk
         hbm_w = {"K": wk_words, "Q": wq_words}
         hbm_s = {"K": wk_scales, "Q": wq_scales}
         turned = {}
+        turned_pass = {}
         scores = {}
         sums = {}
 
@@ -122,21 +124,20 @@ def tile_attentionnet_pa_w4_kernel(tc, x_bytes, x_scale, wq_words, wq_scales, wk
             for n in range(count):
                 nc.tensor.matmul(idle_bank[:], zeros[:, 0:P], zeros[:], start=True, stop=True)
 
-        def cast(i, cols=slice(0, D)):
-            dst = xv[i] if i in ON_SCALAR else xw[i]
+        def cast(dst, i, cols):
             nc.scalar.copy(dst[:, cols], xb[i][:, cols].bitcast(FP8))
 
         def cast_behind(i, done):
-            xv[i] = keep.tile([P, D], BF16, name=done, align_bytes=256)
+            xv[i] = keep.tile([P, D], BF16, name="xw_%s" % done, align_bytes=256)
             nc.gpsimd.tensor_copy(out=xv[i][:], in_=xb[i][:].bitcast(FP8))
 
         def reorder(i):
             nc.scalar.copy(xw[i][:].bitcast(U32).rearrange("p (u w) -> p u w", u=2), xv[i][:].bitcast(U32).rearrange("p (w u) -> p u w", u=2))
 
-        def widen(i):
+        def widen(i, cols=slice(0, D)):
             nc.vector.tensor_scalar(
-                out=xw[i][:].rearrange("p (u w e) -> p w u e", u=2, e=2),
-                in0=xb[i][:].bitcast(FP8).rearrange("p (w u e) -> p w u e", u=2, e=2),
+                out=xw[i][:, cols].rearrange("p (u w e) -> p w u e", u=2, e=2),
+                in0=xb[i][:, cols].bitcast(FP8).rearrange("p (w u e) -> p w u e", u=2, e=2),
                 scalar1=ones[:],
                 scalar2=None,
                 op0=ALU.mult,
@@ -144,63 +145,63 @@ def tile_attentionnet_pa_w4_kernel(tc, x_bytes, x_scale, wq_words, wq_scales, wk
 
         def turn(i):
             turned[i] = take(("x", i))
-            words = xw[i][:].bitcast(F32)
+            pairs = xw[i][:].bitcast(F32)
             for g in range(PASSES):
                 for u in range(2):
                     if i in STEPPED:
-                        src = words[:, 256 * g + u : 256 * (g + 1) : 2]
+                        src = pairs[:, 256 * g + u : 256 * (g + 1) : 2]
                     else:
-                        src = words[:, u * 256 + g * P : u * 256 + (g + 1) * P]
+                        src = pairs[:, u * 256 + g * P : u * 256 + (g + 1) * P]
                     nc.tensor.transpose(turned[i][:, u * 256 + g * P : u * 256 + (g + 1) * P], src, ident[:])
 
         def x_values(i):
             return xg[i // 2][:, (i % 2) * D : (i % 2 + 1) * D]
 
-        def scale_turned(i, passes=slice(0, PASSES), rows=slice(0, P)):
+        def scale_turned(i, part=slice(0, PASSES)):
             nc.vector.tensor_tensor(
-                out=x_values(i).rearrange("p (g r u e) -> p g r u e", g=PASSES, u=2, e=2)[:, passes, rows],
-                in0=turned[i][:].bitcast(BF16).rearrange("p (u g r e) -> p g r u e", g=PASSES, u=2, e=2)[:, passes, rows],
-                in1=scale_k[:].rearrange("p (g u e) -> p g u e", u=2, e=2).unsqueeze(2).to_broadcast([P, PASSES, P, 2, 2])[:, passes, rows],
+                out=x_values(i).rearrange("p (g r u e) -> p g r u e", g=PASSES, u=2, e=2)[:, part],
+                in0=turned[i][:].bitcast(BF16).rearrange("p (u g r e) -> p g r u e", g=PASSES, u=2, e=2)[:, part],
+                in1=scale_k[:].rearrange("p (g u e) -> p g u e", u=2, e=2).unsqueeze(2).to_broadcast([P, PASSES, P, 2, 2])[:, part],
                 op=ALU.mult,
             )
-            if passes.stop == PASSES and rows.stop == P:
+            if part.stop == PASSES:
                 give_back(("x", i))
 
-        def turn_passes(i):
-            words = xw[i][:].bitcast(F32)
-            held_banks = []
-            for g in range(PASSES):
-                bank = take(("pass", i, g))
-                for u in range(2):
-                    nc.tensor.transpose(bank[:, u * P : (u + 1) * P], words[:, 256 * g + u : 256 * (g + 1) : 2], ident[:])
-                held_banks.append(bank)
-            return held_banks
+        def turn_pass(i, g):
+            turned_pass[i, g] = take(("pass", i, g))
+            pairs = xw[i][:, g * 512 : (g + 1) * 512].bitcast(F32)
+            for u in range(2):
+                src = pairs[:, u:256:2] if i in STEPPED else pairs[:, u * P : (u + 1) * P]
+                nc.tensor.transpose(turned_pass[i, g][:, u * P : (u + 1) * P], src, ident[:])
 
-        def scale_pass(i, g, bank):
+        def scale_pass(i, g):
             nc.vector.tensor_tensor(
                 out=x_values(i)[:, g * 512 : (g + 1) * 512].rearrange("p (r u e) -> p r u e", u=2, e=2),
-                in0=bank[:, 0:256].bitcast(BF16).rearrange("p (u r e) -> p r u e", u=2, e=2),
+                in0=turned_pass[i, g][:, 0:256].bitcast(BF16).rearrange("p (u r e) -> p r u e", u=2, e=2),
                 in1=scale_k[:, g * 4 : (g + 1) * 4].rearrange("p (u e) -> p u e", e=2).unsqueeze(1).to_broadcast([P, P, 2, 2]),
                 op=ALU.mult,
             )
             give_back(("pass", i, g))
 
-        def scale_slots(i, g, bank):
-            pairs = bank[:, 0:256].bitcast(BF16)
+        def scale_slots(i, g):
+            values = turned_pass[i, g][:, 0:256].bitcast(BF16)
             for t in range(4):
                 u, e = divmod(t, 2)
                 nc.scalar.activation(
                     out=x_values(i)[:, g * 512 + t : (g + 1) * 512 : 4],
-                    in_=pairs[:, u * 256 + e : (u + 1) * 256 : 2],
+                    in_=values[:, u * 256 + e : (u + 1) * 256 : 2],
                     func=ACT.Copy,
                     scale=scale_k[:, g * 4 + t : g * 4 + t + 1],
                 )
             give_back(("pass", i, g))
 
-        def quant_x(i, count=1):
-            quantize(xc[i // 2], xs[i // 2], xg[i // 2], 2 * (i % 2), 2 * count)
+        def quant_pass(i, g):
+            quantize(xc[i // 2], xs[i // 2], xg[i // 2], 2 * (i % 2) + g, 1)
 
-        def passes(m, i, h, g):
+        def quant_x(i):
+            quantize(xc[i // 2], xs[i // 2], xg[i // 2], 2 * (i % 2), PASSES)
+
+        def project_pass(m, i, h, g):
             if g == 0:
                 sums[m, i, h] = take((m, i, h))
             cols = slice((2 * (i % 2) + g) * P, (2 * (i % 2) + g + 1) * P)
@@ -232,7 +233,7 @@ def tile_attentionnet_pa_w4_kernel(tc, x_bytes, x_scale, wq_words, wq_scales, wk
 
         def project(m, i, h, on_vector=False):
             for g in range(PASSES):
-                passes(m, i, h, g)
+                project_pass(m, i, h, g)
             empty(m, i, h, on_vector)
 
         def project_both(m, i):
@@ -272,7 +273,7 @@ def tile_attentionnet_pa_w4_kernel(tc, x_bytes, x_scale, wq_words, wq_scales, wk
             nc.vector.reciprocal(inv[i][:], total[i][:])
 
         def finish(i):
-            if i in ON_GPSIMD:
+            if i in NORMALISED_ON_GPSIMD:
                 nc.gpsimd.tensor_scalar(out=res[i][:], in0=ex[i][:], scalar1=inv[i][:], scalar2=1.0, op0=ALU.mult, op1=ALU.mult)
             else:
                 nc.vector.tensor_scalar(out=res[i][:], in0=ex[i][:], scalar1=inv[i][:], scalar2=None, op0=ALU.mult)
@@ -285,6 +286,7 @@ def tile_attentionnet_pa_w4_kernel(tc, x_bytes, x_scale, wq_words, wq_scales, wk
         nc.vector.memset(raw_s["K"][:].bitcast(I32), 0)
         nc.vector.memset(zeros[:], 0.0)
         nc.vector.memset(raw_s["Q"][:].bitcast(I32), 0)
+
         load_x(0)
         nc.scalar.dma_start(out=scale_k[:].rearrange("p (g t) -> p g t", t=4), in_=x_scale.rearrange("a b (g p t) -> p (a b g) t", p=P, t=4))
         load_x(1)
@@ -300,68 +302,52 @@ def tile_attentionnet_pa_w4_kernel(tc, x_bytes, x_scale, wq_words, wq_scales, wk
             load_x(i)
 
         warm_up(3)
-        first = []
         for g in range(PASSES):
-            half = slice(g * 512, (g + 1) * 512)
-            nc.vector.tensor_scalar(
-                out=xw[0][:, half].rearrange("p (u w e) -> p w u e", u=2, e=2),
-                in0=xb[0][:, half].bitcast(FP8).rearrange("p (w u e) -> p w u e", u=2, e=2),
-                scalar1=ones[:],
-                scalar2=None,
-                op0=ALU.mult,
-            )
-            bank = take(("first", g))
-            words = xw[0][:, half].bitcast(F32)
-            for u in range(2):
-                nc.tensor.transpose(bank[:, u * P : (u + 1) * P], words[:, u * P : (u + 1) * P], ident[:])
-            first.append(bank)
-        nc.scalar.activation(out=xw[1][:, 0:P], in_=xb[1][:, 0:P].bitcast(FP8), func=ACT.Copy)
-        cast(1, slice(P, D))
-        second = turn_passes(1)
+            widen(0, slice(g * 512, (g + 1) * 512))
+            turn_pass(0, g)
         warm_up(2)
+        nc.scalar.activation(out=xw[1][:, 0:P], in_=xb[1][:, 0:P].bitcast(FP8), func=ACT.Copy)
+        cast(xw[1], 1, slice(P, D))
         for g in range(PASSES):
-            cast(2, slice(g * 512, (g + 1) * 512))
+            turn_pass(1, g)
+        warm_up(1)
+        for g in range(PASSES):
+            cast(xw[2], 2, slice(g * 512, (g + 1) * 512))
         turn(2)
         give_back("idle")
         for g in range(PASSES):
-            nc.vector.tensor_tensor(
-                out=xg[0][:, g * 512 : (g + 1) * 512].rearrange("p (r u e) -> p r u e", u=2, e=2),
-                in0=first[g][:, 0:256].bitcast(BF16).rearrange("p (u r e) -> p r u e", u=2, e=2),
-                in1=scale_k[:, g * 4 : (g + 1) * 4].rearrange("p (u e) -> p u e", e=2).unsqueeze(1).to_broadcast([P, P, 2, 2]),
-                op=ALU.mult,
-            )
-            give_back(("first", g))
+            scale_pass(0, g)
         permute_s("K", nc.gpsimd)
         permute_w("K", 0)
         for g in range(PASSES):
-            quantize(xc[0], xs[0], xg[0], g, 1)
+            quant_pass(0, g)
         permute_w("K", 1)
-        scale_pass(1, 0, second[0])
-        scale_slots(1, 1, second[1])
-        quantize(xc[0], xs[0], xg[0], 2, 1)
+        scale_pass(1, 0)
+        scale_slots(1, 1)
+        quant_pass(1, 0)
         permute_s("Q", nc.vector)
-        quantize(xc[0], xs[0], xg[0], 3, 1)
-        for h in range(2):
-            permute_w("Q", h)
-        cast(3)
-
+        permute_w("Q", 0)
+        quant_pass(1, 1)
+        permute_w("Q", 1)
+        cast(xv[REORDERED_ON_SCALAR], REORDERED_ON_SCALAR, slice(0, D))
 
         project_both("K", 0)
-        reorder(3)
-        for g in range(PASSES):
-            for h in range(2):
-                passes("K", 1, h, g)
+        reorder(REORDERED_ON_SCALAR)
         for h in range(2):
+            project_pass("K", 1, h, 0)
+        project("Q", 0, 0)
+        for h in range(2):
+            project_pass("K", 1, h, 1)
             empty("K", 1, h)
-        project_both("Q", 0)
+        project("Q", 0, 1)
         scale_turned(2)
         widen(4)
         quant_x(2)
         widen(5)
         widen(6)
         project_both("Q", 1)
-        turn(3)
-        cast_behind(7, "xw_3")
+        turn(REORDERED_ON_SCALAR)
+        cast_behind(REORDERED_ON_GPSIMD, REORDERED_ON_SCALAR)
         turn(4)
         turn(5)
         scale_turned(3)
@@ -371,7 +357,7 @@ def tile_attentionnet_pa_w4_kernel(tc, x_bytes, x_scale, wq_words, wq_scales, wk
         for h in range(2):
             quant_k(0, h)
         scale_turned(4, slice(1, 2))
-        reorder(7)
+        reorder(REORDERED_ON_GPSIMD)
         project_both("Q", 2)
         quant_q(0, 0, 4)
         quant_x(4)
@@ -383,13 +369,13 @@ def tile_attentionnet_pa_w4_kernel(tc, x_bytes, x_scale, wq_words, wq_scales, wk
         for h in range(2):
             quant_k(2, h)
         quant_x(5)
+
         project("K", 4, 0)
         score(0)
         scale_turned(6)
         row_min(0)
         quant_x(6)
         quant_q(2, 0, 2)
-
         project("K", 4, 1)
         exps(0)
         score(1)
@@ -415,6 +401,7 @@ def tile_attentionnet_pa_w4_kernel(tc, x_bytes, x_scale, wq_words, wq_scales, wk
         exps(3)
         invert(2)
         quant_k(6, 0)
+
         project("Q", 4, 0, on_vector=True)
         project("Q", 4, 1)
         quant_k(6, 1)
@@ -440,6 +427,7 @@ def tile_attentionnet_pa_w4_kernel(tc, x_bytes, x_scale, wq_words, wq_scales, wk
         quant_q(7, 0, 1)
         finish(4)
         quant_q(7, 1, 1)
+
         for i in (6, 7):
             score(i)
         row_min(6)

@@ -19,14 +19,12 @@ B, S, D = 2, 512, 1024
 P = 128
 TILES = B * S // P
 PER_BATCH = S // P
+PAIRS = TILES // 2
 PASSES = D // 512
 INV = 1.0 / math.sqrt(128.0)
 FLOPS = 2 * 2 * B * S * D * D + 2 * B * S * S * D
 BANKS = 8
 SPLIT = 320
-STEPPED = (1, 2)
-REORDERED_ON_SCALAR, REORDERED_ON_GPSIMD = 3, 7
-NORMALISED_ON_GPSIMD = (0, 1)
 
 
 def tile_attentionnet_pa_w4_kernel(tc, x_bytes, x_scale, wq_words, wq_scales, wk_words, wk_scales, out):
@@ -53,10 +51,11 @@ def tile_attentionnet_pa_w4_kernel(tc, x_bytes, x_scale, wq_words, wq_scales, wk
             return {k: keep.tile(shape, dtype, name="%s_%s" % (name, k), align_bytes=256) for k in keys}
 
         every = range(TILES)
+        pairs = range(PAIRS)
         halves = ["K0", "K1", "Q0", "Q1"]
         zeros = keep.tile([P, 512], BF16, name="zeros")
-        idle_bank = take("idle")
         ident = keep.tile([P, P], F32, name="ident")
+        ident16 = keep.tile([P, P], BF16, name="ident16")
         scale_k = keep.tile([P, PASSES * 4], F32, name="scale_k")
         ones = keep.tile([P, 1], F32, name="ones")
         xb = tiles("xb", every, [P, D], U8)
@@ -65,29 +64,27 @@ def tile_attentionnet_pa_w4_kernel(tc, x_bytes, x_scale, wq_words, wq_scales, wk
         wts = tiles("wts", halves, [P, 2048], U8)
         wts_s = tiles("wts_s", "KQ", [P, 2048], U8)
         xw = tiles("xw", every, [P, D], BF16)
-        xv = tiles("xv", (REORDERED_ON_SCALAR,), [P, D], BF16)
-        xg = tiles("xg", range(TILES // 2), [P, 2 * D], BF16)
-        xc = tiles("xc", range(TILES // 2), [P, 512], U32)
-        xs = tiles("xs", range(TILES // 2), [P, 512], U8)
+        xv = {}
+        xg = tiles("xg", pairs, [P, 2 * D], BF16)
+        xc = tiles("xc", pairs, [P, 512], U32)
+        xs = tiles("xs", pairs, [P, 512], U8)
+        units = [m + str(n) + str(h) for m in "KQ" for n in pairs for h in range(2)]
+        staged = tiles("staged", units, [P, D], BF16)
         yk = tiles("yk", range(2 * B), [P, 4 * S], BF16)
         kc = tiles("kc", range(2 * B), [P, S], U32)
         ks = tiles("ks", range(2 * B), [P, S], U8)
-        yq = tiles("yq", range(TILES // 2), [P, 2 * D], BF16)
-        qc = tiles("qc", range(TILES // 2), [P, 512], U32)
-        qs = tiles("qs", range(TILES // 2), [P, 512], U8)
+        yq = tiles("yq", pairs, [P, 2 * D], BF16)
+        qc = tiles("qc", pairs, [P, 512], U32)
+        qs = tiles("qs", pairs, [P, 512], U8)
         neg = tiles("neg", every, [P, S], F32)
         low = tiles("low", every, [P, 1], F32)
         ex = tiles("ex", every, [P, S], F32)
         total = tiles("total", every, [P, 1], F32)
         inv = tiles("inv", every, [P, 1], F32)
-        res = tiles("res", every, [P, S], F32)
+        res = neg
 
         hbm_w = {"K": wk_words, "Q": wq_words}
         hbm_s = {"K": wk_scales, "Q": wq_scales}
-        turned = {}
-        turned_pass = {}
-        scores = {}
-        sums = {}
 
         def load_x(i):
             nc.sync.dma_start(out=xb[i][:], in_=x_rows[i * P : (i + 1) * P, :])
@@ -104,16 +101,27 @@ def tile_attentionnet_pa_w4_kernel(tc, x_bytes, x_scale, wq_words, wq_scales, wk
             for r in range(4):
                 nc.sync.dma_start(out=dst[r:P:32], in_=src[:, r:16:4, :].rearrange("g q n -> q g n"))
 
-        def permute_w(m, h):
-            nc.vector.tensor_copy(
-                out=wts[m + str(h)][:].bitcast(I32).rearrange("p (t c w) -> p t c w", t=4, w=4),
-                in_=raw[m + str(h)][:].bitcast(I32).rearrange("p (c t w) -> p t c w", t=4, w=4),
+        def move(engine, dst, src):
+            if engine is nc.scalar:
+                nc.scalar.copy(dst, src)
+            else:
+                engine.tensor_copy(out=dst, in_=src)
+
+        def word(engine):
+            return U32 if engine is nc.scalar else I32
+
+        def permute_w(m, h, engine):
+            move(
+                engine,
+                wts[m + str(h)][:].bitcast(word(engine)).rearrange("p (t c w) -> p t c w", t=4, w=4),
+                raw[m + str(h)][:].bitcast(word(engine)).rearrange("p (c t w) -> p t c w", t=4, w=4),
             )
 
         def permute_s(m, engine):
-            engine.tensor_copy(
-                out=wts_s[m][:].bitcast(I32).rearrange("p (t c w) -> p t c w", t=4, w=2),
-                in_=raw_s[m][:].bitcast(I32).rearrange("p (c t w) -> p t c w", t=4, w=2),
+            move(
+                engine,
+                wts_s[m][:].bitcast(word(engine)).rearrange("p (t c w) -> p t c w", t=4, w=2),
+                raw_s[m][:].bitcast(word(engine)).rearrange("p (c t w) -> p t c w", t=4, w=2),
             )
 
         def quantize(codes, scales, values, first, count):
@@ -121,18 +129,20 @@ def tile_attentionnet_pa_w4_kernel(tc, x_bytes, x_scale, wq_words, wq_scales, wk
             nc.vector.quantize_mx(out=codes[:, cols].bitcast(FP8X4), scales=scales[:, cols], in_=values[:, first * 512 : (first + count) * 512])
 
         def warm_up(count):
+            idle = take("idle")
             for n in range(count):
-                nc.tensor.matmul(idle_bank[:], zeros[:, 0:P], zeros[:], start=True, stop=True)
+                nc.tensor.matmul(idle[:], zeros[:, 0:P], zeros[:], start=True, stop=True)
+            give_back("idle")
 
-        def cast(dst, i, cols):
+        def cast(dst, i, cols=slice(0, D)):
             nc.scalar.copy(dst[:, cols], xb[i][:, cols].bitcast(FP8))
 
         def cast_behind(i, done):
-            xv[i] = keep.tile([P, D], BF16, name="xw_%s" % done, align_bytes=256)
+            xv[i] = keep.tile([P, D], BF16, name=done, align_bytes=256)
             nc.gpsimd.tensor_copy(out=xv[i][:], in_=xb[i][:].bitcast(FP8))
 
-        def reorder(i):
-            nc.scalar.copy(xw[i][:].bitcast(U32).rearrange("p (u w) -> p u w", u=2), xv[i][:].bitcast(U32).rearrange("p (w u) -> p u w", u=2))
+        def reorder(i, engine):
+            move(engine, xw[i][:].bitcast(word(engine)).rearrange("p (u w) -> p u w", u=2), xv[i][:].bitcast(word(engine)).rearrange("p (w u) -> p u w", u=2))
 
         def widen(i, cols=slice(0, D)):
             nc.vector.tensor_scalar(
@@ -143,24 +153,18 @@ def tile_attentionnet_pa_w4_kernel(tc, x_bytes, x_scale, wq_words, wq_scales, wk
                 op0=ALU.mult,
             )
 
-        def turn(i):
-            turned[i] = take(("x", i))
-            pairs = xw[i][:].bitcast(F32)
+        def turn(i, stepped=False):
+            bank = take(("x", i))
+            words = xw[i][:].bitcast(F32)
             for g in range(PASSES):
                 for u in range(2):
-                    if i in STEPPED:
-                        src = pairs[:, 256 * g + u : 256 * (g + 1) : 2]
-                    else:
-                        src = pairs[:, u * 256 + g * P : u * 256 + (g + 1) * P]
-                    nc.tensor.transpose(turned[i][:, u * 256 + g * P : u * 256 + (g + 1) * P], src, ident[:])
-
-        def x_values(i):
-            return xg[i // 2][:, (i % 2) * D : (i % 2 + 1) * D]
+                    src = words[:, 256 * g + u : 256 * (g + 1) : 2] if stepped else words[:, u * 256 + g * P : u * 256 + (g + 1) * P]
+                    nc.tensor.transpose(bank[:, u * 256 + g * P : u * 256 + (g + 1) * P], src, ident[:])
 
         def scale_turned(i, part=slice(0, PASSES)):
             nc.vector.tensor_tensor(
-                out=x_values(i).rearrange("p (g r u e) -> p g r u e", g=PASSES, u=2, e=2)[:, part],
-                in0=turned[i][:].bitcast(BF16).rearrange("p (u g r e) -> p g r u e", g=PASSES, u=2, e=2)[:, part],
+                out=xg[i // 2][:].rearrange("p (g j r u e) -> p j g r u e", g=PASSES, j=2, u=2, e=2)[:, i % 2, part],
+                in0=held["x", i][1][:].bitcast(BF16).rearrange("p (u g r e) -> p g r u e", g=PASSES, u=2, e=2)[:, part],
                 in1=scale_k[:].rearrange("p (g u e) -> p g u e", u=2, e=2).unsqueeze(2).to_broadcast([P, PASSES, P, 2, 2])[:, part],
                 op=ALU.mult,
             )
@@ -168,92 +172,90 @@ def tile_attentionnet_pa_w4_kernel(tc, x_bytes, x_scale, wq_words, wq_scales, wk
                 give_back(("x", i))
 
         def turn_pass(i, g):
-            turned_pass[i, g] = take(("pass", i, g))
-            pairs = xw[i][:, g * 512 : (g + 1) * 512].bitcast(F32)
-            for u in range(2):
-                src = pairs[:, u:256:2] if i in STEPPED else pairs[:, u * P : (u + 1) * P]
-                nc.tensor.transpose(turned_pass[i, g][:, u * P : (u + 1) * P], src, ident[:])
+            bank = take(("pass", i, g))
+            for t in range(4):
+                u, e = divmod(t, 2)
+                first = g * 512 + u * 256 + e
+                nc.tensor.matmul(bank[:, t * P : (t + 1) * P], xw[i][:, first : first + 255 : 2], ident16[:], start=True, stop=True)
 
         def scale_pass(i, g):
+            first = (2 * g + i % 2) * 512
             nc.vector.tensor_tensor(
-                out=x_values(i)[:, g * 512 : (g + 1) * 512].rearrange("p (r u e) -> p r u e", u=2, e=2),
-                in0=turned_pass[i, g][:, 0:256].bitcast(BF16).rearrange("p (u r e) -> p r u e", u=2, e=2),
-                in1=scale_k[:, g * 4 : (g + 1) * 4].rearrange("p (u e) -> p u e", e=2).unsqueeze(1).to_broadcast([P, P, 2, 2]),
+                out=xg[i // 2][:, first : first + 512].rearrange("p (r t) -> p r t", t=4),
+                in0=held["pass", i, g][1][:].rearrange("p (t r) -> p r t", t=4),
+                in1=scale_k[:, g * 4 : (g + 1) * 4].unsqueeze(1).to_broadcast([P, P, 4]),
                 op=ALU.mult,
             )
             give_back(("pass", i, g))
 
-        def scale_slots(i, g):
-            values = turned_pass[i, g][:, 0:256].bitcast(BF16)
-            for t in range(4):
-                u, e = divmod(t, 2)
-                nc.scalar.activation(
-                    out=x_values(i)[:, g * 512 + t : (g + 1) * 512 : 4],
-                    in_=values[:, u * 256 + e : (u + 1) * 256 : 2],
-                    func=ACT.Copy,
-                    scale=scale_k[:, g * 4 + t : g * 4 + t + 1],
-                )
-            give_back(("pass", i, g))
+        def quant_x(n, first=0, count=4):
+            quantize(xc[n], xs[n], xg[n], first, count)
 
-        def quant_pass(i, g):
-            quantize(xc[i // 2], xs[i // 2], xg[i // 2], 2 * (i % 2) + g, 1)
+        def project_mx(bank, out_cols, m, h, t, g, n, cols, start, stop):
+            plane = (4 * t + 2 * g + h) * P
+            nc.tensor.matmul_mx(
+                out=bank[:, out_cols],
+                lhsT=wts[m + str(h)][:, t * 512 + g * 256 : t * 512 + (g + 1) * 256].bitcast(FP4X4),
+                lhsT_scale=wts_s[m][:, plane : plane + P],
+                rhs=xc[n][:, cols].bitcast(FP8X4),
+                rhs_scale=xs[n][:, cols],
+                start=start,
+                stop=stop,
+            )
 
-        def quant_x(i):
-            quantize(xc[i // 2], xs[i // 2], xg[i // 2], 2 * (i % 2), PASSES)
-
-        def project_pass(m, i, h, g):
-            if g == 0:
-                sums[m, i, h] = take((m, i, h))
-            cols = slice((2 * (i % 2) + g) * P, (2 * (i % 2) + g + 1) * P)
-            for t in range(4):
-                plane = (4 * t + 2 * g + h) * P
-                nc.tensor.matmul_mx(
-                    out=sums[m, i, h][:, t * P : (t + 1) * P],
-                    lhsT=wts[m + str(h)][:, t * 512 + g * 256 : t * 512 + (g + 1) * 256].bitcast(FP4X4),
-                    lhsT_scale=wts_s[m][:, plane : plane + P],
-                    rhs=xc[i // 2][:, cols].bitcast(FP8X4),
-                    rhs_scale=xs[i // 2][:, cols],
-                    start=(g == 0 and t == 0),
-                    stop=(g == PASSES - 1 and t == 3),
-                )
-
-        def empty(m, i, h, on_vector=False):
-            b, j = divmod(i, PER_BATCH)
+        def values(m, n, h):
             if m == "K":
-                dst = yk[2 * b + h][:, j * 512 : (j + 1) * 512]
-            else:
-                dst = yq[i // 2][:, (2 * (i % 2) + h) * 512 : (2 * (i % 2) + h + 1) * 512]
-            dst = dst.rearrange("p (n t) -> p n t", t=4)
-            src = sums[m, i, h][:].rearrange("p (t n) -> p n t", t=4)
-            if on_vector:
-                nc.vector.tensor_copy(out=dst, in_=src)
-            else:
-                nc.scalar.copy(dst, src)
+                return yk[2 * (n // 2) + h][:, (n % 2) * D : (n % 2 + 1) * D]
+            return yq[n][:, h * D : (h + 1) * D]
+
+        def project(m, i, h, engine=nc.scalar):
+            bank = take((m, i, h))
+            n, j = divmod(i, 2)
+            for g in range(PASSES):
+                for t in range(4):
+                    cols = slice((2 * g + j) * P, (2 * g + j + 1) * P)
+                    project_mx(bank, slice(t * P, (t + 1) * P), m, h, t, g, n, cols, g == 0 and t == 0, g == PASSES - 1 and t == 3)
+            move(engine, values(m, n, h)[:, j * 512 : (j + 1) * 512].rearrange("p (r t) -> p r t", t=4), bank[:].rearrange("p (t r) -> p r t", t=4))
             give_back((m, i, h))
 
-        def project(m, i, h, on_vector=False):
+        def project_pair(m, n, h, u, direct=False, engine=nc.scalar):
+            bank = take((m, n, h, u))
             for g in range(PASSES):
-                project_pass(m, i, h, g)
-            empty(m, i, h, on_vector)
+                for e in range(2):
+                    cols = slice(256 * g, 256 * (g + 1))
+                    project_mx(bank, slice(e * 256, (e + 1) * 256), m, h, 2 * u + e, g, n, cols, g == 0 and e == 0, g == PASSES - 1 and e == 1)
+            if direct:
+                dst = values(m, n, h).rearrange("p (r u e) -> p u r e", u=2, e=2)[:, u]
+            else:
+                dst = staged[m + str(n) + str(h)][:, u * 512 : (u + 1) * 512].rearrange("p (r e) -> p r e", e=2)
+            move(engine, dst, bank[:].rearrange("p (e r) -> p r e", e=2))
+            give_back((m, n, h, u))
 
-        def project_both(m, i):
-            for h in range(2):
-                project(m, i, h)
+        def project_half(m, n, h, direct=False):
+            for u in range(2):
+                project_pair(m, n, h, u, direct)
 
-        def quant_k(i, h):
-            n = 2 * (i // PER_BATCH) + h
-            quantize(kc[n], ks[n], yk[n], i % PER_BATCH, 2)
+        def join(m, n, h, engine=nc.vector):
+            move(
+                engine,
+                values(m, n, h).bitcast(word(engine)).rearrange("p (r u) -> p r u", u=2),
+                staged[m + str(n) + str(h)][:].bitcast(word(engine)).rearrange("p (u r) -> p r u", u=2),
+            )
 
-        def quant_q(i, first, count):
-            quantize(qc[i // 2], qs[i // 2], yq[i // 2], 2 * (i % 2) + first, count)
+        def quant_k(n, h):
+            b = 2 * (n // 2) + h
+            quantize(kc[b], ks[b], yk[b], 2 * (n % 2), 2)
+
+        def quant_q(n, first=0, count=4):
+            quantize(qc[n], qs[n], yq[n], first, count)
 
         def score(i):
             b = i // PER_BATCH
-            scores[i] = take(("s", i))
+            bank = take(("s", i))
             for h in range(2):
-                cols = slice((2 * (i % 2) + h) * P, (2 * (i % 2) + h + 1) * P)
+                cols = slice((2 * h + i % 2) * P, (2 * h + i % 2 + 1) * P)
                 nc.tensor.matmul_mx(
-                    out=scores[i][:],
+                    out=bank[:],
                     lhsT=qc[i // 2][:, cols].bitcast(FP8X4),
                     lhsT_scale=qs[i // 2][:, cols],
                     rhs=kc[2 * b + h][:].bitcast(FP8X4),
@@ -263,7 +265,7 @@ def tile_attentionnet_pa_w4_kernel(tc, x_bytes, x_scale, wq_words, wq_scales, wk
                 )
 
         def row_min(i):
-            nc.vector.tensor_scalar(out=neg[i][:], in0=scores[i][:], scalar1=-INV, scalar2=None, op0=ALU.mult, op1=ALU.min, accum_out=low[i][:])
+            nc.vector.tensor_scalar(out=neg[i][:], in0=held["s", i][1][:], scalar1=-INV, scalar2=None, op0=ALU.mult, op1=ALU.min, accum_out=low[i][:])
             give_back(("s", i))
 
         def exps(i):
@@ -272,176 +274,172 @@ def tile_attentionnet_pa_w4_kernel(tc, x_bytes, x_scale, wq_words, wq_scales, wk
         def invert(i):
             nc.vector.reciprocal(inv[i][:], total[i][:])
 
-        def finish(i):
-            if i in NORMALISED_ON_GPSIMD:
+        def finish(i, on_gpsimd=False):
+            if on_gpsimd:
                 nc.gpsimd.tensor_scalar(out=res[i][:], in0=ex[i][:], scalar1=inv[i][:], scalar2=1.0, op0=ALU.mult, op1=ALU.mult)
             else:
                 nc.vector.tensor_scalar(out=res[i][:], in0=ex[i][:], scalar1=inv[i][:], scalar2=None, op0=ALU.mult)
             nc.sync.dma_start(out=out_rows[i * P : (i + 1) * P, :], in_=res[i][:])
 
+        def finish_last():
+            i = TILES - 1
+            rows = slice(i * P, (i + 1) * P)
+            left, right = slice(0, SPLIT), slice(SPLIT, S)
+            nc.vector.tensor_scalar(out=res[i][:, left], in0=ex[i][:, left], scalar1=inv[i][:], scalar2=None, op0=ALU.mult)
+            nc.scalar.activation(out=res[i][:, right], in_=ex[i][:, right], func=ACT.Copy, scale=inv[i][:])
+            nc.sync.dma_start(out=out_rows[rows, left], in_=res[i][:, left])
+            nc.scalar.dma_start(out=out_rows[rows, right], in_=res[i][:, right])
+
         ctx.enter_context(tc.manual_schedule())
 
-        make_identity(nc, ident[:])
-        nc.gpsimd.memset(ones[:], 1.0)
-        nc.vector.memset(raw_s["K"][:].bitcast(I32), 0)
         nc.vector.memset(zeros[:], 0.0)
+        nc.vector.memset(ident16[:], 0.0)
+        make_identity(nc, ident16[:], nomemset=True)
+        nc.vector.memset(ones[:], 1.0)
+        nc.vector.memset(raw_s["K"][:].bitcast(I32), 0)
         nc.vector.memset(raw_s["Q"][:].bitcast(I32), 0)
 
         load_x(0)
         nc.scalar.dma_start(out=scale_k[:].rearrange("p (g t) -> p g t", t=4), in_=x_scale.rearrange("a b (g p t) -> p (a b g) t", p=P, t=4))
-        load_x(1)
+        for i in (2, 1, 3):
+            load_x(i)
         load_s("K")
-        load_x(2)
         for h in range(2):
             load_w("K", h)
-        load_x(3)
         load_s("Q")
         for h in range(2):
             load_w("Q", h)
-        for i in range(4, TILES):
+        for i in (7, 4, 5, 6):
             load_x(i)
 
         warm_up(3)
+        nc.scalar.activation(out=ident[:], in_=ident16[:], func=ACT.Copy)
         for g in range(PASSES):
             widen(0, slice(g * 512, (g + 1) * 512))
             turn_pass(0, g)
-        warm_up(2)
-        nc.scalar.activation(out=xw[1][:, 0:P], in_=xb[1][:, 0:P].bitcast(FP8), func=ACT.Copy)
-        cast(xw[1], 1, slice(P, D))
+        cast(xw[2], 2)
+        turn(2, True)
         for g in range(PASSES):
+            widen(1, slice(g * 512, (g + 1) * 512))
             turn_pass(1, g)
-        warm_up(1)
-        for g in range(PASSES):
-            cast(xw[2], 2, slice(g * 512, (g + 1) * 512))
-        turn(2)
-        give_back("idle")
+        cast(xw[3], 3)
+        turn(3, True)
         for g in range(PASSES):
             scale_pass(0, g)
-        permute_s("K", nc.gpsimd)
-        permute_w("K", 0)
-        for g in range(PASSES):
-            quant_pass(0, g)
-        permute_w("K", 1)
+        permute_s("K", nc.scalar)
+        for h in range(2):
+            permute_w("K", h, nc.scalar)
+        permute_s("Q", nc.scalar)
+        quant_x(0, 0, 1)
         scale_pass(1, 0)
-        scale_slots(1, 1)
-        quant_pass(1, 0)
-        permute_s("Q", nc.vector)
-        permute_w("Q", 0)
-        quant_pass(1, 1)
-        permute_w("Q", 1)
-        cast(xv[REORDERED_ON_SCALAR], REORDERED_ON_SCALAR, slice(0, D))
+        quant_x(0, 2, 1)
+        scale_pass(1, 1)
+        quant_x(0, 1, 1)
+        scale_turned(2, slice(0, 1))
+        quant_x(0, 3, 1)
 
-        project_both("K", 0)
-        reorder(REORDERED_ON_SCALAR)
+        for i in range(2):
+            for h in range(2):
+                project("K", i, h)
+        permute_w("Q", 0, nc.vector)
+        permute_w("Q", 1, nc.vector)
+        cast_behind(7, "raw_Q1")
+        scale_turned(2, slice(1, 2))
+        scale_turned(3)
         for h in range(2):
-            project_pass("K", 1, h, 0)
-        project("Q", 0, 0)
-        for h in range(2):
-            project_pass("K", 1, h, 1)
-            empty("K", 1, h)
-        project("Q", 0, 1)
-        scale_turned(2)
+            project_half("Q", 0, h)
+        quant_x(1)
         widen(4)
-        quant_x(2)
         widen(5)
         widen(6)
-        project_both("Q", 1)
-        turn(REORDERED_ON_SCALAR)
-        cast_behind(REORDERED_ON_GPSIMD, REORDERED_ON_SCALAR)
-        turn(4)
-        turn(5)
-        scale_turned(3)
-        project_both("K", 2)
-        scale_turned(4, slice(0, 1))
-        quant_x(3)
+        reorder(7, nc.scalar)
+        project_half("K", 1, 0)
+        for i in range(4, TILES):
+            turn(i)
         for h in range(2):
             quant_k(0, h)
-        scale_turned(4, slice(1, 2))
-        reorder(REORDERED_ON_GPSIMD)
-        project_both("Q", 2)
-        quant_q(0, 0, 4)
-        quant_x(4)
-        project_both("K", 3)
+            join("Q", 0, h, nc.scalar)
+        project_half("K", 1, 1, True)
+        scale_turned(4)
         scale_turned(5)
-        turn(6)
-        turn(7)
-        project_both("Q", 3)
-        for h in range(2):
-            quant_k(2, h)
-        quant_x(5)
-
-        project("K", 4, 0)
-        score(0)
+        quant_q(0)
+        project_half("Q", 1, 0, True)
+        project_half("Q", 1, 1)
+        quant_x(2)
+        join("K", 1, 0)
+        quant_k(1, 1)
+        quant_k(1, 0)
         scale_turned(6)
-        row_min(0)
-        quant_x(6)
-        quant_q(2, 0, 2)
-        project("K", 4, 1)
-        exps(0)
-        score(1)
-        row_min(1)
-        invert(0)
+        project_half("K", 2, 0)
+        score(0)
         scale_turned(7)
-        finish(0)
-        project_both("K", 5)
+        project_half("K", 2, 1)
+        score(1)
+        join("Q", 1, 1)
+        quant_x(3)
+        row_min(0)
+        quant_q(1)
+        row_min(1)
+        exps(0)
+        project_half("K", 3, 0)
+        join("K", 2, 0)
+        join("K", 2, 1)
+        invert(0)
         exps(1)
         score(2)
-        quant_q(3, 0, 2)
-        quant_x(7)
+        quant_k(2, 0)
+        quant_k(2, 1)
         row_min(2)
-        project_both("K", 6)
+        finish(0)
+        project_half("K", 3, 1)
+        join("K", 3, 0)
+        invert(1)
         exps(2)
         score(3)
-        quant_k(4, 0)
-        invert(1)
-        quant_k(4, 1)
-        finish(1)
         row_min(3)
-        project_both("K", 7)
-        exps(3)
-        invert(2)
-        quant_k(6, 0)
+        finish(1)
 
-        project("Q", 4, 0, on_vector=True)
+        project("Q", 4, 0)
+        join("K", 3, 1)
+        quant_k(3, 0)
+        invert(2)
+        quant_k(3, 1)
         project("Q", 4, 1)
-        quant_k(6, 1)
-        quant_q(4, 0, 1)
-        invert(3)
-        project_both("Q", 5)
-        quant_q(4, 1, 1)
-        for i in (2, 3):
-            finish(i)
+        exps(3)
+        quant_q(2, 0, 1)
+        project("Q", 5, 0)
+        quant_q(2, 2, 1)
+        finish(2)
+        project("Q", 5, 1)
         score(4)
+        invert(3)
+        quant_q(2, 1, 1)
+        finish(3)
         project("Q", 6, 0)
         row_min(4)
+        quant_q(2, 3, 1)
         exps(4)
-        quant_q(5, 0, 2)
-        project("Q", 6, 1, on_vector=True)
+        project("Q", 6, 1, nc.vector)
         project("Q", 7, 0)
         score(5)
-        project("Q", 7, 1)
         invert(4)
-        quant_q(6, 0, 2)
+        quant_q(3, 0, 1)
+        quant_q(3, 2, 1)
+        project("Q", 7, 1)
         row_min(5)
         exps(5)
-        quant_q(7, 0, 1)
+        quant_q(3, 1, 1)
         finish(4)
-        quant_q(7, 1, 1)
-
-        for i in (6, 7):
-            score(i)
+        quant_q(3, 3, 1)
+        score(6)
+        score(7)
         row_min(6)
         invert(5)
         row_min(7)
         finish(5)
-        for i in (6, 7):
-            exps(i)
+        exps(6)
+        exps(7)
         invert(6)
         finish(6)
         invert(7)
-        rows = slice((TILES - 1) * P, TILES * P)
-        left, right = slice(0, SPLIT), slice(SPLIT, S)
-        nc.vector.tensor_scalar(out=res[7][:, left], in0=ex[7][:, left], scalar1=inv[7][:], scalar2=None, op0=ALU.mult)
-        nc.scalar.activation(out=res[7][:, right], in_=ex[7][:, right], func=ACT.Copy, scale=inv[7][:])
-        nc.sync.dma_start(out=out_rows[rows, left], in_=res[7][:, left])
-        nc.scalar.dma_start(out=out_rows[rows, right], in_=res[7][:, right])
+        finish_last()

@@ -25,6 +25,8 @@ INV = 1.0 / math.sqrt(128.0)
 FLOPS = 2 * 2 * B * S * D * D + 2 * B * S * S * D
 BANKS = 8
 SPLIT = 320
+PAIRED_X = (0, 2)
+PAIRED_Q = (0,)
 
 
 def tile_attentionnet_pa_w4_kernel(tc, x_bytes, x_scale, wq_words, wq_scales, wk_words, wk_scales, out):
@@ -50,12 +52,12 @@ def tile_attentionnet_pa_w4_kernel(tc, x_bytes, x_scale, wq_words, wq_scales, wk
         def tiles(name, keys, shape, dtype):
             return {k: keep.tile(shape, dtype, name="%s_%s" % (name, k), align_bytes=256) for k in keys}
 
+        idle = take("idle")
         every = range(TILES)
         pairs = range(PAIRS)
         halves = ["K0", "K1", "Q0", "Q1"]
         zeros = keep.tile([P, 512], BF16, name="zeros")
         ident = keep.tile([P, P], F32, name="ident")
-        ident16 = keep.tile([P, P], BF16, name="ident16")
         scale_k = keep.tile([P, PASSES * 4], F32, name="scale_k")
         ones = keep.tile([P, 1], F32, name="ones")
         xb = tiles("xb", every, [P, D], U8)
@@ -64,7 +66,7 @@ def tile_attentionnet_pa_w4_kernel(tc, x_bytes, x_scale, wq_words, wq_scales, wk
         wts = tiles("wts", halves, [P, 2048], U8)
         wts_s = tiles("wts_s", "KQ", [P, 2048], U8)
         xw = tiles("xw", every, [P, D], BF16)
-        xv = {}
+        xv = tiles("xv", (3,), [P, D], BF16)
         xg = tiles("xg", pairs, [P, 2 * D], BF16)
         xc = tiles("xc", pairs, [P, 512], U32)
         xs = tiles("xs", pairs, [P, 512], U8)
@@ -79,8 +81,10 @@ def tile_attentionnet_pa_w4_kernel(tc, x_bytes, x_scale, wq_words, wq_scales, wk
         neg = tiles("neg", every, [P, S], F32)
         low = tiles("low", every, [P, 1], F32)
         ex = tiles("ex", every, [P, S], F32)
-        total = tiles("total", every, [P, 1], F32)
-        inv = tiles("inv", every, [P, 1], F32)
+        totals = tiles("total", pairs, [P, 2], F32)
+        invs = tiles("inv", pairs, [P, 2], F32)
+        total = {i: totals[i // 2][:, i % 2 : i % 2 + 1] for i in every}
+        inv = {i: invs[i // 2][:, i % 2 : i % 2 + 1] for i in every}
         res = neg
 
         hbm_w = {"K": wk_words, "Q": wq_words}
@@ -100,6 +104,9 @@ def tile_attentionnet_pa_w4_kernel(tc, x_bytes, x_scale, wq_words, wq_scales, wk
             src = hbm_s[m].bitcast(I32)
             for r in range(4):
                 nc.sync.dma_start(out=dst[r:P:32], in_=src[:, r:16:4, :].rearrange("g q n -> q g n"))
+
+        def block(paired, i, part):
+            return 2 * part + i % 2 if i // 2 in paired else 2 * (i % 2) + part
 
         def move(engine, dst, src):
             if engine is nc.scalar:
@@ -129,10 +136,8 @@ def tile_attentionnet_pa_w4_kernel(tc, x_bytes, x_scale, wq_words, wq_scales, wk
             nc.vector.quantize_mx(out=codes[:, cols].bitcast(FP8X4), scales=scales[:, cols], in_=values[:, first * 512 : (first + count) * 512])
 
         def warm_up(count):
-            idle = take("idle")
             for n in range(count):
                 nc.tensor.matmul(idle[:], zeros[:, 0:P], zeros[:], start=True, stop=True)
-            give_back("idle")
 
         def cast(dst, i, cols=slice(0, D)):
             nc.scalar.copy(dst[:, cols], xb[i][:, cols].bitcast(FP8))
@@ -163,7 +168,7 @@ def tile_attentionnet_pa_w4_kernel(tc, x_bytes, x_scale, wq_words, wq_scales, wk
 
         def scale_turned(i, part=slice(0, PASSES)):
             nc.vector.tensor_tensor(
-                out=xg[i // 2][:].rearrange("p (g j r u e) -> p j g r u e", g=PASSES, j=2, u=2, e=2)[:, i % 2, part],
+                out=xg[i // 2][:].rearrange("p (%s r u e) -> p j g r u e" % ("g j" if i // 2 in PAIRED_X else "j g"), g=PASSES, j=2, u=2, e=2)[:, i % 2, part],
                 in0=held["x", i][1][:].bitcast(BF16).rearrange("p (u g r e) -> p g r u e", g=PASSES, u=2, e=2)[:, part],
                 in1=scale_k[:].rearrange("p (g u e) -> p g u e", u=2, e=2).unsqueeze(2).to_broadcast([P, PASSES, P, 2, 2])[:, part],
                 op=ALU.mult,
@@ -173,17 +178,25 @@ def tile_attentionnet_pa_w4_kernel(tc, x_bytes, x_scale, wq_words, wq_scales, wk
 
         def turn_pass(i, g):
             bank = take(("pass", i, g))
+            words = xw[i][:, g * 512 : (g + 1) * 512].bitcast(F32)
+            for u in range(2):
+                nc.tensor.transpose(bank[:, u * P : (u + 1) * P], words[:, u * P : (u + 1) * P], ident[:])
+
+        def scale_slots(i, g):
+            first = (2 * g + i % 2) * 512
+            src = held["pass", i, g][1][:, 0:256].bitcast(BF16).rearrange("p (u r e) -> p u e r", u=2, e=2)
+            dst = xg[i // 2][:, first : first + 512].rearrange("p (r u e) -> p u e r", u=2, e=2)
             for t in range(4):
                 u, e = divmod(t, 2)
-                first = g * 512 + u * 256 + e
-                nc.tensor.matmul(bank[:, t * P : (t + 1) * P], xw[i][:, first : first + 255 : 2], ident16[:], start=True, stop=True)
+                nc.scalar.activation(out=dst[:, u, e], in_=src[:, u, e], func=ACT.Copy, scale=scale_k[:, 4 * g + t : 4 * g + t + 1])
+            give_back(("pass", i, g))
 
         def scale_pass(i, g):
             first = (2 * g + i % 2) * 512
             nc.vector.tensor_tensor(
-                out=xg[i // 2][:, first : first + 512].rearrange("p (r t) -> p r t", t=4),
-                in0=held["pass", i, g][1][:].rearrange("p (t r) -> p r t", t=4),
-                in1=scale_k[:, g * 4 : (g + 1) * 4].unsqueeze(1).to_broadcast([P, P, 4]),
+                out=xg[i // 2][:, first : first + 512].rearrange("p (r u e) -> p r u e", u=2, e=2),
+                in0=held["pass", i, g][1][:, 0:256].bitcast(BF16).rearrange("p (u r e) -> p r u e", u=2, e=2),
+                in1=scale_k[:, g * 4 : (g + 1) * 4].rearrange("p (u e) -> p u e", e=2).unsqueeze(1).to_broadcast([P, P, 2, 2]),
                 op=ALU.mult,
             )
             give_back(("pass", i, g))
@@ -208,15 +221,25 @@ def tile_attentionnet_pa_w4_kernel(tc, x_bytes, x_scale, wq_words, wq_scales, wk
                 return yk[2 * (n // 2) + h][:, (n % 2) * D : (n % 2 + 1) * D]
             return yq[n][:, h * D : (h + 1) * D]
 
-        def project(m, i, h, engine=nc.scalar):
-            bank = take((m, i, h))
-            n, j = divmod(i, 2)
-            for g in range(PASSES):
-                for t in range(4):
-                    cols = slice((2 * g + j) * P, (2 * g + j + 1) * P)
-                    project_mx(bank, slice(t * P, (t + 1) * P), m, h, t, g, n, cols, g == 0 and t == 0, g == PASSES - 1 and t == 3)
-            move(engine, values(m, n, h)[:, j * 512 : (j + 1) * 512].rearrange("p (r t) -> p r t", t=4), bank[:].rearrange("p (t r) -> p r t", t=4))
+        def project_pass(m, i, h, g):
+            bank = take((m, i, h)) if g == 0 else held[m, i, h][1]
+            n = i // 2
+            cols = slice(block(PAIRED_X, i, g) * P, (block(PAIRED_X, i, g) + 1) * P)
+            for t in range(4):
+                project_mx(bank, slice(t * P, (t + 1) * P), m, h, t, g, n, cols, g == 0 and t == 0, g == PASSES - 1 and t == 3)
+
+        def empty(m, i, h, engine=nc.scalar):
+            if m == "K":
+                dst = values(m, i // 2, h)[:, (i % 2) * 512 : (i % 2 + 1) * 512]
+            else:
+                dst = yq[i // 2][:, block(PAIRED_Q, i, h) * 512 : (block(PAIRED_Q, i, h) + 1) * 512]
+            move(engine, dst.rearrange("p (r t) -> p r t", t=4), held[m, i, h][1][:].rearrange("p (t r) -> p r t", t=4))
             give_back((m, i, h))
+
+        def project(m, i, h, engine=nc.scalar):
+            for g in range(PASSES):
+                project_pass(m, i, h, g)
+            empty(m, i, h, engine)
 
         def project_pair(m, n, h, u, direct=False, engine=nc.scalar):
             bank = take((m, n, h, u))
@@ -246,6 +269,9 @@ def tile_attentionnet_pa_w4_kernel(tc, x_bytes, x_scale, wq_words, wq_scales, wk
             b = 2 * (n // 2) + h
             quantize(kc[b], ks[b], yk[b], 2 * (n % 2), 2)
 
+        def quant_keys(b):
+            quantize(kc[b], ks[b], yk[b], 0, 4)
+
         def quant_q(n, first=0, count=4):
             quantize(qc[n], qs[n], yq[n], first, count)
 
@@ -253,7 +279,7 @@ def tile_attentionnet_pa_w4_kernel(tc, x_bytes, x_scale, wq_words, wq_scales, wk
             b = i // PER_BATCH
             bank = take(("s", i))
             for h in range(2):
-                cols = slice((2 * h + i % 2) * P, (2 * h + i % 2 + 1) * P)
+                cols = slice(block(PAIRED_Q, i, h) * P, (block(PAIRED_Q, i, h) + 1) * P)
                 nc.tensor.matmul_mx(
                     out=bank[:],
                     lhsT=qc[i // 2][:, cols].bitcast(FP8X4),
@@ -269,166 +295,179 @@ def tile_attentionnet_pa_w4_kernel(tc, x_bytes, x_scale, wq_words, wq_scales, wk
             give_back(("s", i))
 
         def exps(i):
-            nc.scalar.activation(out=ex[i][:], in_=neg[i][:], func=ACT.Exp, bias=low[i][:], scale=-1.0, accum_out=total[i][:])
+            nc.scalar.activation(out=ex[i][:], in_=neg[i][:], func=ACT.Exp, bias=low[i][:], scale=-1.0, accum_out=total[i])
 
         def invert(i):
-            nc.vector.reciprocal(inv[i][:], total[i][:])
+            nc.vector.reciprocal(inv[i], total[i])
 
-        def finish(i, on_gpsimd=False):
-            if on_gpsimd:
-                nc.gpsimd.tensor_scalar(out=res[i][:], in0=ex[i][:], scalar1=inv[i][:], scalar2=1.0, op0=ALU.mult, op1=ALU.mult)
+        def invert_pair(n):
+            nc.vector.reciprocal(invs[n][:], totals[n][:])
+
+        def finish(i, engine=nc.vector):
+            if engine is nc.scalar:
+                nc.scalar.activation(out=res[i][:], in_=ex[i][:], func=ACT.Copy, scale=inv[i])
+            elif engine is nc.gpsimd:
+                nc.gpsimd.tensor_scalar(out=res[i][:], in0=ex[i][:], scalar1=inv[i], scalar2=1.0, op0=ALU.mult, op1=ALU.mult)
             else:
-                nc.vector.tensor_scalar(out=res[i][:], in0=ex[i][:], scalar1=inv[i][:], scalar2=None, op0=ALU.mult)
+                nc.vector.tensor_scalar(out=res[i][:], in0=ex[i][:], scalar1=inv[i], scalar2=None, op0=ALU.mult)
             nc.sync.dma_start(out=out_rows[i * P : (i + 1) * P, :], in_=res[i][:])
 
         def finish_last():
             i = TILES - 1
             rows = slice(i * P, (i + 1) * P)
             left, right = slice(0, SPLIT), slice(SPLIT, S)
-            nc.vector.tensor_scalar(out=res[i][:, left], in0=ex[i][:, left], scalar1=inv[i][:], scalar2=None, op0=ALU.mult)
-            nc.scalar.activation(out=res[i][:, right], in_=ex[i][:, right], func=ACT.Copy, scale=inv[i][:])
+            nc.vector.tensor_scalar(out=res[i][:, left], in0=ex[i][:, left], scalar1=inv[i], scalar2=None, op0=ALU.mult)
+            nc.scalar.activation(out=res[i][:, right], in_=ex[i][:, right], func=ACT.Copy, scale=inv[i])
             nc.sync.dma_start(out=out_rows[rows, left], in_=res[i][:, left])
             nc.scalar.dma_start(out=out_rows[rows, right], in_=res[i][:, right])
 
         ctx.enter_context(tc.manual_schedule())
 
-        nc.vector.memset(zeros[:], 0.0)
-        nc.vector.memset(ident16[:], 0.0)
-        make_identity(nc, ident16[:], nomemset=True)
-        nc.vector.memset(ones[:], 1.0)
         nc.vector.memset(raw_s["K"][:].bitcast(I32), 0)
+        nc.vector.memset(ident[:], 0.0)
+        make_identity(nc, ident[:], nomemset=True)
+        nc.vector.memset(ones[:], 1.0)
+        nc.vector.memset(zeros[:], 0.0)
         nc.vector.memset(raw_s["Q"][:].bitcast(I32), 0)
 
         load_x(0)
         nc.scalar.dma_start(out=scale_k[:].rearrange("p (g t) -> p g t", t=4), in_=x_scale.rearrange("a b (g p t) -> p (a b g) t", p=P, t=4))
-        for i in (2, 1, 3):
-            load_x(i)
+        load_x(1)
+        load_x(2)
         load_s("K")
         for h in range(2):
             load_w("K", h)
+        load_x(3)
         load_s("Q")
         for h in range(2):
             load_w("Q", h)
-        for i in (7, 4, 5, 6):
+        for i in range(4, TILES):
             load_x(i)
 
         warm_up(3)
-        nc.scalar.activation(out=ident[:], in_=ident16[:], func=ACT.Copy)
-        for g in range(PASSES):
-            widen(0, slice(g * 512, (g + 1) * 512))
-            turn_pass(0, g)
-        cast(xw[2], 2)
+        for i in range(2):
+            for g in range(PASSES):
+                widen(i, slice(g * 512, (g + 1) * 512))
+                turn_pass(i, g)
+            warm_up(1 + i)
+        nc.scalar.activation(out=xw[2][:, 0:P], in_=xb[2][:, 0:P].bitcast(FP8), func=ACT.Copy)
+        cast(xw[2], 2, slice(P, D))
         turn(2, True)
-        for g in range(PASSES):
-            widen(1, slice(g * 512, (g + 1) * 512))
-            turn_pass(1, g)
-        cast(xw[3], 3)
-        turn(3, True)
+        give_back("idle")
         for g in range(PASSES):
             scale_pass(0, g)
-        permute_s("K", nc.scalar)
+        permute_s("K", nc.gpsimd)
+        scale_slots(1, 0)
         for h in range(2):
-            permute_w("K", h, nc.scalar)
-        permute_s("Q", nc.scalar)
-        quant_x(0, 0, 1)
-        scale_pass(1, 0)
-        quant_x(0, 2, 1)
+            quant_x(0, 2 * h, 1)
+            permute_w("K", h, nc.vector)
         scale_pass(1, 1)
         quant_x(0, 1, 1)
-        scale_turned(2, slice(0, 1))
+        permute_s("Q", nc.vector)
         quant_x(0, 3, 1)
+        cast(xv[3], 3)
 
-        for i in range(2):
+        project("K", 0, 0)
+        project("K", 0, 1)
+        reorder(3, nc.scalar)
+        for g in range(PASSES):
             for h in range(2):
-                project("K", i, h)
-        permute_w("Q", 0, nc.vector)
-        permute_w("Q", 1, nc.vector)
-        cast_behind(7, "raw_Q1")
-        scale_turned(2, slice(1, 2))
-        scale_turned(3)
+                project_pass("K", 1, h, g)
+        for h in range(2):
+            empty("K", 1, h)
+            permute_w("Q", h, nc.vector)
+            scale_turned(2, slice(h, h + 1))
         for h in range(2):
             project_half("Q", 0, h)
-        quant_x(1)
         widen(4)
+        quant_x(1, 0, 2)
         widen(5)
         widen(6)
+        turn(3)
+        cast_behind(7, "xw_3")
+        turn(4)
+        turn(5)
+        scale_turned(3)
+        join("Q", 0, 0, nc.scalar)
+        project("K", 2, 0)
+        project("K", 2, 1)
+        scale_turned(4, slice(0, 1))
+        quant_x(1, 2, 2)
+        scale_turned(4, slice(1, 2))
         reorder(7, nc.scalar)
-        project_half("K", 1, 0)
-        for i in range(4, TILES):
-            turn(i)
+        project("Q", 2, 0)
+        project("Q", 2, 1)
+        project("K", 3, 0)
+        project("K", 3, 1)
         for h in range(2):
             quant_k(0, h)
-            join("Q", 0, h, nc.scalar)
-        project_half("K", 1, 1, True)
-        scale_turned(4)
         scale_turned(5)
-        quant_q(0)
-        project_half("Q", 1, 0, True)
-        project_half("Q", 1, 1)
+        turn(6)
+        turn(7)
+        join("Q", 0, 1)
+        project("Q", 3, 0)
+        project("Q", 3, 1)
         quant_x(2)
-        join("K", 1, 0)
-        quant_k(1, 1)
+        quant_q(0)
         quant_k(1, 0)
+        quant_k(1, 1)
         scale_turned(6)
-        project_half("K", 2, 0)
+        project_half("K", 2, 0, True)
         score(0)
-        scale_turned(7)
-        project_half("K", 2, 1)
-        score(1)
-        join("Q", 1, 1)
-        quant_x(3)
-        row_min(0)
         quant_q(1)
-        row_min(1)
+        row_min(0)
+        project_pair("K", 2, 1, 0, True)
         exps(0)
-        project_half("K", 3, 0)
-        join("K", 2, 0)
-        join("K", 2, 1)
+        project_pair("K", 2, 1, 1, True)
+        quant_x(3, 0, 2)
+        score(1)
+        scale_turned(7)
+        row_min(1)
+        quant_x(3, 2, 2)
         invert(0)
-        exps(1)
+        finish(0, nc.gpsimd)
         score(2)
+        project("K", 6, 0)
+        exps(1)
+        project("K", 6, 1)
+        row_min(2)
+        score(3)
+        exps(2)
+        row_min(3)
+        invert(1)
         quant_k(2, 0)
         quant_k(2, 1)
-        row_min(2)
-        finish(0)
-        project_half("K", 3, 1)
-        join("K", 3, 0)
-        invert(1)
-        exps(2)
-        score(3)
-        row_min(3)
         finish(1)
-
-        project("Q", 4, 0)
-        join("K", 3, 1)
-        quant_k(3, 0)
         invert(2)
-        quant_k(3, 1)
+        project("K", 7, 0)
+        project("K", 7, 1)
+        quant_k(3, 0)
+
+        project("Q", 4, 0, nc.vector)
         project("Q", 4, 1)
         exps(3)
+        quant_k(3, 1)
         quant_q(2, 0, 1)
         project("Q", 5, 0)
-        quant_q(2, 2, 1)
-        finish(2)
+        quant_q(2, 1, 1)
+        invert(3)
         project("Q", 5, 1)
         score(4)
-        invert(3)
-        quant_q(2, 1, 1)
+        finish(2)
         finish(3)
         project("Q", 6, 0)
         row_min(4)
-        quant_q(2, 3, 1)
         exps(4)
+        quant_q(2, 2, 2)
         project("Q", 6, 1, nc.vector)
         project("Q", 7, 0)
         score(5)
-        invert(4)
-        quant_q(3, 0, 1)
-        quant_q(3, 2, 1)
         project("Q", 7, 1)
+        invert(4)
+        quant_q(3, 0, 2)
         row_min(5)
         exps(5)
-        quant_q(3, 1, 1)
+        quant_q(3, 2, 1)
         finish(4)
         quant_q(3, 3, 1)
         score(6)

@@ -326,7 +326,6 @@ def tile_attentionnet_pa_w4_kernel(tc, x_bytes, x_scale, wq_words, wq_scales, wk
         nc.vector.memset(raw_s["K"][:].bitcast(I32), 0)
         nc.vector.memset(ident[:], 0.0)
         make_identity(nc, ident[:], nomemset=True)
-        nc.vector.memset(ones[:], 1.0)
         nc.vector.memset(zeros[:], 0.0)
         nc.vector.memset(raw_s["Q"][:].bitcast(I32), 0)
 
@@ -344,14 +343,14 @@ def tile_attentionnet_pa_w4_kernel(tc, x_bytes, x_scale, wq_words, wq_scales, wk
         for i in range(4, TILES):
             load_x(i)
 
+        nc.scalar.activation(out=ones[:], in_=zeros[:, 0:1], func=ACT.Exp)
         warm_up(3)
         for i in range(2):
             for g in range(PASSES):
                 widen(i, slice(g * 512, (g + 1) * 512))
                 turn_pass(i, g)
             warm_up(1 + i)
-        nc.scalar.activation(out=xw[2][:, 0:P], in_=xb[2][:, 0:P].bitcast(FP8), func=ACT.Copy)
-        cast(xw[2], 2, slice(P, D))
+        cast(xw[2], 2)
         turn(2, True)
         give_back("idle")
         for g in range(PASSES):
@@ -434,31 +433,31 @@ def tile_attentionnet_pa_w4_kernel(tc, x_bytes, x_scale, wq_words, wq_scales, wk
         score(3)
         exps(2)
         row_min(3)
-        invert(1)
         quant_k(2, 0)
+        invert(1)
         quant_k(2, 1)
         finish(1)
-        invert(2)
         project("K", 7, 0)
         project("K", 7, 1)
-        quant_k(3, 0)
 
         project("Q", 4, 0, nc.vector)
         project("Q", 4, 1)
         exps(3)
+        quant_k(3, 0)
         quant_k(3, 1)
         quant_q(2, 0, 1)
         project("Q", 5, 0)
         quant_q(2, 1, 1)
-        invert(3)
+        invert(2)
         project("Q", 5, 1)
         score(4)
         finish(2)
-        finish(3)
         project("Q", 6, 0)
         row_min(4)
         exps(4)
+        invert(3)
         quant_q(2, 2, 2)
+        finish(3)
         project("Q", 6, 1, nc.vector)
         project("Q", 7, 0)
         score(5)

@@ -25,6 +25,8 @@ INV = 1.0 / math.sqrt(128.0)
 FLOPS = 2 * 2 * B * S * D * D + 2 * B * S * S * D
 BANKS = 8
 SPLIT = 320
+CAST_ON_SCALAR = 3
+CAST_ON_GPSIMD = 7
 PAIRED_X = (0, 2)
 PAIRED_Q = (0,)
 
@@ -66,12 +68,11 @@ def tile_attentionnet_pa_w4_kernel(tc, x_bytes, x_scale, wq_words, wq_scales, wk
         wts = tiles("wts", halves, [P, 2048], U8)
         wts_s = tiles("wts_s", "KQ", [P, 2048], U8)
         xw = tiles("xw", every, [P, D], BF16)
-        xv = tiles("xv", (3,), [P, D], BF16)
+        xv = tiles("xv", (CAST_ON_SCALAR,), [P, D], BF16)
         xg = tiles("xg", pairs, [P, 2 * D], BF16)
         xc = tiles("xc", pairs, [P, 512], U32)
         xs = tiles("xs", pairs, [P, 512], U8)
-        units = [m + str(n) + str(h) for m in "KQ" for n in pairs for h in range(2)]
-        staged = tiles("staged", units, [P, D], BF16)
+        staged = tiles("staged", ("Q00", "Q01"), [P, D], BF16)
         yk = tiles("yk", range(2 * B), [P, 4 * S], BF16)
         kc = tiles("kc", range(2 * B), [P, S], U32)
         ks = tiles("ks", range(2 * B), [P, S], U8)
@@ -117,18 +118,16 @@ def tile_attentionnet_pa_w4_kernel(tc, x_bytes, x_scale, wq_words, wq_scales, wk
         def word(engine):
             return U32 if engine is nc.scalar else I32
 
-        def permute_w(m, h, engine):
-            move(
-                engine,
-                wts[m + str(h)][:].bitcast(word(engine)).rearrange("p (t c w) -> p t c w", t=4, w=4),
-                raw[m + str(h)][:].bitcast(word(engine)).rearrange("p (c t w) -> p t c w", t=4, w=4),
+        def permute_w(m, h):
+            nc.vector.tensor_copy(
+                out=wts[m + str(h)][:].bitcast(I32).rearrange("p (t c w) -> p t c w", t=4, w=4),
+                in_=raw[m + str(h)][:].bitcast(I32).rearrange("p (c t w) -> p t c w", t=4, w=4),
             )
 
         def permute_s(m, engine):
-            move(
-                engine,
-                wts_s[m][:].bitcast(word(engine)).rearrange("p (t c w) -> p t c w", t=4, w=2),
-                raw_s[m][:].bitcast(word(engine)).rearrange("p (c t w) -> p t c w", t=4, w=2),
+            engine.tensor_copy(
+                out=wts_s[m][:].bitcast(I32).rearrange("p (t c w) -> p t c w", t=4, w=2),
+                in_=raw_s[m][:].bitcast(I32).rearrange("p (c t w) -> p t c w", t=4, w=2),
             )
 
         def quantize(codes, scales, values, first, count):
@@ -136,18 +135,18 @@ def tile_attentionnet_pa_w4_kernel(tc, x_bytes, x_scale, wq_words, wq_scales, wk
             nc.vector.quantize_mx(out=codes[:, cols].bitcast(FP8X4), scales=scales[:, cols], in_=values[:, first * 512 : (first + count) * 512])
 
         def warm_up(count):
-            for n in range(count):
+            for _ in range(count):
                 nc.tensor.matmul(idle[:], zeros[:, 0:P], zeros[:], start=True, stop=True)
 
-        def cast(dst, i, cols=slice(0, D)):
-            nc.scalar.copy(dst[:, cols], xb[i][:, cols].bitcast(FP8))
+        def cast(dst, i):
+            nc.scalar.copy(dst[:], xb[i][:].bitcast(FP8))
 
         def cast_behind(i, done):
             xv[i] = keep.tile([P, D], BF16, name=done, align_bytes=256)
             nc.gpsimd.tensor_copy(out=xv[i][:], in_=xb[i][:].bitcast(FP8))
 
-        def reorder(i, engine):
-            move(engine, xw[i][:].bitcast(word(engine)).rearrange("p (u w) -> p u w", u=2), xv[i][:].bitcast(word(engine)).rearrange("p (w u) -> p u w", u=2))
+        def reorder(i):
+            nc.scalar.copy(xw[i][:].bitcast(U32).rearrange("p (u w) -> p u w", u=2), xv[i][:].bitcast(U32).rearrange("p (w u) -> p u w", u=2))
 
         def widen(i, cols=slice(0, D)):
             nc.vector.tensor_scalar(
@@ -183,7 +182,7 @@ def tile_attentionnet_pa_w4_kernel(tc, x_bytes, x_scale, wq_words, wq_scales, wk
                 nc.tensor.transpose(bank[:, u * P : (u + 1) * P], words[:, u * P : (u + 1) * P], ident[:])
 
         def scale_slots(i, g):
-            first = (2 * g + i % 2) * 512
+            first = block(PAIRED_X, i, g) * 512
             src = held["pass", i, g][1][:, 0:256].bitcast(BF16).rearrange("p (u r e) -> p u e r", u=2, e=2)
             dst = xg[i // 2][:, first : first + 512].rearrange("p (r u e) -> p u e r", u=2, e=2)
             for t in range(4):
@@ -192,7 +191,7 @@ def tile_attentionnet_pa_w4_kernel(tc, x_bytes, x_scale, wq_words, wq_scales, wk
             give_back(("pass", i, g))
 
         def scale_pass(i, g):
-            first = (2 * g + i % 2) * 512
+            first = block(PAIRED_X, i, g) * 512
             nc.vector.tensor_tensor(
                 out=xg[i // 2][:, first : first + 512].rearrange("p (r u e) -> p r u e", u=2, e=2),
                 in0=held["pass", i, g][1][:, 0:256].bitcast(BF16).rearrange("p (u r e) -> p r u e", u=2, e=2),
@@ -241,7 +240,7 @@ def tile_attentionnet_pa_w4_kernel(tc, x_bytes, x_scale, wq_words, wq_scales, wk
                 project_pass(m, i, h, g)
             empty(m, i, h, engine)
 
-        def project_pair(m, n, h, u, direct=False, engine=nc.scalar):
+        def project_pair(m, n, h, u, direct=False):
             bank = take((m, n, h, u))
             for g in range(PASSES):
                 for e in range(2):
@@ -251,7 +250,7 @@ def tile_attentionnet_pa_w4_kernel(tc, x_bytes, x_scale, wq_words, wq_scales, wk
                 dst = values(m, n, h).rearrange("p (r u e) -> p u r e", u=2, e=2)[:, u]
             else:
                 dst = staged[m + str(n) + str(h)][:, u * 512 : (u + 1) * 512].rearrange("p (r e) -> p r e", e=2)
-            move(engine, dst, bank[:].rearrange("p (e r) -> p r e", e=2))
+            nc.scalar.copy(dst, bank[:].rearrange("p (e r) -> p r e", e=2))
             give_back((m, n, h, u))
 
         def project_half(m, n, h, direct=False):
@@ -268,9 +267,6 @@ def tile_attentionnet_pa_w4_kernel(tc, x_bytes, x_scale, wq_words, wq_scales, wk
         def quant_k(n, h):
             b = 2 * (n // 2) + h
             quantize(kc[b], ks[b], yk[b], 2 * (n % 2), 2)
-
-        def quant_keys(b):
-            quantize(kc[b], ks[b], yk[b], 0, 4)
 
         def quant_q(n, first=0, count=4):
             quantize(qc[n], qs[n], yq[n], first, count)
@@ -300,13 +296,8 @@ def tile_attentionnet_pa_w4_kernel(tc, x_bytes, x_scale, wq_words, wq_scales, wk
         def invert(i):
             nc.vector.reciprocal(inv[i], total[i])
 
-        def invert_pair(n):
-            nc.vector.reciprocal(invs[n][:], totals[n][:])
-
         def finish(i, engine=nc.vector):
-            if engine is nc.scalar:
-                nc.scalar.activation(out=res[i][:], in_=ex[i][:], func=ACT.Copy, scale=inv[i])
-            elif engine is nc.gpsimd:
+            if engine is nc.gpsimd:
                 nc.gpsimd.tensor_scalar(out=res[i][:], in0=ex[i][:], scalar1=inv[i], scalar2=1.0, op0=ALU.mult, op1=ALU.mult)
             else:
                 nc.vector.tensor_scalar(out=res[i][:], in0=ex[i][:], scalar1=inv[i], scalar2=None, op0=ALU.mult)
@@ -351,30 +342,30 @@ def tile_attentionnet_pa_w4_kernel(tc, x_bytes, x_scale, wq_words, wq_scales, wk
                 turn_pass(i, g)
             warm_up(1 + i)
         cast(xw[2], 2)
-        turn(2, True)
+        turn(2, stepped=True)
         give_back("idle")
         for g in range(PASSES):
             scale_pass(0, g)
         permute_s("K", nc.gpsimd)
         scale_slots(1, 0)
         for h in range(2):
-            quant_x(0, 2 * h, 1)
-            permute_w("K", h, nc.vector)
+            quant_x(0, block(PAIRED_X, 0, h), 1)
+            permute_w("K", h)
         scale_pass(1, 1)
-        quant_x(0, 1, 1)
+        quant_x(0, block(PAIRED_X, 1, 0), 1)
         permute_s("Q", nc.vector)
-        quant_x(0, 3, 1)
-        cast(xv[3], 3)
+        quant_x(0, block(PAIRED_X, 1, 1), 1)
+        cast(xv[CAST_ON_SCALAR], CAST_ON_SCALAR)
 
         project("K", 0, 0)
         project("K", 0, 1)
-        reorder(3, nc.scalar)
+        reorder(CAST_ON_SCALAR)
         for g in range(PASSES):
             for h in range(2):
                 project_pass("K", 1, h, g)
         for h in range(2):
             empty("K", 1, h)
-            permute_w("Q", h, nc.vector)
+            permute_w("Q", h)
             scale_turned(2, slice(h, h + 1))
         for h in range(2):
             project_half("Q", 0, h)
@@ -383,7 +374,7 @@ def tile_attentionnet_pa_w4_kernel(tc, x_bytes, x_scale, wq_words, wq_scales, wk
         widen(5)
         widen(6)
         turn(3)
-        cast_behind(7, "xw_3")
+        cast_behind(CAST_ON_GPSIMD, "xw_3")
         turn(4)
         turn(5)
         scale_turned(3)
@@ -393,7 +384,7 @@ def tile_attentionnet_pa_w4_kernel(tc, x_bytes, x_scale, wq_words, wq_scales, wk
         scale_turned(4, slice(0, 1))
         quant_x(1, 2, 2)
         scale_turned(4, slice(1, 2))
-        reorder(7, nc.scalar)
+        reorder(CAST_ON_GPSIMD)
         project("Q", 2, 0)
         project("Q", 2, 1)
         project("K", 3, 0)
@@ -411,13 +402,14 @@ def tile_attentionnet_pa_w4_kernel(tc, x_bytes, x_scale, wq_words, wq_scales, wk
         quant_k(1, 0)
         quant_k(1, 1)
         scale_turned(6)
-        project_half("K", 2, 0, True)
+
+        project_half("K", 2, 0, direct=True)
         score(0)
         quant_q(1)
         row_min(0)
-        project_pair("K", 2, 1, 0, True)
+        project_pair("K", 2, 1, 0, direct=True)
         exps(0)
-        project_pair("K", 2, 1, 1, True)
+        project_pair("K", 2, 1, 1, direct=True)
         quant_x(3, 0, 2)
         score(1)
         scale_turned(7)

@@ -118,16 +118,18 @@ def tile_attentionnet_pa_w4_kernel(tc, x_bytes, x_scale, wq_words, wq_scales, wk
         def word(engine):
             return U32 if engine is nc.scalar else I32
 
-        def permute_w(m, h):
-            nc.vector.tensor_copy(
-                out=wts[m + str(h)][:].bitcast(I32).rearrange("p (t c w) -> p t c w", t=4, w=4),
-                in_=raw[m + str(h)][:].bitcast(I32).rearrange("p (c t w) -> p t c w", t=4, w=4),
+        def permute_w(m, h, engine=nc.vector):
+            move(
+                engine,
+                wts[m + str(h)][:].bitcast(word(engine)).rearrange("p (t c w) -> p t c w", t=4, w=4),
+                raw[m + str(h)][:].bitcast(word(engine)).rearrange("p (c t w) -> p t c w", t=4, w=4),
             )
 
         def permute_s(m, engine):
-            engine.tensor_copy(
-                out=wts_s[m][:].bitcast(I32).rearrange("p (t c w) -> p t c w", t=4, w=2),
-                in_=raw_s[m][:].bitcast(I32).rearrange("p (c t w) -> p t c w", t=4, w=2),
+            move(
+                engine,
+                wts_s[m][:].bitcast(word(engine)).rearrange("p (t c w) -> p t c w", t=4, w=2),
+                raw_s[m][:].bitcast(word(engine)).rearrange("p (c t w) -> p t c w", t=4, w=2),
             )
 
         def quantize(codes, scales, values, first, count):
@@ -141,9 +143,9 @@ def tile_attentionnet_pa_w4_kernel(tc, x_bytes, x_scale, wq_words, wq_scales, wk
         def cast(dst, i):
             nc.scalar.copy(dst[:], xb[i][:].bitcast(FP8))
 
-        def cast_behind(i, done):
-            xv[i] = keep.tile([P, D], BF16, name=done, align_bytes=256)
-            nc.gpsimd.tensor_copy(out=xv[i][:], in_=xb[i][:].bitcast(FP8))
+        def cast_behind(i, done, into=xv):
+            into[i] = keep.tile([P, D], BF16, name=done, align_bytes=256)
+            nc.gpsimd.tensor_copy(out=into[i][:], in_=xb[i][:].bitcast(FP8))
 
         def reorder(i):
             nc.scalar.copy(xw[i][:].bitcast(U32).rearrange("p (u w) -> p u w", u=2), xv[i][:].bitcast(U32).rearrange("p (w u) -> p u w", u=2))
@@ -240,22 +242,33 @@ def tile_attentionnet_pa_w4_kernel(tc, x_bytes, x_scale, wq_words, wq_scales, wk
                 project_pass(m, i, h, g)
             empty(m, i, h, engine)
 
-        def project_pair(m, n, h, u, direct=False):
+        def project_both(m, i, engine=nc.scalar):
+            for h in range(2):
+                for g in range(PASSES):
+                    project_pass(m, i, h, g)
+            empty(m, i, 1)
+            empty(m, i, 0, engine)
+
+        def pair_passes(m, n, h, u):
             bank = take((m, n, h, u))
             for g in range(PASSES):
                 for e in range(2):
                     cols = slice(256 * g, 256 * (g + 1))
                     project_mx(bank, slice(e * 256, (e + 1) * 256), m, h, 2 * u + e, g, n, cols, g == 0 and e == 0, g == PASSES - 1 and e == 1)
+
+        def empty_pair(m, n, h, u, direct):
             if direct:
                 dst = values(m, n, h).rearrange("p (r u e) -> p u r e", u=2, e=2)[:, u]
             else:
                 dst = staged[m + str(n) + str(h)][:, u * 512 : (u + 1) * 512].rearrange("p (r e) -> p r e", e=2)
-            nc.scalar.copy(dst, bank[:].rearrange("p (e r) -> p r e", e=2))
+            nc.scalar.copy(dst, held[m, n, h, u][1][:].rearrange("p (e r) -> p r e", e=2))
             give_back((m, n, h, u))
 
         def project_half(m, n, h, direct=False):
             for u in range(2):
-                project_pair(m, n, h, u, direct)
+                pair_passes(m, n, h, u)
+            for u in (1, 0):
+                empty_pair(m, n, h, u, direct)
 
         def join(m, n, h, engine=nc.vector):
             move(
@@ -264,9 +277,9 @@ def tile_attentionnet_pa_w4_kernel(tc, x_bytes, x_scale, wq_words, wq_scales, wk
                 staged[m + str(n) + str(h)][:].bitcast(word(engine)).rearrange("p (u r) -> p r u", u=2),
             )
 
-        def quant_k(n, h):
-            b = 2 * (n // 2) + h
-            quantize(kc[b], ks[b], yk[b], 2 * (n % 2), 2)
+        def quant_k(i, h, count=2):
+            b = 2 * (i // PER_BATCH) + h
+            quantize(kc[b], ks[b], yk[b], i % PER_BATCH, count)
 
         def quant_q(n, first=0, count=4):
             quantize(qc[n], qs[n], yq[n], first, count)
@@ -295,6 +308,9 @@ def tile_attentionnet_pa_w4_kernel(tc, x_bytes, x_scale, wq_words, wq_scales, wk
 
         def invert(i):
             nc.vector.reciprocal(inv[i], total[i])
+
+        def invert_pair(n):
+            nc.vector.reciprocal(invs[n][:], totals[n][:])
 
         def finish(i, engine=nc.vector):
             if engine is nc.gpsimd:
@@ -353,111 +369,108 @@ def tile_attentionnet_pa_w4_kernel(tc, x_bytes, x_scale, wq_words, wq_scales, wk
             permute_w("K", h)
         scale_pass(1, 1)
         quant_x(0, block(PAIRED_X, 1, 0), 1)
-        permute_s("Q", nc.vector)
         quant_x(0, block(PAIRED_X, 1, 1), 1)
-        cast(xv[CAST_ON_SCALAR], CAST_ON_SCALAR)
+        permute_s("Q", nc.scalar)
 
-        project("K", 0, 0)
-        project("K", 0, 1)
-        reorder(CAST_ON_SCALAR)
+        for h in range(2):
+            for g in range(PASSES):
+                project_pass("K", 0, h, g)
+        permute_w("Q", 0, nc.scalar)
+        empty("K", 0, 1)
+        empty("K", 0, 0)
         for g in range(PASSES):
             for h in range(2):
                 project_pass("K", 1, h, g)
-        for h in range(2):
-            empty("K", 1, h)
-            permute_w("Q", h)
-            scale_turned(2, slice(h, h + 1))
+        widen(3)
+        empty("K", 1, 1)
+        empty("K", 1, 0)
+        scale_turned(2, slice(0, 1))
+        permute_w("Q", 1)
+        scale_turned(2, slice(1, 2))
         for h in range(2):
             project_half("Q", 0, h)
-        widen(4)
-        quant_x(1, 0, 2)
         widen(5)
+        quant_x(1, 0, 2)
+        widen(4)
         widen(6)
         turn(3)
         cast_behind(CAST_ON_GPSIMD, "xw_3")
-        turn(4)
         turn(5)
+        turn(4)
         scale_turned(3)
         join("Q", 0, 0, nc.scalar)
-        project("K", 2, 0)
-        project("K", 2, 1)
+        join("Q", 0, 1, nc.scalar)
+        project_both("K", 2)
         scale_turned(4, slice(0, 1))
         quant_x(1, 2, 2)
         scale_turned(4, slice(1, 2))
         reorder(CAST_ON_GPSIMD)
-        project("Q", 2, 0)
-        project("Q", 2, 1)
-        project("K", 3, 0)
-        project("K", 3, 1)
-        for h in range(2):
-            quant_k(0, h)
+        project_both("Q", 2)
+        quant_q(0)
+        project_both("K", 3)
         scale_turned(5)
+        quant_k(0, 0)
+        quant_k(0, 1)
         turn(6)
         turn(7)
-        join("Q", 0, 1)
-        project("Q", 3, 0)
-        project("Q", 3, 1)
+        project_both("Q", 3)
         quant_x(2)
-        quant_q(0)
-        quant_k(1, 0)
-        quant_k(1, 1)
         scale_turned(6)
+        quant_k(2, 0)
+        quant_k(2, 1)
 
         project_half("K", 2, 0, direct=True)
         score(0)
+        quant_x(3, 0, 2)
         quant_q(1)
         row_min(0)
-        project_pair("K", 2, 1, 0, direct=True)
         exps(0)
-        project_pair("K", 2, 1, 1, direct=True)
-        quant_x(3, 0, 2)
+        project_half("K", 2, 1, direct=True)
         score(1)
         scale_turned(7)
         row_min(1)
         quant_x(3, 2, 2)
-        invert(0)
-        finish(0, nc.gpsimd)
         score(2)
-        project("K", 6, 0)
         exps(1)
-        project("K", 6, 1)
+        for h in range(2):
+            for g in range(PASSES):
+                project_pass("K", 6, h, g)
+        empty("K", 6, 1)
         row_min(2)
-        score(3)
         exps(2)
+        empty("K", 6, 0)
+        quant_k(4, 0)
+        quant_k(4, 1)
+        invert_pair(0)
+        finish(0, nc.gpsimd)
+        finish(1, nc.gpsimd)
+        score(3)
         row_min(3)
-        quant_k(2, 0)
-        invert(1)
-        quant_k(2, 1)
-        finish(1)
-        project("K", 7, 0)
-        project("K", 7, 1)
-
+        project_both("K", 7, nc.vector)
         project("Q", 4, 0, nc.vector)
         project("Q", 4, 1)
+        quant_k(6, 0)
+        quant_k(6, 1)
+        quant_q(2, 0, 2)
         exps(3)
-        quant_k(3, 0)
-        quant_k(3, 1)
-        quant_q(2, 0, 1)
-        project("Q", 5, 0)
-        quant_q(2, 1, 1)
-        invert(2)
+        project("Q", 5, 0, nc.vector)
         project("Q", 5, 1)
-        score(4)
-        finish(2)
+        invert_pair(1)
         project("Q", 6, 0)
-        row_min(4)
-        exps(4)
-        invert(3)
+        score(4)
         quant_q(2, 2, 2)
-        finish(3)
-        project("Q", 6, 1, nc.vector)
+        row_min(4)
+        project("Q", 6, 1)
+        exps(4)
         project("Q", 7, 0)
         score(5)
         project("Q", 7, 1)
-        invert(4)
+        finish(2)
+        finish(3)
         quant_q(3, 0, 2)
         row_min(5)
         exps(5)
+        invert(4)
         quant_q(3, 2, 1)
         finish(4)
         quant_q(3, 3, 1)

@@ -313,7 +313,9 @@ def tile_attentionnet_pa_w4_kernel(tc, x_bytes, x_scale, wq_words, wq_scales, wk
             nc.vector.reciprocal(invs[n][:], totals[n][:])
 
         def finish(i, engine=nc.vector):
-            if engine is nc.gpsimd:
+            if engine is nc.scalar:
+                nc.scalar.activation(out=res[i][:], in_=ex[i][:], func=ACT.Copy, scale=inv[i])
+            elif engine is nc.gpsimd:
                 nc.gpsimd.tensor_scalar(out=res[i][:], in0=ex[i][:], scalar1=inv[i], scalar2=1.0, op0=ALU.mult, op1=ALU.mult)
             else:
                 nc.vector.tensor_scalar(out=res[i][:], in0=ex[i][:], scalar1=inv[i], scalar2=None, op0=ALU.mult)
@@ -410,26 +412,26 @@ def tile_attentionnet_pa_w4_kernel(tc, x_bytes, x_scale, wq_words, wq_scales, wk
         project_both("K", 3)
         scale_turned(5)
         quant_k(0, 0)
-        quant_k(0, 1)
         turn(6)
         turn(7)
         project_both("Q", 3)
         quant_x(2)
-        scale_turned(6)
+        quant_k(0, 1)
         quant_k(2, 0)
         quant_k(2, 1)
+        scale_turned(6)
 
         project_half("K", 2, 0, direct=True)
         score(0)
-        quant_x(3, 0, 2)
         quant_q(1)
+        quant_x(3, 0, 2)
+        scale_turned(7)
+        project_half("K", 2, 1, direct=True)
         row_min(0)
         exps(0)
-        project_half("K", 2, 1, direct=True)
         score(1)
-        scale_turned(7)
-        row_min(1)
         quant_x(3, 2, 2)
+        row_min(1)
         score(2)
         exps(1)
         for h in range(2):
@@ -443,7 +445,6 @@ def tile_attentionnet_pa_w4_kernel(tc, x_bytes, x_scale, wq_words, wq_scales, wk
         quant_k(4, 1)
         invert_pair(0)
         finish(0, nc.gpsimd)
-        finish(1, nc.gpsimd)
         score(3)
         row_min(3)
         project_both("K", 7, nc.vector)
@@ -456,6 +457,7 @@ def tile_attentionnet_pa_w4_kernel(tc, x_bytes, x_scale, wq_words, wq_scales, wk
         project("Q", 5, 0, nc.vector)
         project("Q", 5, 1)
         invert_pair(1)
+        finish(1)
         project("Q", 6, 0)
         score(4)
         quant_q(2, 2, 2)

@@ -28,7 +28,7 @@ SPLIT = 320
 CAST_ON_SCALAR = 3
 CAST_ON_GPSIMD = 7
 PAIRED_X = (0, 2)
-PAIRED_Q = (0,)
+PAIRED_Q = (0, 2)
 
 
 def tile_attentionnet_pa_w4_kernel(tc, x_bytes, x_scale, wq_words, wq_scales, wk_words, wk_scales, out):
@@ -72,7 +72,7 @@ def tile_attentionnet_pa_w4_kernel(tc, x_bytes, x_scale, wq_words, wq_scales, wk
         xg = tiles("xg", pairs, [P, 2 * D], BF16)
         xc = tiles("xc", pairs, [P, 512], U32)
         xs = tiles("xs", pairs, [P, 512], U8)
-        staged = tiles("staged", ("Q00", "Q01"), [P, D], BF16)
+        staged = tiles("staged", ("Q00", "Q01", "Q20", "Q21"), [P, D], BF16)
         yk = tiles("yk", range(2 * B), [P, 4 * S], BF16)
         kc = tiles("kc", range(2 * B), [P, S], U32)
         ks = tiles("ks", range(2 * B), [P, S], U8)
@@ -256,12 +256,12 @@ def tile_attentionnet_pa_w4_kernel(tc, x_bytes, x_scale, wq_words, wq_scales, wk
                     cols = slice(256 * g, 256 * (g + 1))
                     project_mx(bank, slice(e * 256, (e + 1) * 256), m, h, 2 * u + e, g, n, cols, g == 0 and e == 0, g == PASSES - 1 and e == 1)
 
-        def empty_pair(m, n, h, u, direct):
+        def empty_pair(m, n, h, u, direct, engine=nc.scalar):
             if direct:
                 dst = values(m, n, h).rearrange("p (r u e) -> p u r e", u=2, e=2)[:, u]
             else:
                 dst = staged[m + str(n) + str(h)][:, u * 512 : (u + 1) * 512].rearrange("p (r e) -> p r e", e=2)
-            nc.scalar.copy(dst, held[m, n, h, u][1][:].rearrange("p (e r) -> p r e", e=2))
+            move(engine, dst, held[m, n, h, u][1][:].rearrange("p (e r) -> p r e", e=2))
             give_back((m, n, h, u))
 
         def project_half(m, n, h, direct=False):
@@ -308,9 +308,6 @@ def tile_attentionnet_pa_w4_kernel(tc, x_bytes, x_scale, wq_words, wq_scales, wk
 
         def invert(i):
             nc.vector.reciprocal(inv[i], total[i])
-
-        def invert_pair(n):
-            nc.vector.reciprocal(invs[n][:], totals[n][:])
 
         def finish(i, engine=nc.vector):
             if engine is nc.scalar:
@@ -424,60 +421,64 @@ def tile_attentionnet_pa_w4_kernel(tc, x_bytes, x_scale, wq_words, wq_scales, wk
         project_half("K", 2, 0, direct=True)
         score(0)
         quant_q(1)
+        row_min(0)
         quant_x(3, 0, 2)
         scale_turned(7)
         project_half("K", 2, 1, direct=True)
-        row_min(0)
         exps(0)
         score(1)
-        quant_x(3, 2, 2)
         row_min(1)
-        score(2)
-        exps(1)
-        for h in range(2):
-            for g in range(PASSES):
-                project_pass("K", 6, h, g)
-        empty("K", 6, 1)
-        row_min(2)
-        exps(2)
-        empty("K", 6, 0)
+        quant_x(3, 2, 2)
         quant_k(4, 0)
-        quant_k(4, 1)
-        invert_pair(0)
+        invert(0)
         finish(0, nc.gpsimd)
+        project_half("Q", 2, 0)
+        exps(1)
+        score(2)
+        row_min(2)
+        for u in range(2):
+            pair_passes("Q", 2, 1, u)
+        empty_pair("Q", 2, 1, 0, False, nc.vector)
+        empty_pair("Q", 2, 1, 1, False)
         score(3)
         row_min(3)
-        project_both("K", 7, nc.vector)
-        project("Q", 4, 0, nc.vector)
-        project("Q", 4, 1)
-        quant_k(6, 0)
-        quant_k(6, 1)
-        quant_q(2, 0, 2)
-        exps(3)
-        project("Q", 5, 0, nc.vector)
-        project("Q", 5, 1)
-        invert_pair(1)
+        project("K", 6, 0)
+        project("K", 6, 1)
+        quant_k(4, 1)
+        join("Q", 2, 0)
+        join("Q", 2, 1)
+        invert(1)
+        quant_k(6, 0, 1)
+        quant_q(2)
         finish(1)
-        project("Q", 6, 0)
-        score(4)
-        quant_q(2, 2, 2)
-        row_min(4)
+        project("K", 7, 0)
+        project("K", 7, 1)
+        quant_k(6, 1, 1)
+        quant_k(7, 0, 1)
+        quant_k(7, 1, 1)
+        exps(2)
+        exps(3)
+        project("Q", 6, 0, nc.vector)
         project("Q", 6, 1)
-        exps(4)
+        invert(2)
+        finish(2, nc.gpsimd)
+        score(4)
+        row_min(4)
+        invert(3)
+        quant_q(3, 0, 2)
+        finish(3)
         project("Q", 7, 0)
+        exps(4)
         score(5)
         project("Q", 7, 1)
-        finish(2)
-        finish(3)
-        quant_q(3, 0, 2)
         row_min(5)
         exps(5)
-        invert(4)
         quant_q(3, 2, 1)
-        finish(4)
+        invert(4)
         quant_q(3, 3, 1)
         score(6)
         score(7)
+        finish(4, nc.scalar)
         row_min(6)
         invert(5)
         row_min(7)

@@ -140,8 +140,8 @@ def tile_attentionnet_pa_w4_kernel(tc, x_bytes, x_scale, wq_words, wq_scales, wk
             for _ in range(count):
                 nc.tensor.matmul(idle[:], zeros[:, 0:P], zeros[:], start=True, stop=True)
 
-        def cast(dst, i):
-            nc.scalar.copy(dst[:], xb[i][:].bitcast(FP8))
+        def cast(dst, i, cols=slice(0, D)):
+            nc.scalar.copy(dst[:, cols], xb[i][:, cols].bitcast(FP8))
 
         def cast_behind(i, done, into=xv):
             into[i] = keep.tile([P, D], BF16, name=done, align_bytes=256)
@@ -177,11 +177,11 @@ def tile_attentionnet_pa_w4_kernel(tc, x_bytes, x_scale, wq_words, wq_scales, wk
             if part.stop == PASSES:
                 give_back(("x", i))
 
-        def turn_pass(i, g):
+        def turn_pass(i, g, stepped=False):
             bank = take(("pass", i, g))
             words = xw[i][:, g * 512 : (g + 1) * 512].bitcast(F32)
             for u in range(2):
-                nc.tensor.transpose(bank[:, u * P : (u + 1) * P], words[:, u * P : (u + 1) * P], ident[:])
+                nc.tensor.transpose(bank[:, u * P : (u + 1) * P], words[:, u:256:2] if stepped else words[:, u * P : (u + 1) * P], ident[:])
 
         def scale_slots(i, g):
             first = block(PAIRED_X, i, g) * 512
@@ -447,10 +447,8 @@ def tile_attentionnet_pa_w4_kernel(tc, x_bytes, x_scale, wq_words, wq_scales, wk
         quant_k(4, 1)
         join("Q", 2, 0)
         join("Q", 2, 1)
-        invert(1)
         quant_k(6, 0, 1)
         quant_q(2)
-        finish(1)
         project("K", 7, 0)
         project("K", 7, 1)
         quant_k(6, 1, 1)
@@ -460,7 +458,9 @@ def tile_attentionnet_pa_w4_kernel(tc, x_bytes, x_scale, wq_words, wq_scales, wk
         exps(3)
         project("Q", 6, 0, nc.vector)
         project("Q", 6, 1)
+        invert(1)
         invert(2)
+        finish(1)
         finish(2, nc.gpsimd)
         score(4)
         row_min(4)

@@ -94,11 +94,8 @@ def tile_attentionnet_pa_w4_kernel(tc, x_bytes, x_scale, wq_words, wq_scales, wk
         def load_x(i):
             nc.sync.dma_start(out=xb[i][:], in_=x_rows[i * P : (i + 1) * P, :])
 
-        def load_w(m, h):
-            nc.sync.dma_start(
-                out=raw[m + str(h)][:].bitcast(I32).rearrange("p (g n) -> p g n", g=PASSES),
-                in_=hbm_w[m].bitcast(I32)[:, :, h * 256 : (h + 1) * 256].rearrange("g p n -> p g n"),
-            )
+        def load_w(m, g):
+            nc.sync.dma_start(out=raw[m + str(g)][:].bitcast(I32), in_=hbm_w[m].bitcast(I32)[g])
 
         def load_s(m):
             dst = raw_s[m][:].bitcast(I32).rearrange("p (g n) -> p g n", g=PASSES)
@@ -118,11 +115,11 @@ def tile_attentionnet_pa_w4_kernel(tc, x_bytes, x_scale, wq_words, wq_scales, wk
         def word(engine):
             return U32 if engine is nc.scalar else I32
 
-        def permute_w(m, h, engine=nc.vector):
+        def permute_w(m, g, engine=nc.vector):
             move(
                 engine,
-                wts[m + str(h)][:].bitcast(word(engine)).rearrange("p (t c w) -> p t c w", t=4, w=4),
-                raw[m + str(h)][:].bitcast(word(engine)).rearrange("p (c t w) -> p t c w", t=4, w=4),
+                wts[m + str(g)][:].bitcast(word(engine)).rearrange("p (t c w) -> p t c w", t=4, w=4),
+                raw[m + str(g)][:].bitcast(word(engine)).rearrange("p (c t w) -> p t c w", t=4, w=4),
             )
 
         def permute_s(m, engine):
@@ -209,7 +206,7 @@ def tile_attentionnet_pa_w4_kernel(tc, x_bytes, x_scale, wq_words, wq_scales, wk
             plane = (4 * t + 2 * g + h) * P
             nc.tensor.matmul_mx(
                 out=bank[:, out_cols],
-                lhsT=wts[m + str(h)][:, t * 512 + g * 256 : t * 512 + (g + 1) * 256].bitcast(FP4X4),
+                lhsT=wts[m + str(g)][:, t * 512 + h * 256 : t * 512 + (h + 1) * 256].bitcast(FP4X4),
                 lhsT_scale=wts_s[m][:, plane : plane + P],
                 rhs=xc[n][:, cols].bitcast(FP8X4),
                 rhs_scale=xs[n][:, cols],
@@ -329,10 +326,10 @@ def tile_attentionnet_pa_w4_kernel(tc, x_bytes, x_scale, wq_words, wq_scales, wk
 
         ctx.enter_context(tc.manual_schedule())
 
+        nc.vector.memset(zeros[:].bitcast(I32), 0)
         nc.vector.memset(raw_s["K"][:].bitcast(I32), 0)
         nc.vector.memset(ident[:], 0.0)
         make_identity(nc, ident[:], nomemset=True)
-        nc.vector.memset(zeros[:], 0.0)
         nc.vector.memset(raw_s["Q"][:].bitcast(I32), 0)
 
         load_x(0)
@@ -350,12 +347,15 @@ def tile_attentionnet_pa_w4_kernel(tc, x_bytes, x_scale, wq_words, wq_scales, wk
             load_x(i)
 
         nc.scalar.activation(out=ones[:], in_=zeros[:, 0:1], func=ACT.Exp)
-        warm_up(3)
-        for i in range(2):
-            for g in range(PASSES):
-                widen(i, slice(g * 512, (g + 1) * 512))
-                turn_pass(i, g)
-            warm_up(1 + i)
+        warm_up(4)
+        for g in range(PASSES):
+            widen(0, slice(g * 512, (g + 1) * 512))
+            turn_pass(0, g)
+        widen(1, slice(0, 512))
+        turn_pass(1, 0)
+        cast(xw[1], 1, slice(512, D))
+        turn_pass(1, 1, stepped=True)
+        warm_up(2)
         cast(xw[2], 2)
         turn(2, stepped=True)
         give_back("idle")
@@ -371,8 +371,8 @@ def tile_attentionnet_pa_w4_kernel(tc, x_bytes, x_scale, wq_words, wq_scales, wk
         quant_x(0, block(PAIRED_X, 1, 1), 1)
         permute_s("Q", nc.scalar)
 
-        for h in range(2):
-            for g in range(PASSES):
+        for g in range(PASSES):
+            for h in range(2):
                 project_pass("K", 0, h, g)
         permute_w("Q", 0, nc.scalar)
         empty("K", 0, 1)
@@ -383,9 +383,8 @@ def tile_attentionnet_pa_w4_kernel(tc, x_bytes, x_scale, wq_words, wq_scales, wk
         widen(3)
         empty("K", 1, 1)
         empty("K", 1, 0)
-        scale_turned(2, slice(0, 1))
         permute_w("Q", 1)
-        scale_turned(2, slice(1, 2))
+        scale_turned(2)
         for h in range(2):
             project_half("Q", 0, h)
         widen(5)

import math
from contextlib import ExitStack

import concourse.mybir as mybir
from concourse.masks import make_identity

F32 = mybir.dt.float32
BF16 = mybir.dt.bfloat16
I32 = mybir.dt.int32
U32 = mybir.dt.uint32
U8 = mybir.dt.uint8
FP8 = mybir.dt.float8_e4m3fn
FP8X4 = mybir.dt.float8_e4m3fn_x4
FP4X4 = mybir.dt.float4_e2m1fn_x4
ACT = mybir.ActivationFunctionType
ALU = mybir.AluOpType

B, S, D = 2, 512, 1024
P = 128
TILES = B * S // P
PER_BATCH = S // P
PAIRS = TILES // 2
PASSES = D // 512
INV = 1.0 / math.sqrt(128.0)
FLOPS = 2 * 2 * B * S * D * D + 2 * B * S * S * D
BANKS = 8
SPLIT = 320
CAST_ON_SCALAR = 3
CAST_ON_GPSIMD = 7
PAIRED_X = (0, 2)
PAIRED_Q = (0, 2)


def tile_attentionnet_pa_w4_kernel(tc, x_bytes, x_scale, wq_words, wq_scales, wk_words, wk_scales, out):
    nc = tc.nc
    x_rows = x_bytes.rearrange("b s d -> (b s) d")
    out_rows = out.rearrange("b s t -> (b s) t")

    with ExitStack() as ctx:
        keep = ctx.enter_context(tc.tile_pool(name="keep", bufs=1))
        banks = ctx.enter_context(tc.psum_pool(name="banks", bufs=1))

        free = list(range(BANKS))
        held = {}

        def take(key):
            number = free.pop(0)
            held[key] = (number, banks.tile([P, 512], F32, name="bank%d" % number))
            return held[key][1]

        def give_back(key):
            free.append(held[key][0])

        def tiles(name, keys, shape, dtype):
            return {k: keep.tile(shape, dtype, name="%s_%s" % (name, k), align_bytes=256) for k in keys}

        idle = take("idle")
        every = range(TILES)
        pairs = range(PAIRS)
        halves = ["K0", "K1", "Q0", "Q1"]
        zeros = keep.tile([P, 512], BF16, name="zeros")
        ident = keep.tile([P, P], F32, name="ident")
        scale_k = keep.tile([P, PASSES * 4], F32, name="scale_k")
        ones = keep.tile([P, 1], F32, name="ones")
        xb = tiles("xb", every, [P, D], U8)
        raw = tiles("raw", halves, [P, 2048], U8)
        raw_s = tiles("raw_s", "KQ", [P, 2048], U8)
        wts = tiles("wts", halves, [P, 2048], U8)
        wts_s = tiles("wts_s", "KQ", [P, 2048], U8)
        xw = tiles("xw", every, [P, D], BF16)
        xv = tiles("xv", (CAST_ON_SCALAR,), [P, D], BF16)
        xg = tiles("xg", pairs, [P, 2 * D], BF16)
        xc = tiles("xc", pairs, [P, 512], U32)
        xs = tiles("xs", pairs, [P, 512], U8)
        staged = tiles("staged", ("Q00", "Q01", "Q20", "Q21"), [P, D], BF16)
        yk = tiles("yk", range(2 * B), [P, 4 * S], BF16)
        kc = tiles("kc", range(2 * B), [P, S], U32)
        ks = tiles("ks", range(2 * B), [P, S], U8)
        yq = tiles("yq", pairs, [P, 2 * D], BF16)
        qc = tiles("qc", pairs, [P, 512], U32)
        qs = tiles("qs", pairs, [P, 512], U8)
        neg = tiles("neg", every, [P, S], F32)
        low = tiles("low", every, [P, 1], F32)
        ex = tiles("ex", every, [P, S], F32)
        totals = tiles("total", pairs, [P, 2], F32)
        invs = tiles("inv", pairs, [P, 2], F32)
        total = {i: totals[i // 2][:, i % 2 : i % 2 + 1] for i in every}
        inv = {i: invs[i // 2][:, i % 2 : i % 2 + 1] for i in every}
        res = neg

        hbm_w = {"K": wk_words, "Q": wq_words}
        hbm_s = {"K": wk_scales, "Q": wq_scales}

        def load_x(i):
            nc.sync.dma_start(out=xb[i][:], in_=x_rows[i * P : (i + 1) * P, :])

        def load_w(m, g):
            nc.sync.dma_start(out=raw[m + str(g)][:].bitcast(I32), in_=hbm_w[m].bitcast(I32)[g])

        def load_s(m):
            dst = raw_s[m][:].bitcast(I32).rearrange("p (g n) -> p g n", g=PASSES)
            src = hbm_s[m].bitcast(I32)
            for r in range(4):
                nc.sync.dma_start(out=dst[r:P:32], in_=src[:, r:16:4, :].rearrange("g q n -> q g n"))

        def block(paired, i, part):
            return 2 * part + i % 2 if i // 2 in paired else 2 * (i % 2) + part

        def move(engine, dst, src):
            if engine is nc.scalar:
                nc.scalar.copy(dst, src)
            else:
                engine.tensor_copy(out=dst, in_=src)

        def word(engine):
            return U32 if engine is nc.scalar else I32

        def permute_w(m, g, engine=nc.vector):
            move(
                engine,
                wts[m + str(g)][:].bitcast(word(engine)).rearrange("p (t c w) -> p t c w", t=4, w=4),
                raw[m + str(g)][:].bitcast(word(engine)).rearrange("p (c t w) -> p t c w", t=4, w=4),
            )

        def permute_s(m, engine):
            move(
                engine,
                wts_s[m][:].bitcast(word(engine)).rearrange("p (t c w) -> p t c w", t=4, w=2),
                raw_s[m][:].bitcast(word(engine)).rearrange("p (c t w) -> p t c w", t=4, w=2),
            )

        def quantize(codes, scales, values, first, count):
            cols = slice(first * P, (first + count) * P)
            nc.vector.quantize_mx(out=codes[:, cols].bitcast(FP8X4), scales=scales[:, cols], in_=values[:, first * 512 : (first + count) * 512])

        def warm_up(count):
            for _ in range(count):
                nc.tensor.matmul(idle[:], zeros[:, 0:P], zeros[:], start=True, stop=True)

        def cast(dst, i, cols=slice(0, D)):
            nc.scalar.copy(dst[:, cols], xb[i][:, cols].bitcast(FP8))

        def cast_behind(i, done, into=xv):
            into[i] = keep.tile([P, D], BF16, name=done, align_bytes=256)
            nc.gpsimd.tensor_copy(out=into[i][:], in_=xb[i][:].bitcast(FP8))

        def reorder(i):
            nc.scalar.copy(xw[i][:].bitcast(U32).rearrange("p (u w) -> p u w", u=2), xv[i][:].bitcast(U32).rearrange("p (w u) -> p u w", u=2))

        def widen(i, cols=slice(0, D)):
            nc.vector.tensor_scalar(
                out=xw[i][:, cols].rearrange("p (u w e) -> p w u e", u=2, e=2),
                in0=xb[i][:, cols].bitcast(FP8).rearrange("p (w u e) -> p w u e", u=2, e=2),
                scalar1=ones[:],
                scalar2=None,
                op0=ALU.mult,
            )

        def turn(i, stepped=False):
            bank = take(("x", i))
            words = xw[i][:].bitcast(F32)
            for g in range(PASSES):
                for u in range(2):
                    src = words[:, 256 * g + u : 256 * (g + 1) : 2] if stepped else words[:, u * 256 + g * P : u * 256 + (g + 1) * P]
                    nc.tensor.transpose(bank[:, u * 256 + g * P : u * 256 + (g + 1) * P], src, ident[:])

        def scale_turned(i, part=slice(0, PASSES)):
            nc.vector.tensor_tensor(
                out=xg[i // 2][:].rearrange("p (%s r u e) -> p j g r u e" % ("g j" if i // 2 in PAIRED_X else "j g"), g=PASSES, j=2, u=2, e=2)[:, i % 2, part],
                in0=held["x", i][1][:].bitcast(BF16).rearrange("p (u g r e) -> p g r u e", g=PASSES, u=2, e=2)[:, part],
                in1=scale_k[:].rearrange("p (g u e) -> p g u e", u=2, e=2).unsqueeze(2).to_broadcast([P, PASSES, P, 2, 2])[:, part],
                op=ALU.mult,
            )
            if part.stop == PASSES:
                give_back(("x", i))

        def turn_pass(i, g, stepped=False):
            bank = take(("pass", i, g))
            words = xw[i][:, g * 512 : (g + 1) * 512].bitcast(F32)
            for u in range(2):
                nc.tensor.transpose(bank[:, u * P : (u + 1) * P], words[:, u:256:2] if stepped else words[:, u * P : (u + 1) * P], ident[:])

        def scale_slots(i, g):
            first = block(PAIRED_X, i, g) * 512
            src = held["pass", i, g][1][:, 0:256].bitcast(BF16).rearrange("p (u r e) -> p u e r", u=2, e=2)
            dst = xg[i // 2][:, first : first + 512].rearrange("p (r u e) -> p u e r", u=2, e=2)
            for t in range(4):
                u, e = divmod(t, 2)
                nc.scalar.activation(out=dst[:, u, e], in_=src[:, u, e], func=ACT.Copy, scale=scale_k[:, 4 * g + t : 4 * g + t + 1])
            give_back(("pass", i, g))

        def scale_pass(i, g):
            first = block(PAIRED_X, i, g) * 512
            nc.vector.tensor_tensor(
                out=xg[i // 2][:, first : first + 512].rearrange("p (r u e) -> p r u e", u=2, e=2),
                in0=held["pass", i, g][1][:, 0:256].bitcast(BF16).rearrange("p (u r e) -> p r u e", u=2, e=2),
                in1=scale_k[:, g * 4 : (g + 1) * 4].rearrange("p (u e) -> p u e", e=2).unsqueeze(1).to_broadcast([P, P, 2, 2]),
                op=ALU.mult,
            )
            give_back(("pass", i, g))

        def quant_x(n, first=0, count=4):
            quantize(xc[n], xs[n], xg[n], first, count)

        def project_mx(bank, out_cols, m, h, t, g, n, cols, start, stop):
            plane = (4 * t + 2 * g + h) * P
            nc.tensor.matmul_mx(
                out=bank[:, out_cols],
                lhsT=wts[m + str(g)][:, t * 512 + h * 256 : t * 512 + (h + 1) * 256].bitcast(FP4X4),
                lhsT_scale=wts_s[m][:, plane : plane + P],
                rhs=xc[n][:, cols].bitcast(FP8X4),
                rhs_scale=xs[n][:, cols],
                start=start,
                stop=stop,
            )

        def values(m, n, h):
            if m == "K":
                return yk[2 * (n // 2) + h][:, (n % 2) * D : (n % 2 + 1) * D]
            return yq[n][:, h * D : (h + 1) * D]

        def project_pass(m, i, h, g):
            bank = take((m, i, h)) if g == 0 else held[m, i, h][1]
            n = i // 2
            cols = slice(block(PAIRED_X, i, g) * P, (block(PAIRED_X, i, g) + 1) * P)
            for t in range(4):
                project_mx(bank, slice(t * P, (t + 1) * P), m, h, t, g, n, cols, g == 0 and t == 0, g == PASSES - 1 and t == 3)

        def empty(m, i, h, engine=nc.scalar):
            if m == "K":
                dst = values(m, i // 2, h)[:, (i % 2) * 512 : (i % 2 + 1) * 512]
            else:
                dst = yq[i // 2][:, block(PAIRED_Q, i, h) * 512 : (block(PAIRED_Q, i, h) + 1) * 512]
            move(engine, dst.rearrange("p (r t) -> p r t", t=4), held[m, i, h][1][:].rearrange("p (t r) -> p r t", t=4))
            give_back((m, i, h))

        def project(m, i, h, engine=nc.scalar):
            for g in range(PASSES):
                project_pass(m, i, h, g)
            empty(m, i, h, engine)

        def project_both(m, i, engine=nc.scalar):
            for h in range(2):
                for g in range(PASSES):
                    project_pass(m, i, h, g)
            empty(m, i, 1)
            empty(m, i, 0, engine)

        def pair_passes(m, n, h, u):
            bank = take((m, n, h, u))
            for g in range(PASSES):
                for e in range(2):
                    cols = slice(256 * g, 256 * (g + 1))
                    project_mx(bank, slice(e * 256, (e + 1) * 256), m, h, 2 * u + e, g, n, cols, g == 0 and e == 0, g == PASSES - 1 and e == 1)

        def empty_pair(m, n, h, u, direct, engine=nc.scalar):
            if direct:
                dst = values(m, n, h).rearrange("p (r u e) -> p u r e", u=2, e=2)[:, u]
            else:
                dst = staged[m + str(n) + str(h)][:, u * 512 : (u + 1) * 512].rearrange("p (r e) -> p r e", e=2)
            move(engine, dst, held[m, n, h, u][1][:].rearrange("p (e r) -> p r e", e=2))
            give_back((m, n, h, u))

        def project_half(m, n, h, direct=False):
            for u in range(2):
                pair_passes(m, n, h, u)
            for u in (1, 0):
                empty_pair(m, n, h, u, direct)

        def join(m, n, h, engine=nc.vector):
            move(
                engine,
                values(m, n, h).bitcast(word(engine)).rearrange("p (r u) -> p r u", u=2),
                staged[m + str(n) + str(h)][:].bitcast(word(engine)).rearrange("p (u r) -> p r u", u=2),
            )

        def quant_k(i, h, count=2):
            b = 2 * (i // PER_BATCH) + h
            quantize(kc[b], ks[b], yk[b], i % PER_BATCH, count)

        def quant_q(n, first=0, count=4):
            quantize(qc[n], qs[n], yq[n], first, count)

        def score(i):
            b = i // PER_BATCH
            bank = take(("s", i))
            for h in range(2):
                cols = slice(block(PAIRED_Q, i, h) * P, (block(PAIRED_Q, i, h) + 1) * P)
                nc.tensor.matmul_mx(
                    out=bank[:],
                    lhsT=qc[i // 2][:, cols].bitcast(FP8X4),
                    lhsT_scale=qs[i // 2][:, cols],
                    rhs=kc[2 * b + h][:].bitcast(FP8X4),
                    rhs_scale=ks[2 * b + h][:],
                    start=(h == 0),
                    stop=(h == 1),
                )

        def row_min(i):
            nc.vector.tensor_scalar(out=neg[i][:], in0=held["s", i][1][:], scalar1=-INV, scalar2=None, op0=ALU.mult, op1=ALU.min, accum_out=low[i][:])
            give_back(("s", i))

        def exps(i):
            nc.scalar.activation(out=ex[i][:], in_=neg[i][:], func=ACT.Exp, bias=low[i][:], scale=-1.0, accum_out=total[i])

        def invert(i):
            nc.vector.reciprocal(inv[i], total[i])

        def finish(i, engine=nc.vector):
            if engine is nc.scalar:
                nc.scalar.activation(out=res[i][:], in_=ex[i][:], func=ACT.Copy, scale=inv[i])
            elif engine is nc.gpsimd:
                nc.gpsimd.tensor_scalar(out=res[i][:], in0=ex[i][:], scalar1=inv[i], scalar2=1.0, op0=ALU.mult, op1=ALU.mult)
            else:
                nc.vector.tensor_scalar(out=res[i][:], in0=ex[i][:], scalar1=inv[i], scalar2=None, op0=ALU.mult)
            nc.sync.dma_start(out=out_rows[i * P : (i + 1) * P, :], in_=res[i][:])

        def finish_last():
            i = TILES - 1
            rows = slice(i * P, (i + 1) * P)
            left, right = slice(0, SPLIT), slice(SPLIT, S)
            nc.vector.tensor_scalar(out=res[i][:, left], in0=ex[i][:, left], scalar1=inv[i], scalar2=None, op0=ALU.mult)
            nc.scalar.activation(out=res[i][:, right], in_=ex[i][:, right], func=ACT.Copy, scale=inv[i])
            nc.sync.dma_start(out=out_rows[rows, left], in_=res[i][:, left])
            nc.scalar.dma_start(out=out_rows[rows, right], in_=res[i][:, right])

        ctx.enter_context(tc.manual_schedule())

        nc.vector.memset(zeros[:].bitcast(I32), 0)
        nc.vector.memset(raw_s["K"][:].bitcast(I32), 0)
        nc.vector.memset(ident[:], 0.0)
        make_identity(nc, ident[:], nomemset=True)
        nc.vector.memset(raw_s["Q"][:].bitcast(I32), 0)

        load_x(0)
        nc.scalar.dma_start(out=scale_k[:].rearrange("p (g t) -> p g t", t=4), in_=x_scale.rearrange("a b (g p t) -> p (a b g) t", p=P, t=4))
        load_x(1)
        load_x(2)
        load_s("K")
        for h in range(2):
            load_w("K", h)
        load_x(3)
        load_s("Q")
        for h in range(2):
            load_w("Q", h)
        for i in range(4, TILES):
            load_x(i)

        nc.scalar.activation(out=ones[:], in_=zeros[:, 0:1], func=ACT.Exp)
        warm_up(4)
        for g in range(PASSES):
            widen(0, slice(g * 512, (g + 1) * 512))
            turn_pass(0, g)
        widen(1, slice(0, 512))
        turn_pass(1, 0)
        cast(xw[1], 1, slice(512, D))
        turn_pass(1, 1, stepped=True)
        warm_up(2)
        cast(xw[2], 2)
        turn(2, stepped=True)
        give_back("idle")
        for g in range(PASSES):
            scale_pass(0, g)
        permute_s("K", nc.gpsimd)
        scale_slots(1, 0)
        for h in range(2):
            quant_x(0, block(PAIRED_X, 0, h), 1)
            permute_w("K", h)
        scale_pass(1, 1)
        quant_x(0, block(PAIRED_X, 1, 0), 1)
        quant_x(0, block(PAIRED_X, 1, 1), 1)
        permute_s("Q", nc.scalar)

        for g in range(PASSES):
            for h in range(2):
                project_pass("K", 0, h, g)
        permute_w("Q", 0, nc.scalar)
        empty("K", 0, 1)
        empty("K", 0, 0)
        for g in range(PASSES):
            for h in range(2):
                project_pass("K", 1, h, g)
        widen(3)
        empty("K", 1, 1)
        empty("K", 1, 0)
        permute_w("Q", 1)
        scale_turned(2)
        for h in range(2):
            project_half("Q", 0, h)
        widen(5)
        quant_x(1, 0, 2)
        widen(4)
        widen(6)
        turn(3)
        cast_behind(CAST_ON_GPSIMD, "xw_3")
        turn(5)
        turn(4)
        scale_turned(3)
        join("Q", 0, 0, nc.scalar)
        join("Q", 0, 1, nc.scalar)
        project_both("K", 2)
        scale_turned(4, slice(0, 1))
        quant_x(1, 2, 2)
        scale_turned(4, slice(1, 2))
        reorder(CAST_ON_GPSIMD)
        project_both("Q", 2)
        quant_q(0)
        project_both("K", 3)
        scale_turned(5)
        quant_k(0, 0)
        turn(6)
        turn(7)
        project_both("Q", 3)
        quant_x(2)
        quant_k(0, 1)
        quant_k(2, 0)
        quant_k(2, 1)
        scale_turned(6)

        project_half("K", 2, 0, direct=True)
        score(0)
        quant_q(1)
        row_min(0)
        quant_x(3, 0, 2)
        scale_turned(7)
        project_half("K", 2, 1, direct=True)
        exps(0)
        score(1)
        row_min(1)
        quant_x(3, 2, 2)
        quant_k(4, 0)
        invert(0)
        finish(0, nc.gpsimd)
        project_half("Q", 2, 0)
        exps(1)
        score(2)
        row_min(2)
        for u in range(2):
            pair_passes("Q", 2, 1, u)
        empty_pair("Q", 2, 1, 0, False, nc.vector)
        empty_pair("Q", 2, 1, 1, False)
        score(3)
        row_min(3)
        project("K", 6, 0)
        project("K", 6, 1)
        quant_k(4, 1)
        join("Q", 2, 0)
        join("Q", 2, 1)
        quant_k(6, 0, 1)
        quant_q(2)
        project("K", 7, 0)
        project("K", 7, 1)
        quant_k(6, 1, 1)
        quant_k(7, 0, 1)
        quant_k(7, 1, 1)
        exps(2)
        exps(3)
        project("Q", 6, 0, nc.vector)
        project("Q", 6, 1)
        invert(1)
        invert(2)
        finish(1)
        finish(2, nc.gpsimd)
        score(4)
        row_min(4)
        invert(3)
        quant_q(3, 0, 2)
        finish(3)
        project("Q", 7, 0)
        exps(4)
        score(5)
        project("Q", 7, 1)
        row_min(5)
        exps(5)
        quant_q(3, 2, 1)
        invert(4)
        quant_q(3, 3, 1)
        score(6)
        score(7)
        finish(4, nc.scalar)
        row_min(6)
        invert(5)
        row_min(7)
        finish(5)
        exps(6)
        exps(7)
        invert(6)
        finish(6)
        invert(7)
        finish_last()
